import numpy as np
import ml_dtypes


def mxq(x, axis, fmt="e4m3"):
    dtype, down = {"e4m3": (ml_dtypes.float8_e4m3fn, 7), "e5m2": (ml_dtypes.float8_e5m2, 14)}[fmt]
    v = np.moveaxis(np.asarray(x, np.float32).astype(ml_dtypes.bfloat16).astype(np.float64), axis, -1)
    blocks = v.reshape(v.shape[:-1] + (-1, 32))
    amax = np.abs(blocks).max(-1, keepdims=True)
    byte = np.maximum(np.where(amax > 0, np.frexp(amax)[1] - 1 + 127, 0) - down, 1)
    scale = np.exp2(byte - 127.0)
    codes = (blocks / scale).astype(np.float32).astype(dtype).astype(np.float64)
    return np.moveaxis((codes * scale).reshape(v.shape), -1, axis)


WIDE = False


def mx_kscale(k):
    if not WIDE:
        return np.ones(k)
    levels = np.array([10, -10, 5, -5, 0])
    if k % 512:
        return np.exp2(np.random.permutation(np.resize(levels, k // 32))).repeat(32)
    a = np.empty((k // 512, 16))
    for p in range(k // 512):
        a[p, :8] = np.random.permutation(np.resize(levels, 8))
        for g in range(8):
            far = levels[np.abs(levels - a[p, g]) >= 10]
            a[p, g + 8] = far[np.random.randint(len(far))]
    return np.exp2(a.ravel()).repeat(32)


BF16 = ml_dtypes.bfloat16


def bf(x):
    return np.asarray(x, np.float32).astype(BF16)


def f64(x):
    return np.asarray(x).astype(np.float64)


B, EMBED, DETER, STOC, HID, ACT = 4096, 512, 512, 64, 512, 12
DIST = 2 * STOC
CAT = DETER + EMBED


def softplus(v):
    return np.maximum(v, 0.0) + np.log(1.0 + np.exp(-np.abs(v)))


def draw0():
    s = mx_kscale(CAT)
    tp, tq = mx_kscale(HID), mx_kscale(HID)
    r = np.random.standard_normal
    return {
        "h": bf(r((B, DETER)) * 0.65 * s[:DETER]),
        "embedding": bf(r((B, EMBED)) * s[DETER:]),
        "wp1": bf(r((HID, DETER)) / np.sqrt(DETER) / s[:DETER] * tp[:, None]),
        "bp1": bf(r(HID) * 0.1 * tp),
        "wp2": bf(r((DIST, HID)) / np.sqrt(HID) / tp),
        "bp2": bf(r(DIST) * 0.1),
        "wq1": bf(r((HID, CAT)) / np.sqrt(CAT) / s * tq[:, None]),
        "bq1": bf(r(HID) * 0.1 * tq),
        "wq2": bf(r((DIST, HID)) / np.sqrt(HID) / tq),
        "bq2": bf(r(DIST) * 0.1),
    }


def core(h, embedding, wp1, bp1, wp2, bp2, wq1, bq1, wq2, bq2):
    cq = mxq(np.concatenate([f64(h), f64(embedding)], -1), 1, "e4m3")
    ap = np.maximum((cq[:, :DETER] @ mxq(f64(wp1), 1, "e4m3").T) + f64(bp1), 0.0)
    prior = (mxq(ap, 1, "e4m3") @ mxq(f64(wp2), 1, "e4m3").T) + f64(bp2)
    prior_mean, prior_std = np.split(prior, 2, axis=-1)
    prior_std = softplus(prior_std) + 0.1
    aq = np.maximum((cq @ mxq(f64(wq1), 1, "e4m3").T) + f64(bq1), 0.0)
    post = (mxq(aq, 1, "e4m3") @ mxq(f64(wq2), 1, "e4m3").T) + f64(bq2)
    post_mean, post_std = np.split(post, 2, axis=-1)
    post_std = softplus(post_std) + 0.1
    return (post_mean, post_std, prior_mean, prior_std)


def e4m3fn_bytes(y):
    return np.clip(np.asarray(y, np.float64), -448.0, 448.0).astype(np.float32).astype(ml_dtypes.float8_e4m3fn).view(np.uint8)


def e4m3fn_values(b):
    return np.asarray(b, np.uint8).view(ml_dtypes.float8_e4m3fn).astype(np.float64)


def setup_inputs():
    d = draw0()
    x0 = np.asarray(d['h']).astype(np.float64)
    s = (np.max(np.abs(x0), axis=(0,), keepdims=True) / 448.0).astype(np.float32)
    out = {}
    for k, v in d.items():
        if k == 'h':
            out['h_bytes'] = e4m3fn_bytes(x0 / s.astype(np.float64))
            out['h_scale'] = s
        else:
            out[k] = v
    return out


def reference(h_bytes, h_scale, embedding, wp1, bp1, wp2, bp2, wq1, bq1, wq2, bq2):
    return core(e4m3fn_values(h_bytes) * h_scale.astype(np.float64), embedding, wp1, bp1, wp2, bp2, wq1, bq1, wq2, bq2)

@@ -1,0 +1,365 @@
+import math
+from contextlib import ExitStack
+
+import concourse.mybir as mybir
+from concourse.masks import make_identity
+
+B, KIN, HID, DIST, LAT = 4096, 512, 512, 128, 64
+FLOPS = 2 * B * (HID * KIN + HID * 2 * KIN + 2 * DIST * HID)
+
+P = 128
+J = 4
+PACK = 4
+CHUNK = P * J
+CHUNKS = B // CHUNK
+
+F32 = mybir.dt.float32
+BF16 = mybir.dt.bfloat16
+U32 = mybir.dt.uint32
+U8 = mybir.dt.uint8
+FP8 = mybir.dt.float8_e4m3fn
+FP8X4 = mybir.dt.float8_e4m3fn_x4
+ACT = mybir.ActivationFunctionType
+ALU = mybir.AluOpType
+ENG = mybir.EngineType
+
+EXACT_ABOVE = 40.0
+PRIOR, POST = 0, 1
+HEADS = (PRIOR, POST)
+MEAN, STD = 0, 1
+PASSES = {PRIOR: ((0, 0),), POST: ((1, 0), (2, 1))}
+
+
+def tile_rssmcell_pb_t_kernel(
+    tc, h_bytes, h_scale, embedding, wp1, bp1, wp2, bp2, wq1, bq1, wq2, bq2,
+    post_mean, post_std, prior_mean, prior_std,
+):
+    nc = tc.nc
+    with ExitStack() as ctx:
+        keep = ctx.enter_context(tc.tile_pool(name="keep", bufs=1))
+        work = ctx.enter_context(tc.tile_pool(name="work", bufs=2))
+        psum = ctx.enter_context(tc.psum_pool(name="psum", bufs=1))
+
+        scale_row = keep.tile([P, KIN], F32, name="scale_row", tag="scale_row")
+        bias2_row = keep.tile([P, 2 * DIST], BF16, name="bias2_row", tag="bias2_row")
+        ones = keep.tile([P, P], F32, name="ones", tag="ones")
+        ones_bf16 = keep.tile([P, P], BF16, name="ones_bf16", tag="ones_bf16")
+        ident = keep.tile([P, P], F32, name="ident", tag="ident")
+        zero = keep.tile([P, 1], F32, name="zero", tag="zero")
+        bias1_raw = [keep.tile([P, PACK], BF16, name="bias1_raw_%d" % e, tag="bias1_raw_%d" % e) for e in HEADS]
+        bias1 = [keep.tile([P, PACK], F32, name="bias1_%d" % e, tag="bias1_%d" % e) for e in HEADS]
+        bias2 = keep.tile([P, 2, 2, LAT], F32, name="bias2", tag="bias2")
+        scale = keep.tile([P, 2, KIN], F32, name="scale", tag="scale", align_bytes=64)
+        exp_tenth = keep.tile([P, 1], F32, name="exp_tenth", tag="exp_tenth")
+        wp1_rows = keep.tile([P, PACK, KIN], BF16, name="wp1_rows", tag="wp1_rows")
+        wq1_rows = keep.tile([P, PACK, 2 * KIN], BF16, name="wq1_rows", tag="wq1_rows")
+        w2_rows = keep.tile([P, 2, HID], BF16, name="w2_rows", tag="w2_rows")
+        value = keep.tile([P, 2 * CHUNKS, 2, J, LAT], F32, name="value", tag="value")
+        soft = keep.tile([P, 2 * CHUNKS, J * LAT], F32, name="soft", tag="soft")
+        w1_grouped = keep.tile([P, 3, HID, PACK], BF16, name="w1_grouped", tag="w1_grouped", align_bytes=64)
+        w1_codes = keep.tile([P, 3, HID], U32, name="w1_codes", tag="w1_codes", align_bytes=64)
+        w1_scales = keep.tile([P, 3, HID], U8, name="w1_scales", tag="w1_scales", align_bytes=64)
+        w2_grouped = keep.tile([P, 2, DIST, PACK], BF16, name="w2_grouped", tag="w2_grouped", align_bytes=64)
+        w2_codes = keep.tile([P, 2, DIST], U32, name="w2_codes", tag="w2_codes", align_bytes=64)
+        w2_scales = keep.tile([P, 2, DIST], U8, name="w2_scales", tag="w2_scales", align_bytes=64)
+
+        h_raw, emb, h_wide, c_grouped, c_codes, c_scales = {}, {}, {}, {}, {}, {}
+        planes, a_grouped, a_codes, a_scales, result = {}, {}, {}, {}, {}
+
+
+        def turn_weights(rows, k0, t0):
+            bank = psum.tile([P, 2, 2, P], F32, name="turned", tag="turned", bufs=2)
+            for a in (0, 1):
+                words = rows[:, t0 + a, k0 : k0 + KIN].bitcast(F32)
+                for u in (0, 1):
+                    nc.tensor.transpose(bank[:, a, u, :], words[:, u : KIN // 2 : 2], ident[:])
+            return bank
+
+        def unload_weights(copy, w, t0, bank):
+            dst = w1_grouped[:, w, t0 * P : (t0 + 2) * P, :].rearrange("p (a m) e -> p a m e", a=2).bitcast(F32)
+            copy(out=dst, in_=bank[:].rearrange("p a u m -> p a m u"))
+
+        def quantise_weights(w):
+            nc.vector.quantize_mx(
+                out=w1_codes[:, w, :].bitcast(FP8X4), scales=w1_scales[:, w, :],
+                in_=w1_grouped[:, w].rearrange("p m t -> p (m t)"))
+
+        def filler(count):
+            for n in range(count):
+                nc.tensor.matmul(out=unread[:], lhsT=ones[:], rhs=ones[:], start=True, stop=True)
+
+
+        def load_h(i):
+            h_raw[i] = work.tile([P, J, KIN], U8, name="h_raw", tag="h_raw", bufs=5, align_bytes=64)
+            nc.sync.dma_start(out=h_raw[i][:], in_=h_bytes.rearrange("(c p j) k -> c p j k", p=P, j=J)[i])
+
+        def load_embedding(i):
+            emb[i] = work.tile([P, J, KIN], BF16, name="emb", tag="emb", bufs=5)
+            nc.sync.dma_start(out=emb[i][:], in_=embedding.rearrange("(c p j) k -> c p j k", p=P, j=J)[i])
+
+        def widen(i):
+            h_wide[i] = work.tile([P, J, KIN], BF16, name="h_wide", tag="h_wide", bufs=3, align_bytes=64)
+            step = 1 if i < 2 else 2
+            for j in range(0, J, step):
+                rows = slice(j, j + step)
+                nc.vector.tensor_tensor(
+                    out=h_wide[i][:, rows].rearrange("p j k -> p (j k)"),
+                    in0=h_raw[i][:, rows].rearrange("p j k -> p (j k)").bitcast(FP8),
+                    in1=scale[:, 0:step].rearrange("p j k -> p (j k)"), op=ALU.mult)
+
+        def turn(i, j):
+            bank = psum.tile([P, 2, 2, P], F32, name="turned", tag="turned", bufs=2)
+            for g, rows in enumerate((h_wide[i], emb[i])):
+                words = rows[:, j, :].bitcast(F32)
+                for u in (0, 1):
+                    nc.tensor.transpose(bank[:, g, u, :], words[:, u : KIN // 2 : 2], ident[:])
+            if j == 0:
+                c_grouped[i] = work.tile([P, 2, CHUNK, PACK], BF16, name="c_grouped", tag="c_grouped", bufs=2, align_bytes=64)
+            dst = c_grouped[i][:, :, j * P : (j + 1) * P, :].bitcast(F32)
+            nc.scalar.copy(out=dst, in_=bank[:].rearrange("p g u r -> p g r u"))
+
+        def quantise_c(i):
+            c_codes[i] = work.tile([P, 2, CHUNK], U32, name="c_codes", tag="c_codes", bufs=3, align_bytes=64)
+            c_scales[i] = work.tile([P, 2, CHUNK], U8, name="c_scales", tag="c_scales", bufs=3, align_bytes=64)
+            step = 1 if i == 0 else 2
+            for g in range(0, 2, step):
+                part = slice(g, g + step)
+                nc.vector.quantize_mx(
+                    out=c_codes[i][:, part].rearrange("p g n -> p (g n)").bitcast(FP8X4),
+                    scales=c_scales[i][:, part].rearrange("p g n -> p (g n)"),
+                    in_=c_grouped[i][:, part].rearrange("p g n t -> p (g n t)"))
+
+
+        def first(i, head):
+            planes[i, head] = work.tile([P, PACK, CHUNK], BF16, name="planes", tag="planes", bufs=3, align_bytes=64)
+            passes = PASSES[head]
+            for t in range(PACK):
+                acc = psum.tile([P, CHUNK], F32, name="acc", tag="acc", bufs=4)
+                cols = slice(t * P, (t + 1) * P)
+                for n, (w, g) in enumerate(passes):
+                    nc.tensor.matmul_mx(
+                        out=acc[:], lhsT=w1_codes[:, w, cols].bitcast(FP8X4), lhsT_scale=w1_scales[:, w, cols],
+                        rhs=c_codes[i][:, g, :].bitcast(FP8X4), rhs_scale=c_scales[i][:, g, :],
+                        start=(n == 0), stop=(n == len(passes) - 1))
+                dst = planes[i, head][:, t, :]
+                bias = bias1[head][:, t : t + 1]
+                if (i, head, t) == (0, PRIOR, 2):
+                    nc.vector.tensor_scalar(out=dst, in0=acc[:], scalar1=bias, scalar2=0.0, op0=ALU.add, op1=ALU.max)
+                else:
+                    nc.scalar.activation(out=dst, in_=acc[:], func=ACT.Relu, bias=bias)
+
+        def interleave(i, head):
+            a_grouped[i, head] = work.tile([P, CHUNK, PACK], BF16, name="a_grouped", tag="a_grouped", bufs=3, align_bytes=64)
+            nc.vector.tensor_copy(
+                out=a_grouped[i, head][:].rearrange("p (c i) t -> p c t i", i=4),
+                in_=planes[i, head][:].rearrange("p t (c i) -> p c t i", i=4))
+
+        def quantise_a(i, head):
+            a_codes[i, head] = work.tile([P, CHUNK], U32, name="a_codes", tag="a_codes", bufs=4, align_bytes=64)
+            a_scales[i, head] = work.tile([P, CHUNK], U8, name="a_scales", tag="a_scales", bufs=4, align_bytes=64)
+            nc.vector.quantize_mx(
+                out=a_codes[i, head][:].bitcast(FP8X4), scales=a_scales[i, head][:],
+                in_=a_grouped[i, head][:].rearrange("p n t -> p (n t)"))
+
+
+        def second(i, head):
+            result[i, head] = psum.tile([P, J, 2, LAT], F32, name="result", tag="result_%d" % head, bufs=1)
+            for j in range(J):
+                cols = slice(j * P, (j + 1) * P)
+                nc.tensor.matmul_mx(
+                    out=result[i, head][:, j, :, :].rearrange("p h c -> p (h c)"),
+                    lhsT=a_codes[i, head][:, cols].bitcast(FP8X4), lhsT_scale=a_scales[i, head][:, cols],
+                    rhs=w2_codes[:, head, :].bitcast(FP8X4), rhs_scale=w2_scales[:, head, :], start=True, stop=True)
+
+        def add_bias(i, head):
+            nc.vector.tensor_tensor(
+                out=value[:, 2 * i + head].rearrange("p h j c -> p j h c"),
+                in0=result[i, head][:],
+                in1=bias2[:, head].unsqueeze(1).to_broadcast([P, J, 2, LAT]),
+                op=ALU.add)
+            dst = prior_mean if head == PRIOR else post_mean
+            nc.sync.dma_start(
+                out=dst.rearrange("(c p j) d -> c p j d", p=P, j=J)[i], in_=value[:, 2 * i + head, MEAN])
+
+        def exp(e0, e1):
+            nc.scalar.activation(
+                out=soft[:, e0:e1], in_=value[:, e0:e1, STD].rearrange("p e j c -> p e (j c)"), func=ACT.Exp)
+
+        def log(e0, e1):
+            nc.scalar.activation(out=soft[:, e0:e1], in_=soft[:, e0:e1], func=ACT.Ln, bias=exp_tenth[:])
+
+        def std(e0, e1):
+            w = value[:, e0:e1, STD].rearrange("p e j c -> p e (j c)")
+            nc.vector.scalar_tensor_tensor(
+                out=w, in0=soft[:, e0:e1], scalar=EXACT_ABOVE, in1=w, op0=ALU.min, op1=ALU.max)
+            for e in range(e0, e1):
+                dst = prior_std if e % 2 == PRIOR else post_std
+                nc.sync.dma_start(
+                    out=dst.rearrange("(c p j) d -> c p j d", p=P, j=J)[e // 2], in_=value[:, e, STD])
+
+
+        nc.vector.memset(scale_row[:, 0 : KIN // 2], 0.0)
+        nc.gpsimd.memset(scale_row[:, KIN // 2 : KIN], 0.0)
+        nc.gpsimd.memset(ones[:], 1.0)
+        nc.vector.memset(zero[:], 0.0)
+        nc.vector.tensor_scalar(out=exp_tenth[:], in0=zero[:], scalar1=math.exp(0.1), scalar2=None, op0=ALU.add)
+        nc.vector.memset(ones_bf16[:], 1.0)
+        nc.vector.memset(bias2_row[:], 0.0)
+        make_identity(nc, ident[:])
+        nc.scalar.activation(out=zero[:], in_=zero[:], func=ACT.Exp)
+
+        nc.sync.dma_start(out=scale_row[0:1, :], in_=h_scale)
+        nc.scalar.dma_start(out=bias1_raw[PRIOR][:], in_=bp1.rearrange("(m t) -> m t", t=PACK))
+        nc.scalar.dma_start(out=bias1_raw[POST][:], in_=bq1.rearrange("(m t) -> m t", t=PACK))
+        nc.sync.dma_start(out=wp1_rows[:], in_=wp1.rearrange("(m t) k -> m t k", t=PACK))
+        load_h(0)
+        load_embedding(0)
+        load_h(1)
+        nc.sync.dma_start(out=wq1_rows[:], in_=wq1.rearrange("(m t) k -> m t k", t=PACK))
+        load_embedding(1)
+        load_h(2)
+        nc.sync.dma_start(out=w2_rows[:, PRIOR, :], in_=wp2)
+        nc.sync.dma_start(out=w2_rows[:, POST, :], in_=wq2)
+        nc.sync.dma_start(out=bias2_row[0:1, 0:DIST], in_=bp2.unsqueeze(0))
+        nc.sync.dma_start(out=bias2_row[0:1, DIST : 2 * DIST], in_=bq2.unsqueeze(0))
+        load_embedding(2)
+        load_h(3)
+        load_embedding(3)
+        load_h(4)
+        load_embedding(4)
+
+        with tc.manual_schedule(engines={ENG.PE, ENG.Activation, ENG.DVE}):
+            unread = psum.tile([P, P], F32, name="unread", tag="result_1", bufs=1)
+            filler(6)
+            for half, tag, count in ((0, "result_0", 1), (1, "acc", 4)):
+                cols = slice(half * KIN // 2, (half + 1) * KIN // 2)
+                spread = psum.tile([P, KIN // 2], F32, name="spread", tag=tag, bufs=count)
+                nc.tensor.matmul(out=spread[:], lhsT=ones[:], rhs=scale_row[:, cols], start=True, stop=True)
+                nc.scalar.copy(out=scale[:, 0, cols], in_=spread[:])
+            for t0 in (0, 2):
+                unload_weights(nc.scalar.copy, 0, t0, turn_weights(wp1_rows, 0, t0))
+            widen(0)
+            filler(2)
+            quantise_weights(0)
+            turn(0, 0)
+            filler(2)
+            turn(0, 1)
+            turn(0, 2)
+            filler(1)
+            turn(0, 3)
+            load_h(5)
+            load_embedding(5)
+            filler(1)
+            unload_weights(nc.scalar.copy, 1, 0, turn_weights(wq1_rows, 0, 0))
+            nc.scalar.copy(out=scale[:, 1], in_=scale[:, 0])
+            filler(2)
+            unload_weights(nc.scalar.copy, 1, 2, turn_weights(wq1_rows, 0, 2))
+            for head in HEADS:
+                nc.vector.tensor_copy(out=bias1[head][:], in_=bias1_raw[head][:])
+            widen(1)
+            quantise_c(0)
+            quantise_weights(1)
+            unload_weights(nc.vector.tensor_copy, 2, 2, turn_weights(wq1_rows, KIN, 2))
+            first(0, PRIOR)
+            turn(1, 0)
+            unload_weights(nc.scalar.copy, 2, 0, turn_weights(wq1_rows, KIN, 0))
+            filler(2)
+            turn(1, 1)
+            filler(1)
+            turn(1, 2)
+            turn(1, 3)
+            widen(2)
+            quantise_weights(2)
+            first(0, POST)
+            interleave(0, PRIOR)
+            quantise_c(1)
+            turn(2, 0)
+            turn(2, 1)
+            filler(1)
+            quantise_a(0, PRIOR)
+            turn(2, 2)
+            widen(3)
+            turn(2, 3)
+            filler(2)
+            quantise_c(2)
+            bank = psum.tile([P, 2, 2, P], F32, name="turned", tag="turned", bufs=2)
+            for head in HEADS:
+                words = w2_rows[:, head, :].bitcast(F32)
+                for u in (0, 1):
+                    nc.tensor.transpose(bank[:, head, u, :], words[:, u : KIN // 2 : 2], ident[:])
+            nc.scalar.copy(out=w2_grouped[:].bitcast(F32), in_=bank[:].rearrange("p a u m -> p a m u"))
+            spread2 = psum.tile([P, 2, 2, LAT], F32, name="spread2", tag="result_1", bufs=1)
+            nc.tensor.matmul(
+                out=spread2[:].rearrange("p e h c -> p (e h c)"), lhsT=ones_bf16[:], rhs=bias2_row[:], start=True, stop=True)
+            nc.vector.quantize_mx(
+                out=w2_codes[:].rearrange("p e m -> p (e m)").bitcast(FP8X4),
+                scales=w2_scales[:].rearrange("p e m -> p (e m)"),
+                in_=w2_grouped[:].rearrange("p e m t -> p (e m t)"))
+            nc.vector.tensor_copy(out=bias2[:, :, MEAN], in_=spread2[:, :, MEAN])
+            nc.vector.tensor_scalar(out=bias2[:, :, STD], in0=spread2[:, :, STD], scalar1=0.1, scalar2=None, op0=ALU.add)
+
+            for i in range(1, CHUNKS - 1):
+                turning = i + 2 < CHUNKS
+                if i + 5 < CHUNKS:
+                    load_h(i + 5)
+                    load_embedding(i + 5)
+                if turning:
+                    turn(i + 2, 0)
+                    turn(i + 2, 1)
+                interleave(i - 1, POST)
+                first(i, PRIOR)
+                if i >= 2:
+                    for head in HEADS:
+                        second(i - 2, head)
+                if i >= 3:
+                    exp(2 * (i - 3), 2 * (i - 2))
+                if turning:
+                    turn(i + 2, 2)
+                    turn(i + 2, 3)
+                if i + 3 < CHUNKS:
+                    widen(i + 3)
+                if i >= 2:
+                    for head in HEADS:
+                        add_bias(i - 2, head)
+                quantise_a(i - 1, POST)
+                first(i, POST)
+                interleave(i, PRIOR)
+                if turning:
+                    quantise_c(i + 2)
+                quantise_a(i, PRIOR)
+
+            last = CHUNKS - 1
+            early = 2 * (last - 1)
+            first(last, PRIOR)
+            for head in HEADS:
+                second(last - 2, head)
+            exp(2 * (last - 3), 2 * (last - 2))
+            interleave(last - 1, POST)
+            for head in HEADS:
+                add_bias(last - 2, head)
+            quantise_a(last - 1, POST)
+            first(last, POST)
+            exp(2 * (last - 2), 2 * (last - 1))
+            for e in range(0, early, 4):
+                log(e, e + 4)
+            interleave(last, PRIOR)
+            for head in HEADS:
+                second(last - 1, head)
+            add_bias(last - 1, PRIOR)
+            quantise_a(last, PRIOR)
+            add_bias(last - 1, POST)
+            exp(2 * (last - 1), 2 * last)
+            interleave(last, POST)
+            second(last, PRIOR)
+            add_bias(last, PRIOR)
+            exp(2 * last, 2 * last + 1)
+            quantise_a(last, POST)
+            std(0, 4)
+            second(last, POST)
+            add_bias(last, POST)
+            exp(2 * last + 1, 2 * last + 2)
+            for e in range(4, early, 4):
+                std(e, e + 4)
+            for e in (early, early + 2):
+                log(e, e + 2)
+                std(e, e + 2)

@@ -12,6 +12,7 @@ J = 4
 PACK = 4
 CHUNK = P * J
 CHUNKS = B // CHUNK
+HALF = CHUNK // 2
 
 F32 = mybir.dt.float32
 BF16 = mybir.dt.bfloat16
@@ -21,13 +22,14 @@ FP8 = mybir.dt.float8_e4m3fn
 FP8X4 = mybir.dt.float8_e4m3fn_x4
 ACT = mybir.ActivationFunctionType
 ALU = mybir.AluOpType
-ENG = mybir.EngineType
 
+TURNED, ACCS = 2, 4
 EXACT_ABOVE = 40.0
 PRIOR, POST = 0, 1
 HEADS = (PRIOR, POST)
 MEAN, STD = 0, 1
-PASSES = {PRIOR: ((0, 0),), POST: ((1, 0), (2, 1))}
+H, E = 0, 1
+PASSES = {PRIOR: ((0, H),), POST: ((1, H), (2, E))}
 
 
 def tile_rssmcell_pb_t_kernel(
@@ -40,126 +42,140 @@ def tile_rssmcell_pb_t_kernel(
         work = ctx.enter_context(tc.tile_pool(name="work", bufs=2))
         psum = ctx.enter_context(tc.psum_pool(name="psum", bufs=1))
 
-        scale_row = keep.tile([P, KIN], F32, name="scale_row", tag="scale_row")
         bias2_row = keep.tile([P, 2 * DIST], BF16, name="bias2_row", tag="bias2_row")
-        ones = keep.tile([P, P], F32, name="ones", tag="ones")
-        ones_bf16 = keep.tile([P, P], BF16, name="ones_bf16", tag="ones_bf16")
+        ones = keep.tile([P, P], BF16, name="ones", tag="ones")
         ident = keep.tile([P, P], F32, name="ident", tag="ident")
-        zero = keep.tile([P, 1], F32, name="zero", tag="zero")
+        scale = keep.tile([P, PACK], F32, name="scale", tag="scale")
         bias1_raw = [keep.tile([P, PACK], BF16, name="bias1_raw_%d" % e, tag="bias1_raw_%d" % e) for e in HEADS]
         bias1 = [keep.tile([P, PACK], F32, name="bias1_%d" % e, tag="bias1_%d" % e) for e in HEADS]
         bias2 = keep.tile([P, 2, 2, LAT], F32, name="bias2", tag="bias2")
-        scale = keep.tile([P, 2, KIN], F32, name="scale", tag="scale", align_bytes=64)
         exp_tenth = keep.tile([P, 1], F32, name="exp_tenth", tag="exp_tenth")
-        wp1_rows = keep.tile([P, PACK, KIN], BF16, name="wp1_rows", tag="wp1_rows")
-        wq1_rows = keep.tile([P, PACK, 2 * KIN], BF16, name="wq1_rows", tag="wq1_rows")
+        w1_rows = [keep.tile([P, PACK, KIN], BF16, name="w1_rows_%d" % w, tag="w1_rows_%d" % w) for w in range(3)]
         w2_rows = keep.tile([P, 2, HID], BF16, name="w2_rows", tag="w2_rows")
-        value = keep.tile([P, 2 * CHUNKS, 2, J, LAT], F32, name="value", tag="value")
-        soft = keep.tile([P, 2 * CHUNKS, J * LAT], F32, name="soft", tag="soft")
-        w1_grouped = keep.tile([P, 3, HID, PACK], BF16, name="w1_grouped", tag="w1_grouped", align_bytes=64)
+        value = keep.tile([P, 2, 2, CHUNKS * J, LAT], F32, name="value", tag="value")
+        soft = keep.tile([P, 2, CHUNKS * J * LAT], F32, name="soft", tag="soft")
         w1_codes = keep.tile([P, 3, HID], U32, name="w1_codes", tag="w1_codes", align_bytes=64)
         w1_scales = keep.tile([P, 3, HID], U8, name="w1_scales", tag="w1_scales", align_bytes=64)
-        w2_grouped = keep.tile([P, 2, DIST, PACK], BF16, name="w2_grouped", tag="w2_grouped", align_bytes=64)
         w2_codes = keep.tile([P, 2, DIST], U32, name="w2_codes", tag="w2_codes", align_bytes=64)
         w2_scales = keep.tile([P, 2, DIST], U8, name="w2_scales", tag="w2_scales", align_bytes=64)
 
-        h_raw, emb, h_wide, c_grouped, c_codes, c_scales = {}, {}, {}, {}, {}, {}
-        planes, a_grouped, a_codes, a_scales, result = {}, {}, {}, {}, {}
+        h_raw, emb, h_wide, turned, c_grouped, c_codes, c_scales = {}, {}, {}, {}, {}, {}, {}
+        w1_grouped, acc, planes, a_grouped, a_codes, a_scales, result = {}, {}, {}, {}, {}, {}, {}
 
-
-        def turn_weights(rows, k0, t0):
-            bank = psum.tile([P, 2, 2, P], F32, name="turned", tag="turned", bufs=2)
+        def turn(key, rows, tag="turned", bufs=TURNED):
+            turned[key] = psum.tile([P, 2, HALF], F32, name="turned", tag=tag, bufs=bufs)
             for a in (0, 1):
-                words = rows[:, t0 + a, k0 : k0 + KIN].bitcast(F32)
+                words = rows[:, a, :].bitcast(F32)
                 for u in (0, 1):
-                    nc.tensor.transpose(bank[:, a, u, :], words[:, u : KIN // 2 : 2], ident[:])
-            return bank
+                    nc.tensor.transpose(turned[key][:, u, a * P : (a + 1) * P], words[:, u : KIN // 2 : 2], ident[:])
 
-        def unload_weights(copy, w, t0, bank):
-            dst = w1_grouped[:, w, t0 * P : (t0 + 2) * P, :].rearrange("p (a m) e -> p a m e", a=2).bitcast(F32)
-            copy(out=dst, in_=bank[:].rearrange("p a u m -> p a m u"))
+        def unload(copy, key, dst):
+            copy(out=dst.bitcast(F32), in_=turned[key][:].rearrange("p u n -> p n u"))
 
-        def quantise_weights(w):
-            nc.vector.quantize_mx(
-                out=w1_codes[:, w, :].bitcast(FP8X4), scales=w1_scales[:, w, :],
-                in_=w1_grouped[:, w].rearrange("p m t -> p (m t)"))
+        def quantise(codes, scales, grouped):
+            nc.vector.quantize_mx(out=codes.bitcast(FP8X4), scales=scales, in_=grouped.rearrange("p n t -> p (n t)"))
 
-        def filler(count):
-            for n in range(count):
-                nc.tensor.matmul(out=unread[:], lhsT=ones[:], rhs=ones[:], start=True, stop=True)
+
+        def turn_w1(w, a):
+            turn(("w", w, a), w1_rows[w][:, 2 * a : 2 * a + 2], "acc", ACCS)
+
+        def unload_w1(copy, w, a):
+            if a == 0:
+                w1_grouped[w] = work.tile([P, HID, PACK], BF16, name="w1_grouped", tag="w1_grouped", bufs=2, align_bytes=64)
+            unload(copy, ("w", w, a), w1_grouped[w][:, a * HALF : (a + 1) * HALF])
+
+        def quantise_w1(w):
+            quantise(w1_codes[:, w], w1_scales[:, w], w1_grouped[w][:])
+
+        def warm_up(tag, bufs):
+            unread = psum.tile([P, 2, P], F32, name="unread", tag=tag, bufs=bufs)
+            nc.tensor.matmul(out=unread[:], lhsT=ident[:], rhs=ident[:].unsqueeze(1).to_broadcast([P, 2, P]), start=True, stop=True)
 
 
         def load_h(i):
-            h_raw[i] = work.tile([P, J, KIN], U8, name="h_raw", tag="h_raw", bufs=5, align_bytes=64)
-            nc.sync.dma_start(out=h_raw[i][:], in_=h_bytes.rearrange("(c p j) k -> c p j k", p=P, j=J)[i])
+            h_raw[i] = work.tile([P, J, KIN], U8, name="h_raw", tag="h_raw", bufs=CHUNKS, align_bytes=64)
+            nc.sync.dma_start(out=h_raw[i][:], in_=h_bytes.rearrange("(p c j) k -> c p j k", p=P, j=J)[i])
 
         def load_embedding(i):
-            emb[i] = work.tile([P, J, KIN], BF16, name="emb", tag="emb", bufs=5)
-            nc.sync.dma_start(out=emb[i][:], in_=embedding.rearrange("(c p j) k -> c p j k", p=P, j=J)[i])
+            emb[i] = work.tile([P, J, KIN], BF16, name="emb", tag="emb", bufs=CHUNKS)
+            nc.sync.dma_start(out=emb[i][:], in_=embedding.rearrange("(p c j) k -> c p j k", p=P, j=J)[i])
 
-        def widen(i):
-            h_wide[i] = work.tile([P, J, KIN], BF16, name="h_wide", tag="h_wide", bufs=3, align_bytes=64)
-            step = 1 if i < 2 else 2
-            for j in range(0, J, step):
-                rows = slice(j, j + step)
-                nc.vector.tensor_tensor(
-                    out=h_wide[i][:, rows].rearrange("p j k -> p (j k)"),
-                    in0=h_raw[i][:, rows].rearrange("p j k -> p (j k)").bitcast(FP8),
-                    in1=scale[:, 0:step].rearrange("p j k -> p (j k)"), op=ALU.mult)
+        def widen(copy, i, j0=0, j1=J):
+            if j0 == 0:
+                h_wide[i] = work.tile([P, J, KIN], BF16, name="h_wide", tag="h_wide", bufs=2, align_bytes=64)
+            copy(out=h_wide[i][:, j0:j1].rearrange("p j k -> p (j k)"),
+                 in_=h_raw[i][:, j0:j1].rearrange("p j k -> p (j k)").bitcast(FP8))
 
-        def turn(i, j):
-            bank = psum.tile([P, 2, 2, P], F32, name="turned", tag="turned", bufs=2)
-            for g, rows in enumerate((h_wide[i], emb[i])):
-                words = rows[:, j, :].bitcast(F32)
-                for u in (0, 1):
-                    nc.tensor.transpose(bank[:, g, u, :], words[:, u : KIN // 2 : 2], ident[:])
-            if j == 0:
-                c_grouped[i] = work.tile([P, 2, CHUNK, PACK], BF16, name="c_grouped", tag="c_grouped", bufs=2, align_bytes=64)
-            dst = c_grouped[i][:, :, j * P : (j + 1) * P, :].bitcast(F32)
-            nc.scalar.copy(out=dst, in_=bank[:].rearrange("p g u r -> p g r u"))
+        def turn_c(i, g, a, tag="turned", bufs=TURNED):
+            turn((i, g, a), (h_wide, emb)[g][i][:, 2 * a : 2 * a + 2], tag, bufs)
 
-        def quantise_c(i):
-            c_codes[i] = work.tile([P, 2, CHUNK], U32, name="c_codes", tag="c_codes", bufs=3, align_bytes=64)
-            c_scales[i] = work.tile([P, 2, CHUNK], U8, name="c_scales", tag="c_scales", bufs=3, align_bytes=64)
-            step = 1 if i == 0 else 2
-            for g in range(0, 2, step):
-                part = slice(g, g + step)
-                nc.vector.quantize_mx(
-                    out=c_codes[i][:, part].rearrange("p g n -> p (g n)").bitcast(FP8X4),
-                    scales=c_scales[i][:, part].rearrange("p g n -> p (g n)"),
-                    in_=c_grouped[i][:, part].rearrange("p g n t -> p (g n t)"))
+        def grouped_half(i, g, a):
+            if a == 0:
+                c_grouped[i, g] = work.tile([P, CHUNK, PACK], BF16, name="c_grouped", tag="c_grouped_%d" % g, bufs=2, align_bytes=64)
+            return c_grouped[i, g][:, a * HALF : (a + 1) * HALF]
+
+        def scale_h(i, a):
+            nc.vector.tensor_tensor(
+                out=grouped_half(i, H, a).rearrange("p n (u e) -> p n u e", u=2),
+                in0=turned[i, H, a][:].bitcast(BF16).rearrange("p u (n e) -> p n u e", e=2),
+                in1=scale[:].rearrange("p (u e) -> p u e", u=2).unsqueeze(1).to_broadcast([P, HALF, 2, 2]),
+                op=ALU.mult)
+
+        def unload_e(copy, i, a):
+            unload(copy, (i, E, a), grouped_half(i, E, a))
+
+        def quantise_c(i, g):
+            c_codes[i, g] = work.tile([P, CHUNK], U32, name="c_codes", tag="c_codes_%d" % g, bufs=3, align_bytes=64)
+            c_scales[i, g] = work.tile([P, CHUNK], U8, name="c_scales", tag="c_scales_%d" % g, bufs=3, align_bytes=64)
+            quantise(c_codes[i, g][:], c_scales[i, g][:], c_grouped[i, g][:])
 
 
-        def first(i, head):
-            planes[i, head] = work.tile([P, PACK, CHUNK], BF16, name="planes", tag="planes", bufs=3, align_bytes=64)
+        def first(i, head, t):
+            acc[i, head, t] = psum.tile([P, CHUNK], F32, name="acc", tag="acc", bufs=ACCS)
+            cols = slice(t * P, (t + 1) * P)
             passes = PASSES[head]
+            for n, (w, g) in enumerate(passes):
+                nc.tensor.matmul_mx(
+                    out=acc[i, head, t][:], lhsT=w1_codes[:, w, cols].bitcast(FP8X4), lhsT_scale=w1_scales[:, w, cols],
+                    rhs=c_codes[i, g][:].bitcast(FP8X4), rhs_scale=c_scales[i, g][:],
+                    start=(n == 0), stop=(n == len(passes) - 1))
+
+        def plane(i, head, t):
+            if t == 0:
+                planes[i, head] = work.tile([P, PACK, CHUNK], BF16, name="planes", tag="planes_%d" % head, bufs=2, align_bytes=64)
+            return planes[i, head][:, t, :]
+
+        def relu(i, head, t):
+            nc.scalar.activation(out=plane(i, head, t), in_=acc[i, head, t][:], func=ACT.Relu, bias=bias1[head][:, t : t + 1])
+
+        def relu_on_vector(i, head, t):
+            nc.vector.tensor_scalar(out=plane(i, head, t), in0=acc[i, head, t][:], scalar1=bias1[head][:, t : t + 1],
+                                    scalar2=0.0, op0=ALU.add, op1=ALU.max)
+
+        def layer1(i, head):
             for t in range(PACK):
-                acc = psum.tile([P, CHUNK], F32, name="acc", tag="acc", bufs=4)
-                cols = slice(t * P, (t + 1) * P)
-                for n, (w, g) in enumerate(passes):
-                    nc.tensor.matmul_mx(
-                        out=acc[:], lhsT=w1_codes[:, w, cols].bitcast(FP8X4), lhsT_scale=w1_scales[:, w, cols],
-                        rhs=c_codes[i][:, g, :].bitcast(FP8X4), rhs_scale=c_scales[i][:, g, :],
-                        start=(n == 0), stop=(n == len(passes) - 1))
-                dst = planes[i, head][:, t, :]
-                bias = bias1[head][:, t : t + 1]
-                if (i, head, t) == (0, PRIOR, 2):
-                    nc.vector.tensor_scalar(out=dst, in0=acc[:], scalar1=bias, scalar2=0.0, op0=ALU.add, op1=ALU.max)
-                else:
-                    nc.scalar.activation(out=dst, in_=acc[:], func=ACT.Relu, bias=bias)
+                first(i, head, t)
+                relu(i, head, t)
+
+        def new_grouped(i, head):
+            a_grouped[i, head] = work.tile([P, CHUNK, PACK], BF16, name="a_grouped", tag="a_grouped_%d" % head, bufs=1, align_bytes=64)
 
         def interleave(i, head):
-            a_grouped[i, head] = work.tile([P, CHUNK, PACK], BF16, name="a_grouped", tag="a_grouped", bufs=3, align_bytes=64)
+            new_grouped(i, head)
             nc.vector.tensor_copy(
                 out=a_grouped[i, head][:].rearrange("p (c i) t -> p c t i", i=4),
                 in_=planes[i, head][:].rearrange("p t (c i) -> p c t i", i=4))
 
+        def interleave_on_gpsimd(i, head):
+            new_grouped(i, head)
+            nc.gpsimd.tensor_scalar(
+                out=a_grouped[i, head][:], in0=planes[i, head][:].rearrange("p t n -> p n t"),
+                scalar1=1.0, scalar2=0.0, op0=ALU.mult, op1=ALU.add)
+
         def quantise_a(i, head):
             a_codes[i, head] = work.tile([P, CHUNK], U32, name="a_codes", tag="a_codes", bufs=4, align_bytes=64)
             a_scales[i, head] = work.tile([P, CHUNK], U8, name="a_scales", tag="a_scales", bufs=4, align_bytes=64)
-            nc.vector.quantize_mx(
-                out=a_codes[i, head][:].bitcast(FP8X4), scales=a_scales[i, head][:],
-                in_=a_grouped[i, head][:].rearrange("p n t -> p (n t)"))
+            quantise(a_codes[i, head][:], a_scales[i, head][:], a_grouped[i, head][:])
 
 
         def second(i, head):
@@ -171,195 +187,170 @@ def tile_rssmcell_pb_t_kernel(
                     lhsT=a_codes[i, head][:, cols].bitcast(FP8X4), lhsT_scale=a_scales[i, head][:, cols],
                     rhs=w2_codes[:, head, :].bitcast(FP8X4), rhs_scale=w2_scales[:, head, :], start=True, stop=True)
 
+        def store(dst, head, half, i0, i1):
+            tokens = slice(i0 * J, i1 * J)
+            nc.sync.dma_start(out=dst.rearrange("(p n) d -> p n d", p=P)[:, tokens], in_=value[:, head, half, tokens])
+
         def add_bias(i, head):
             nc.vector.tensor_tensor(
-                out=value[:, 2 * i + head].rearrange("p h j c -> p j h c"),
+                out=value[:, head, :, i * J : (i + 1) * J].rearrange("p h j c -> p j h c"),
                 in0=result[i, head][:],
                 in1=bias2[:, head].unsqueeze(1).to_broadcast([P, J, 2, LAT]),
                 op=ALU.add)
-            dst = prior_mean if head == PRIOR else post_mean
-            nc.sync.dma_start(
-                out=dst.rearrange("(c p j) d -> c p j d", p=P, j=J)[i], in_=value[:, 2 * i + head, MEAN])
+            store((prior_mean, post_mean)[head], head, MEAN, i, i + 1)
 
-        def exp(e0, e1):
-            nc.scalar.activation(
-                out=soft[:, e0:e1], in_=value[:, e0:e1, STD].rearrange("p e j c -> p e (j c)"), func=ACT.Exp)
+        def w_of(i0, i1):
+            return value[:, :, STD, i0 * J : i1 * J].rearrange("p e n c -> p e (n c)")
 
-        def log(e0, e1):
-            nc.scalar.activation(out=soft[:, e0:e1], in_=soft[:, e0:e1], func=ACT.Ln, bias=exp_tenth[:])
+        def soft_of(i0, i1):
+            return soft[:, :, i0 * J * LAT : i1 * J * LAT]
 
-        def std(e0, e1):
-            w = value[:, e0:e1, STD].rearrange("p e j c -> p e (j c)")
+        def exp(i0, i1):
+            nc.scalar.activation(out=soft_of(i0, i1), in_=w_of(i0, i1), func=ACT.Exp)
+
+        def log(i0, i1):
+            nc.scalar.activation(out=soft_of(i0, i1), in_=soft_of(i0, i1), func=ACT.Ln, bias=exp_tenth[:])
+
+        def std(i0, i1):
             nc.vector.scalar_tensor_tensor(
-                out=w, in0=soft[:, e0:e1], scalar=EXACT_ABOVE, in1=w, op0=ALU.min, op1=ALU.max)
-            for e in range(e0, e1):
-                dst = prior_std if e % 2 == PRIOR else post_std
+                out=w_of(i0, i1), in0=soft_of(i0, i1), scalar=EXACT_ABOVE, in1=w_of(i0, i1), op0=ALU.min, op1=ALU.max)
+            for head in HEADS:
+                store((prior_std, post_std)[head], head, STD, i0, i1)
+
+        def turn_w2():
+            turn("w2", w2_rows[:], "result_1", 1)
+            new_grouped("w2", POST)
+            unload(nc.scalar.copy, "w2", a_grouped["w2", POST][:, 0:HALF])
+
+        def quantise_w2():
+            quantise(w2_codes[:].rearrange("p e m -> p (e m)"), w2_scales[:].rearrange("p e m -> p (e m)"),
+                     a_grouped["w2", POST][:, 0:HALF])
+
+        def spread_bias2():
+            spread = psum.tile([P, 2, 2, LAT], F32, name="spread", tag="result_0", bufs=1)
+            nc.tensor.matmul(
+                out=spread[:].rearrange("p e h c -> p (e h c)"), lhsT=ones[:], rhs=bias2_row[:], start=True, stop=True)
+            nc.vector.tensor_copy(out=bias2[:, :, MEAN], in_=spread[:, :, MEAN])
+            nc.vector.tensor_scalar(out=bias2[:, :, STD], in0=spread[:, :, STD], scalar1=0.1, scalar2=None, op0=ALU.add)
+
+        with tc.manual_schedule():
+            nc.vector.memset(ones[:], 1.0)
+            nc.vector.memset(bias2_row[:], 0.0)
+            make_identity(nc, ident[:])
+            nc.scalar.dma_start(out=scale[:], in_=h_scale.rearrange("o (p t) -> p (o t)", t=PACK))
+            nc.scalar.dma_start(out=bias1_raw[PRIOR][:], in_=bp1.rearrange("(m t) -> m t", t=PACK))
+            nc.scalar.dma_start(out=bias1_raw[POST][:], in_=bq1.rearrange("(m t) -> m t", t=PACK))
+            nc.scalar.activation(out=exp_tenth[:], in_=ones[:, 0:1], func=ACT.Exp, scale=0.1)
+            load_h(0)
+            nc.sync.dma_start(out=w1_rows[0][:], in_=wp1.rearrange("(m t) k -> m t k", t=PACK))
+            load_h(1)
+            load_embedding(0)
+            for g in (H, E):
                 nc.sync.dma_start(
-                    out=dst.rearrange("(c p j) d -> c p j d", p=P, j=J)[e // 2], in_=value[:, e, STD])
+                    out=w1_rows[1 + g][:], in_=wq1.rearrange("(m t) k -> m t k", t=PACK)[:, :, g * KIN : (g + 1) * KIN])
+            load_embedding(1)
+            load_h(2)
+            nc.sync.dma_start(out=w2_rows[:, PRIOR, :], in_=wp2)
+            nc.sync.dma_start(out=w2_rows[:, POST, :], in_=wq2)
+            nc.sync.dma_start(out=bias2_row[0:1, 0:DIST], in_=bp2.unsqueeze(0))
+            nc.sync.dma_start(out=bias2_row[0:1, DIST : 2 * DIST], in_=bq2.unsqueeze(0))
+            for i in range(2, CHUNKS):
+                load_embedding(i)
+                if i + 1 < CHUNKS:
+                    load_h(i + 1)
 
-
-        nc.vector.memset(scale_row[:, 0 : KIN // 2], 0.0)
-        nc.gpsimd.memset(scale_row[:, KIN // 2 : KIN], 0.0)
-        nc.gpsimd.memset(ones[:], 1.0)
-        nc.vector.memset(zero[:], 0.0)
-        nc.vector.tensor_scalar(out=exp_tenth[:], in0=zero[:], scalar1=math.exp(0.1), scalar2=None, op0=ALU.add)
-        nc.vector.memset(ones_bf16[:], 1.0)
-        nc.vector.memset(bias2_row[:], 0.0)
-        make_identity(nc, ident[:])
-        nc.scalar.activation(out=zero[:], in_=zero[:], func=ACT.Exp)
-
-        nc.sync.dma_start(out=scale_row[0:1, :], in_=h_scale)
-        nc.scalar.dma_start(out=bias1_raw[PRIOR][:], in_=bp1.rearrange("(m t) -> m t", t=PACK))
-        nc.scalar.dma_start(out=bias1_raw[POST][:], in_=bq1.rearrange("(m t) -> m t", t=PACK))
-        nc.sync.dma_start(out=wp1_rows[:], in_=wp1.rearrange("(m t) k -> m t k", t=PACK))
-        load_h(0)
-        load_embedding(0)
-        load_h(1)
-        nc.sync.dma_start(out=wq1_rows[:], in_=wq1.rearrange("(m t) k -> m t k", t=PACK))
-        load_embedding(1)
-        load_h(2)
-        nc.sync.dma_start(out=w2_rows[:, PRIOR, :], in_=wp2)
-        nc.sync.dma_start(out=w2_rows[:, POST, :], in_=wq2)
-        nc.sync.dma_start(out=bias2_row[0:1, 0:DIST], in_=bp2.unsqueeze(0))
-        nc.sync.dma_start(out=bias2_row[0:1, DIST : 2 * DIST], in_=bq2.unsqueeze(0))
-        load_embedding(2)
-        load_h(3)
-        load_embedding(3)
-        load_h(4)
-        load_embedding(4)
-
-        with tc.manual_schedule(engines={ENG.PE, ENG.Activation, ENG.DVE}):
-            unread = psum.tile([P, P], F32, name="unread", tag="result_1", bufs=1)
-            filler(6)
-            for half, tag, count in ((0, "result_0", 1), (1, "acc", 4)):
-                cols = slice(half * KIN // 2, (half + 1) * KIN // 2)
-                spread = psum.tile([P, KIN // 2], F32, name="spread", tag=tag, bufs=count)
-                nc.tensor.matmul(out=spread[:], lhsT=ones[:], rhs=scale_row[:, cols], start=True, stop=True)
-                nc.scalar.copy(out=scale[:, 0, cols], in_=spread[:])
-            for t0 in (0, 2):
-                unload_weights(nc.scalar.copy, 0, t0, turn_weights(wp1_rows, 0, t0))
-            widen(0)
-            filler(2)
-            quantise_weights(0)
-            turn(0, 0)
-            filler(2)
-            turn(0, 1)
-            turn(0, 2)
-            filler(1)
-            turn(0, 3)
-            load_h(5)
-            load_embedding(5)
-            filler(1)
-            unload_weights(nc.scalar.copy, 1, 0, turn_weights(wq1_rows, 0, 0))
-            nc.scalar.copy(out=scale[:, 1], in_=scale[:, 0])
-            filler(2)
-            unload_weights(nc.scalar.copy, 1, 2, turn_weights(wq1_rows, 0, 2))
+            for n in range(3):
+                warm_up("acc", ACCS)
+            widen(nc.vector.tensor_copy, 0, 0, 2)
+            widen(nc.vector.tensor_copy, 0, 2, 4)
+            for a in (0, 1):
+                turn_c(0, H, a)
+                scale_h(0, a)
+            widen(nc.scalar.copy, 1)
+            for a in (0, 1):
+                turn_w1(0, a)
+                unload_w1(nc.scalar.copy, 0, a)
+            warm_up("acc", ACCS)
             for head in HEADS:
                 nc.vector.tensor_copy(out=bias1[head][:], in_=bias1_raw[head][:])
-            widen(1)
-            quantise_c(0)
-            quantise_weights(1)
-            unload_weights(nc.vector.tensor_copy, 2, 2, turn_weights(wq1_rows, KIN, 2))
-            first(0, PRIOR)
-            turn(1, 0)
-            unload_weights(nc.scalar.copy, 2, 0, turn_weights(wq1_rows, KIN, 0))
-            filler(2)
-            turn(1, 1)
-            filler(1)
-            turn(1, 2)
-            turn(1, 3)
-            widen(2)
-            quantise_weights(2)
-            first(0, POST)
-            interleave(0, PRIOR)
-            quantise_c(1)
-            turn(2, 0)
-            turn(2, 1)
-            filler(1)
-            quantise_a(0, PRIOR)
-            turn(2, 2)
-            widen(3)
-            turn(2, 3)
-            filler(2)
-            quantise_c(2)
-            bank = psum.tile([P, 2, 2, P], F32, name="turned", tag="turned", bufs=2)
-            for head in HEADS:
-                words = w2_rows[:, head, :].bitcast(F32)
-                for u in (0, 1):
-                    nc.tensor.transpose(bank[:, head, u, :], words[:, u : KIN // 2 : 2], ident[:])
-            nc.scalar.copy(out=w2_grouped[:].bitcast(F32), in_=bank[:].rearrange("p a u m -> p a m u"))
-            spread2 = psum.tile([P, 2, 2, LAT], F32, name="spread2", tag="result_1", bufs=1)
-            nc.tensor.matmul(
-                out=spread2[:].rearrange("p e h c -> p (e h c)"), lhsT=ones_bf16[:], rhs=bias2_row[:], start=True, stop=True)
-            nc.vector.quantize_mx(
-                out=w2_codes[:].rearrange("p e m -> p (e m)").bitcast(FP8X4),
-                scales=w2_scales[:].rearrange("p e m -> p (e m)"),
-                in_=w2_grouped[:].rearrange("p e m t -> p (e m t)"))
-            nc.vector.tensor_copy(out=bias2[:, :, MEAN], in_=spread2[:, :, MEAN])
-            nc.vector.tensor_scalar(out=bias2[:, :, STD], in0=spread2[:, :, STD], scalar1=0.1, scalar2=None, op0=ALU.add)
+            quantise_w1(0)
+            quantise_c(0, H)
+            for a in (0, 1):
+                turn_c(0, E, a, "result_%d" % a, 1)
+                unload_e(nc.scalar.copy, 0, a)
+            for a in (0, 1):
+                turn_c(1, H, a)
+                scale_h(1, a)
+            for t in (0, 1):
+                first(0, PRIOR, t)
+                relu(0, PRIOR, t)
+            for a in (0, 1):
+                turn_w1(1, a)
+                unload_w1(nc.scalar.copy, 1, a)
+            quantise_c(0, E)
+            for t in (2, 3):
+                first(0, PRIOR, t)
+                relu(0, PRIOR, t)
+            for a in (0, 1):
+                turn(("w", 2, a), w1_rows[2][:, 2 * a : 2 * a + 2], "result_%d" % a, 1)
+                unload_w1(nc.vector.tensor_copy, 2, a)
+            quantise_w1(1)
+            quantise_w1(2)
 
-            for i in range(1, CHUNKS - 1):
-                turning = i + 2 < CHUNKS
-                if i + 5 < CHUNKS:
-                    load_h(i + 5)
-                    load_embedding(i + 5)
-                if turning:
-                    turn(i + 2, 0)
-                    turn(i + 2, 1)
-                interleave(i - 1, POST)
-                first(i, PRIOR)
+            for i in range(CHUNKS - 1):
+                if i >= 1:
+                    interleave_on_gpsimd(i - 1, POST)
+                    for a in (0, 1):
+                        scale_h(i + 1, a)
+                    layer1(i, PRIOR)
+                if i == 1:
+                    spread_bias2()
                 if i >= 2:
                     for head in HEADS:
                         second(i - 2, head)
-                if i >= 3:
-                    exp(2 * (i - 3), 2 * (i - 2))
-                if turning:
-                    turn(i + 2, 2)
-                    turn(i + 2, 3)
-                if i + 3 < CHUNKS:
-                    widen(i + 3)
-                if i >= 2:
-                    for head in HEADS:
                         add_bias(i - 2, head)
-                quantise_a(i - 1, POST)
-                first(i, POST)
+                for a in (0, 1):
+                    turn_c(i + 1, E, a)
+                    unload_e(nc.scalar.copy, i + 1, a)
+                if i + 2 < CHUNKS:
+                    widen(nc.scalar.copy, i + 2)
+                quantise_c(i + 1, H)
                 interleave(i, PRIOR)
-                if turning:
-                    quantise_c(i + 2)
+                if i == 0:
+                    turn_w2()
+                layer1(i, POST)
+                quantise_c(i + 1, E)
+                if i == 0:
+                    quantise_w2()
+                else:
+                    quantise_a(i - 1, POST)
                 quantise_a(i, PRIOR)
+                if i + 2 < CHUNKS:
+                    for a in (0, 1):
+                        turn_c(i + 2, H, a)
 
             last = CHUNKS - 1
-            early = 2 * (last - 1)
-            first(last, PRIOR)
-            for head in HEADS:
-                second(last - 2, head)
-            exp(2 * (last - 3), 2 * (last - 2))
+            layer1(last, POST)
             interleave(last - 1, POST)
             for head in HEADS:
+                second(last - 2, head)
                 add_bias(last - 2, head)
             quantise_a(last - 1, POST)
-            first(last, POST)
-            exp(2 * (last - 2), 2 * (last - 1))
-            for e in range(0, early, 4):
-                log(e, e + 4)
-            interleave(last, PRIOR)
-            for head in HEADS:
-                second(last - 1, head)
-            add_bias(last - 1, PRIOR)
-            quantise_a(last, PRIOR)
-            add_bias(last - 1, POST)
-            exp(2 * (last - 1), 2 * last)
+            layer1(last, PRIOR)
             interleave(last, POST)
-            second(last, PRIOR)
-            add_bias(last, PRIOR)
-            exp(2 * last, 2 * last + 1)
+            second(last - 1, PRIOR)
+            add_bias(last - 1, PRIOR)
             quantise_a(last, POST)
-            std(0, 4)
-            second(last, POST)
-            add_bias(last, POST)
-            exp(2 * last + 1, 2 * last + 2)
-            for e in range(4, early, 4):
-                std(e, e + 4)
-            for e in (early, early + 2):
-                log(e, e + 2)
-                std(e, e + 2)
+            interleave(last, PRIOR)
+            second(last - 1, POST)
+            add_bias(last - 1, POST)
+            quantise_a(last, PRIOR)
+            exp(0, last - 1)
+            exp(last - 1, last)
+            for head in (POST, PRIOR):
+                second(last, head)
+                add_bias(last, head)
+            exp(last, CHUNKS)
+            for i0, i1 in ((0, 1), (1, 3), (3, 5), (5, 7), (7, 8)):
+                log(i0, i1)
+                std(i0, i1)

@@ -27,9 +27,9 @@ TURNED, ACCS = 2, 4
 EXACT_ABOVE = 40.0
 PRIOR, POST = 0, 1
 HEADS = (PRIOR, POST)
+BOTH, ONLY = slice(0, 2), (slice(0, 1), slice(1, 2))
 MEAN, STD = 0, 1
 H, E = 0, 1
-PASSES = {PRIOR: ((0, H),), POST: ((1, H), (2, E))}
 
 
 def tile_rssmcell_pb_t_kernel(
@@ -42,20 +42,25 @@ def tile_rssmcell_pb_t_kernel(
         work = ctx.enter_context(tc.tile_pool(name="work", bufs=2))
         psum = ctx.enter_context(tc.psum_pool(name="psum", bufs=1))
 
-        bias2_row = keep.tile([P, 2 * DIST], BF16, name="bias2_row", tag="bias2_row")
-        ones = keep.tile([P, P], BF16, name="ones", tag="ones")
+        bias2_raw = [keep.tile([P, 1], BF16, name="bias2_raw_%d" % e, tag="bias2_raw_%d" % e) for e in HEADS]
+        bias2_column = keep.tile([P, 2], F32, name="bias2_column", tag="bias2_column")
+        ones = keep.tile([P, P], F32, name="ones", tag="ones")
         ident = keep.tile([P, P], F32, name="ident", tag="ident")
         scale = keep.tile([P, PACK], F32, name="scale", tag="scale")
         bias1_raw = [keep.tile([P, PACK], BF16, name="bias1_raw_%d" % e, tag="bias1_raw_%d" % e) for e in HEADS]
         bias1 = [keep.tile([P, PACK], F32, name="bias1_%d" % e, tag="bias1_%d" % e) for e in HEADS]
         bias2 = keep.tile([P, 2, 2, LAT], F32, name="bias2", tag="bias2")
         exp_tenth = keep.tile([P, 1], F32, name="exp_tenth", tag="exp_tenth")
-        w1_rows = [keep.tile([P, PACK, KIN], BF16, name="w1_rows_%d" % w, tag="w1_rows_%d" % w) for w in range(3)]
+        w1_rows, w1_codes, w1_scales = {}, {}, {}
+        for head in HEADS:
+            for a in (0, 1):
+                name = "w1_%d_%d" % (head, a)
+                w1_rows[head, a] = keep.tile([P, 2, (1 + head) * KIN], BF16, name=name, tag=name)
+                w1_codes[head, a] = keep.tile([P, 1 + head, HALF], U32, name=name + "c", tag=name + "c", align_bytes=64)
+                w1_scales[head, a] = keep.tile([P, 1 + head, HALF], U8, name=name + "s", tag=name + "s", align_bytes=64)
         w2_rows = keep.tile([P, 2, HID], BF16, name="w2_rows", tag="w2_rows")
         value = keep.tile([P, 2, 2, CHUNKS * J, LAT], F32, name="value", tag="value")
         soft = keep.tile([P, 2, CHUNKS * J * LAT], F32, name="soft", tag="soft")
-        w1_codes = keep.tile([P, 3, HID], U32, name="w1_codes", tag="w1_codes", align_bytes=64)
-        w1_scales = keep.tile([P, 3, HID], U8, name="w1_scales", tag="w1_scales", align_bytes=64)
         w2_codes = keep.tile([P, 2, DIST], U32, name="w2_codes", tag="w2_codes", align_bytes=64)
         w2_scales = keep.tile([P, 2, DIST], U8, name="w2_scales", tag="w2_scales", align_bytes=64)
 
@@ -76,20 +81,27 @@ def tile_rssmcell_pb_t_kernel(
             nc.vector.quantize_mx(out=codes.bitcast(FP8X4), scales=scales, in_=grouped.rearrange("p n t -> p (n t)"))
 
 
-        def turn_w1(w, a):
-            turn(("w", w, a), w1_rows[w][:, 2 * a : 2 * a + 2], "acc", ACCS)
+        def load_w1(head, a):
+            rows = (wp1, wq1)[head].rearrange("(m t) k -> m t k", t=PACK)
+            nc.sync.dma_start(out=w1_rows[head, a][:], in_=rows[:, 2 * a : 2 * a + 2])
 
-        def unload_w1(copy, w, a):
-            if a == 0:
-                w1_grouped[w] = work.tile([P, HID, PACK], BF16, name="w1_grouped", tag="w1_grouped", bufs=2, align_bytes=64)
-            unload(copy, ("w", w, a), w1_grouped[w][:, a * HALF : (a + 1) * HALF])
+        def turn_w1(head, a, g, tag, bufs):
+            turn(("w", head, a, g), w1_rows[head, a][:, :, g * KIN : (g + 1) * KIN], tag, bufs)
 
-        def quantise_w1(w):
-            quantise(w1_codes[:, w], w1_scales[:, w], w1_grouped[w][:])
+        def unload_w1(copy, head, a, g):
+            if g == H:
+                w1_grouped[head, a] = work.tile(
+                    [P, CHUNK, PACK], BF16, name="w1_grouped", tag="a_grouped_%d" % (1 - a), bufs=1, align_bytes=64)
+            unload(copy, ("w", head, a, g), w1_grouped[head, a][:, g * HALF : (g + 1) * HALF])
 
-        def warm_up(tag, bufs):
-            unread = psum.tile([P, 2, P], F32, name="unread", tag=tag, bufs=bufs)
-            nc.tensor.matmul(out=unread[:], lhsT=ident[:], rhs=ident[:].unsqueeze(1).to_broadcast([P, 2, P]), start=True, stop=True)
+        def quantise_w1(head, a):
+            quantise(w1_codes[head, a][:].rearrange("p g m -> p (g m)"), w1_scales[head, a][:].rearrange("p g m -> p (g m)"),
+                     w1_grouped[head, a][:, 0 : (1 + head) * HALF])
+
+        def warm_up(copies):
+            unread = psum.tile([P, copies, P], F32, name="unread", tag="acc", bufs=ACCS)
+            nc.tensor.matmul(
+                out=unread[:], lhsT=ones[:], rhs=ones[:].unsqueeze(1).to_broadcast([P, copies, P]), start=True, stop=True)
 
 
         def load_h(i):
@@ -125,46 +137,48 @@ def tile_rssmcell_pb_t_kernel(
             unload(copy, (i, E, a), grouped_half(i, E, a))
 
         def quantise_c(i, g):
-            c_codes[i, g] = work.tile([P, CHUNK], U32, name="c_codes", tag="c_codes_%d" % g, bufs=3, align_bytes=64)
-            c_scales[i, g] = work.tile([P, CHUNK], U8, name="c_scales", tag="c_scales_%d" % g, bufs=3, align_bytes=64)
+            c_codes[i, g] = work.tile([P, CHUNK], U32, name="c_codes", tag="c_codes_%d" % g, bufs=4 - g, align_bytes=64)
+            c_scales[i, g] = work.tile([P, CHUNK], U8, name="c_scales", tag="c_scales_%d" % g, bufs=4 - g, align_bytes=64)
             quantise(c_codes[i, g][:], c_scales[i, g][:], c_grouped[i, g][:])
 
 
-        def first(i, head, t):
-            acc[i, head, t] = psum.tile([P, CHUNK], F32, name="acc", tag="acc", bufs=ACCS)
-            cols = slice(t * P, (t + 1) * P)
-            passes = PASSES[head]
-            for n, (w, g) in enumerate(passes):
+        def first(i, head, t, n0=0, n1=CHUNK):
+            acc[i, head, t] = psum.tile([P, n1 - n0], F32, name="acc", tag="acc", bufs=ACCS)
+            a, cols = t // 2, slice(t % 2 * P, (t % 2 + 1) * P)
+            for g in range(1 + head):
                 nc.tensor.matmul_mx(
-                    out=acc[i, head, t][:], lhsT=w1_codes[:, w, cols].bitcast(FP8X4), lhsT_scale=w1_scales[:, w, cols],
-                    rhs=c_codes[i, g][:].bitcast(FP8X4), rhs_scale=c_scales[i, g][:],
-                    start=(n == 0), stop=(n == len(passes) - 1))
+                    out=acc[i, head, t][:],
+                    lhsT=w1_codes[head, a][:, g, cols].bitcast(FP8X4), lhsT_scale=w1_scales[head, a][:, g, cols],
+                    rhs=c_codes[i, g][:, n0:n1].bitcast(FP8X4), rhs_scale=c_scales[i, g][:, n0:n1],
+                    start=(g == 0), stop=(g == head))
 
-        def plane(i, head, t):
-            if t == 0:
+        def plane(i, head, t, n0, n1):
+            if t == 0 and n0 == 0:
                 planes[i, head] = work.tile([P, PACK, CHUNK], BF16, name="planes", tag="planes_%d" % head, bufs=2, align_bytes=64)
-            return planes[i, head][:, t, :]
+            return planes[i, head][:, t, n0:n1]
 
-        def relu(i, head, t):
-            nc.scalar.activation(out=plane(i, head, t), in_=acc[i, head, t][:], func=ACT.Relu, bias=bias1[head][:, t : t + 1])
+        def relu(i, head, t, n0=0, n1=CHUNK):
+            nc.scalar.activation(
+                out=plane(i, head, t, n0, n1), in_=acc[i, head, t][:], func=ACT.Relu, bias=bias1[head][:, t : t + 1])
 
-        def relu_on_vector(i, head, t):
-            nc.vector.tensor_scalar(out=plane(i, head, t), in0=acc[i, head, t][:], scalar1=bias1[head][:, t : t + 1],
+        def relu_on_vector(i, head, t, n0=0, n1=CHUNK):
+            nc.vector.tensor_scalar(out=plane(i, head, t, n0, n1), in0=acc[i, head, t][:], scalar1=bias1[head][:, t : t + 1],
                                     scalar2=0.0, op0=ALU.add, op1=ALU.max)
 
-        def layer1(i, head):
-            for t in range(PACK):
-                first(i, head, t)
-                relu(i, head, t)
+        def layer1(i, head, tiles=range(PACK), n0=0, n1=CHUNK, on_vector=()):
+            for t in tiles:
+                first(i, head, t, n0, n1)
+                (relu_on_vector if t in on_vector else relu)(i, head, t, n0, n1)
 
         def new_grouped(i, head):
             a_grouped[i, head] = work.tile([P, CHUNK, PACK], BF16, name="a_grouped", tag="a_grouped_%d" % head, bufs=1, align_bytes=64)
 
-        def interleave(i, head):
-            new_grouped(i, head)
+        def interleave(i, head, n0=0, n1=CHUNK):
+            if n0 == 0:
+                new_grouped(i, head)
             nc.vector.tensor_copy(
-                out=a_grouped[i, head][:].rearrange("p (c i) t -> p c t i", i=4),
-                in_=planes[i, head][:].rearrange("p t (c i) -> p c t i", i=4))
+                out=a_grouped[i, head][:, n0:n1].rearrange("p (c i) t -> p c t i", i=4),
+                in_=planes[i, head][:, :, n0:n1].rearrange("p t (c i) -> p c t i", i=4))
 
         def interleave_on_gpsimd(i, head):
             new_grouped(i, head)
@@ -172,53 +186,57 @@ def tile_rssmcell_pb_t_kernel(
                 out=a_grouped[i, head][:], in0=planes[i, head][:].rearrange("p t n -> p n t"),
                 scalar1=1.0, scalar2=0.0, op0=ALU.mult, op1=ALU.add)
 
-        def quantise_a(i, head):
-            a_codes[i, head] = work.tile([P, CHUNK], U32, name="a_codes", tag="a_codes", bufs=4, align_bytes=64)
-            a_scales[i, head] = work.tile([P, CHUNK], U8, name="a_scales", tag="a_scales", bufs=4, align_bytes=64)
-            quantise(a_codes[i, head][:], a_scales[i, head][:], a_grouped[i, head][:])
+        def quantise_a(i, head, n0=0, n1=CHUNK):
+            if n0 == 0:
+                a_codes[i, head] = work.tile([P, CHUNK], U32, name="a_codes", tag="a_codes", bufs=4, align_bytes=64)
+                a_scales[i, head] = work.tile([P, CHUNK], U8, name="a_scales", tag="a_scales", bufs=4, align_bytes=64)
+            quantise(a_codes[i, head][:, n0:n1], a_scales[i, head][:, n0:n1], a_grouped[i, head][:, n0:n1])
 
 
-        def second(i, head):
-            result[i, head] = psum.tile([P, J, 2, LAT], F32, name="result", tag="result_%d" % head, bufs=1)
-            for j in range(J):
+        def second(i, head, j0=0, j1=J, tag=None, bufs=1):
+            result[i, head, j0] = psum.tile([P, j1 - j0, 2, LAT], F32, name="result", tag=tag or "result_%d" % head, bufs=bufs)
+            for j in range(j0, j1):
                 cols = slice(j * P, (j + 1) * P)
                 nc.tensor.matmul_mx(
-                    out=result[i, head][:, j, :, :].rearrange("p h c -> p (h c)"),
+                    out=result[i, head, j0][:, j - j0, :, :].rearrange("p h c -> p (h c)"),
                     lhsT=a_codes[i, head][:, cols].bitcast(FP8X4), lhsT_scale=a_scales[i, head][:, cols],
                     rhs=w2_codes[:, head, :].bitcast(FP8X4), rhs_scale=w2_scales[:, head, :], start=True, stop=True)
 
-        def store(dst, head, half, i0, i1):
-            tokens = slice(i0 * J, i1 * J)
-            nc.sync.dma_start(out=dst.rearrange("(p n) d -> p n d", p=P)[:, tokens], in_=value[:, head, half, tokens])
+        def store(head, half, n0, n1):
+            dst = ((prior_mean, prior_std), (post_mean, post_std))[head][half]
+            nc.sync.dma_start(out=dst.rearrange("(p n) d -> p n d", p=P)[:, n0:n1], in_=value[:, head, half, n0:n1])
 
-        def add_bias(i, head):
+        def add_bias(i, head, halves=(MEAN, STD), j0=0, j1=J):
+            part = slice(halves[0], halves[-1] + 1)
             nc.vector.tensor_tensor(
-                out=value[:, head, :, i * J : (i + 1) * J].rearrange("p h j c -> p j h c"),
-                in0=result[i, head][:],
-                in1=bias2[:, head].unsqueeze(1).to_broadcast([P, J, 2, LAT]),
+                out=value[:, head, part, i * J + j0 : i * J + j1].rearrange("p h j c -> p j h c"),
+                in0=result[i, head, j0][:, :, part],
+                in1=bias2[:, head, part].unsqueeze(1).to_broadcast([P, j1 - j0, len(halves), LAT]),
                 op=ALU.add)
-            store((prior_mean, post_mean)[head], head, MEAN, i, i + 1)
+            if MEAN in halves:
+                store(head, MEAN, i * J + j0, i * J + j1)
 
-        def w_of(i0, i1):
-            return value[:, :, STD, i0 * J : i1 * J].rearrange("p e n c -> p e (n c)")
+        def w_of(heads, n0, n1):
+            return value[:, heads, STD, n0:n1].rearrange("p e n c -> p e (n c)")
 
-        def soft_of(i0, i1):
-            return soft[:, :, i0 * J * LAT : i1 * J * LAT]
+        def soft_of(heads, n0, n1):
+            return soft[:, heads, n0 * LAT : n1 * LAT]
 
-        def exp(i0, i1):
-            nc.scalar.activation(out=soft_of(i0, i1), in_=w_of(i0, i1), func=ACT.Exp)
+        def exp(heads, n0, n1):
+            nc.scalar.activation(out=soft_of(heads, n0, n1), in_=w_of(heads, n0, n1), func=ACT.Exp)
 
-        def log(i0, i1):
-            nc.scalar.activation(out=soft_of(i0, i1), in_=soft_of(i0, i1), func=ACT.Ln, bias=exp_tenth[:])
+        def log(heads, n0, n1):
+            nc.scalar.activation(out=soft_of(heads, n0, n1), in_=soft_of(heads, n0, n1), func=ACT.Ln, bias=exp_tenth[:])
 
-        def std(i0, i1):
+        def std(heads, n0, n1):
             nc.vector.scalar_tensor_tensor(
-                out=w_of(i0, i1), in0=soft_of(i0, i1), scalar=EXACT_ABOVE, in1=w_of(i0, i1), op0=ALU.min, op1=ALU.max)
-            for head in HEADS:
-                store((prior_std, post_std)[head], head, STD, i0, i1)
+                out=w_of(heads, n0, n1), in0=soft_of(heads, n0, n1), scalar=EXACT_ABOVE, in1=w_of(heads, n0, n1),
+                op0=ALU.min, op1=ALU.max)
+            for head in HEADS[heads]:
+                store(head, STD, n0, n1)
 
-        def turn_w2():
-            turn("w2", w2_rows[:], "result_1", 1)
+        def turn_w2(tag, bufs):
+            turn("w2", w2_rows[:], tag, bufs)
             new_grouped("w2", POST)
             unload(nc.scalar.copy, "w2", a_grouped["w2", POST][:, 0:HALF])
 
@@ -226,131 +244,172 @@ def tile_rssmcell_pb_t_kernel(
             quantise(w2_codes[:].rearrange("p e m -> p (e m)"), w2_scales[:].rearrange("p e m -> p (e m)"),
                      a_grouped["w2", POST][:, 0:HALF])
 
-        def spread_bias2():
-            spread = psum.tile([P, 2, 2, LAT], F32, name="spread", tag="result_0", bufs=1)
-            nc.tensor.matmul(
-                out=spread[:].rearrange("p e h c -> p (e h c)"), lhsT=ones[:], rhs=bias2_row[:], start=True, stop=True)
+        def spread_bias2(tag, bufs):
+            spread = psum.tile([P, 2, 2, LAT], F32, name="spread", tag=tag, bufs=bufs)
+            for head in HEADS:
+                nc.tensor.matmul(
+                    out=spread[:, head].rearrange("p h c -> p (h c)"),
+                    lhsT=bias2_column[:, head : head + 1].to_broadcast([P, P]), rhs=ident[:], start=True, stop=True)
             nc.vector.tensor_copy(out=bias2[:, :, MEAN], in_=spread[:, :, MEAN])
             nc.vector.tensor_scalar(out=bias2[:, :, STD], in0=spread[:, :, STD], scalar1=0.1, scalar2=None, op0=ALU.add)
 
         with tc.manual_schedule():
             nc.vector.memset(ones[:], 1.0)
-            nc.vector.memset(bias2_row[:], 0.0)
             make_identity(nc, ident[:])
             nc.scalar.dma_start(out=scale[:], in_=h_scale.rearrange("o (p t) -> p (o t)", t=PACK))
-            nc.scalar.dma_start(out=bias1_raw[PRIOR][:], in_=bp1.rearrange("(m t) -> m t", t=PACK))
-            nc.scalar.dma_start(out=bias1_raw[POST][:], in_=bq1.rearrange("(m t) -> m t", t=PACK))
+            nc.scalar.dma_start(out=bias2_raw[PRIOR][:], in_=bp2.unsqueeze(1))
+            nc.scalar.dma_start(out=bias2_raw[POST][:], in_=bq2.unsqueeze(1))
             nc.scalar.activation(out=exp_tenth[:], in_=ones[:, 0:1], func=ACT.Exp, scale=0.1)
             load_h(0)
-            nc.sync.dma_start(out=w1_rows[0][:], in_=wp1.rearrange("(m t) k -> m t k", t=PACK))
+            load_w1(PRIOR, 0)
+            load_w1(PRIOR, 1)
             load_h(1)
-            load_embedding(0)
-            for g in (H, E):
-                nc.sync.dma_start(
-                    out=w1_rows[1 + g][:], in_=wq1.rearrange("(m t) k -> m t k", t=PACK)[:, :, g * KIN : (g + 1) * KIN])
-            load_embedding(1)
             load_h(2)
+            load_embedding(0)
+            nc.sync.dma_start(out=bias1_raw[PRIOR][:], in_=bp1.rearrange("(m t) -> m t", t=PACK))
+            nc.sync.dma_start(out=bias1_raw[POST][:], in_=bq1.rearrange("(m t) -> m t", t=PACK))
+            load_w1(POST, 0)
+            load_w1(POST, 1)
+            load_embedding(1)
+            load_h(3)
             nc.sync.dma_start(out=w2_rows[:, PRIOR, :], in_=wp2)
             nc.sync.dma_start(out=w2_rows[:, POST, :], in_=wq2)
-            nc.sync.dma_start(out=bias2_row[0:1, 0:DIST], in_=bp2.unsqueeze(0))
-            nc.sync.dma_start(out=bias2_row[0:1, DIST : 2 * DIST], in_=bq2.unsqueeze(0))
             for i in range(2, CHUNKS):
                 load_embedding(i)
-                if i + 1 < CHUNKS:
-                    load_h(i + 1)
+                if i + 2 < CHUNKS:
+                    load_h(i + 2)
 
-            for n in range(3):
-                warm_up("acc", ACCS)
+            warm_up(4)
+            warm_up(2)
             widen(nc.vector.tensor_copy, 0, 0, 2)
-            widen(nc.vector.tensor_copy, 0, 2, 4)
+            for head in HEADS:
+                nc.vector.tensor_copy(out=bias2_column[:, head : head + 1], in_=bias2_raw[head][:])
+            widen(nc.scalar.copy, 0, 2, 4)
             for a in (0, 1):
                 turn_c(0, H, a)
                 scale_h(0, a)
+            spread_bias2("result_0", 1)
             widen(nc.scalar.copy, 1)
             for a in (0, 1):
-                turn_w1(0, a)
-                unload_w1(nc.scalar.copy, 0, a)
-            warm_up("acc", ACCS)
-            for head in HEADS:
-                nc.vector.tensor_copy(out=bias1[head][:], in_=bias1_raw[head][:])
-            quantise_w1(0)
+                turn_w1(PRIOR, a, H, "acc", ACCS)
+                unload_w1(nc.scalar.copy, PRIOR, a, H)
+            widen(nc.scalar.copy, 2)
+            warm_up(2)
             quantise_c(0, H)
             for a in (0, 1):
-                turn_c(0, E, a, "result_%d" % a, 1)
-                unload_e(nc.scalar.copy, 0, a)
+                quantise_w1(PRIOR, a)
+            for head in HEADS:
+                nc.vector.tensor_copy(out=bias1[head][:], in_=bias1_raw[head][:])
             for a in (0, 1):
                 turn_c(1, H, a)
                 scale_h(1, a)
-            for t in (0, 1):
-                first(0, PRIOR, t)
-                relu(0, PRIOR, t)
+            layer1(0, PRIOR, (0, 1))
             for a in (0, 1):
-                turn_w1(1, a)
-                unload_w1(nc.scalar.copy, 1, a)
+                turn_c(0, E, a, "result_%d" % a, 1)
+                unload_e(nc.scalar.copy, 0, a)
+            layer1(0, PRIOR, (2, 3))
+            quantise_c(1, H)
             quantise_c(0, E)
-            for t in (2, 3):
-                first(0, PRIOR, t)
-                relu(0, PRIOR, t)
+            for g in (H, E):
+                turn_w1(POST, 0, g, "turned", TURNED)
+                unload_w1(nc.scalar.copy, POST, 0, g)
+            layer1(1, PRIOR, (0, 1))
+            for g in (H, E):
+                turn_w1(POST, 1, g, "result_%d" % g, 1)
+                unload_w1(nc.vector.tensor_copy, POST, 1, g)
+            quantise_w1(POST, 0)
+            layer1(1, PRIOR, (2, 3))
             for a in (0, 1):
-                turn(("w", 2, a), w1_rows[2][:, 2 * a : 2 * a + 2], "result_%d" % a, 1)
-                unload_w1(nc.vector.tensor_copy, 2, a)
-            quantise_w1(1)
-            quantise_w1(2)
+                turn_c(2, H, a)
+            quantise_w1(POST, 1)
+            interleave_on_gpsimd(0, PRIOR)
+            for a in (0, 1):
+                scale_h(2, a)
+            layer1(0, POST, (0, 1))
+            widen(nc.scalar.copy, 3)
+            for a in (0, 1):
+                turn_c(1, E, a, "result_%d" % a, 1)
+                unload_e((nc.scalar.copy, nc.vector.tensor_copy)[a], 1, a)
+            turn_w2("acc", ACCS)
+            layer1(0, POST, (2, 3))
+            quantise_c(2, H)
+            quantise_a(0, PRIOR)
+            quantise_c(1, E)
+            interleave(1, PRIOR)
+            quantise_w2()
+            quantise_a(1, PRIOR)
+            for a in (0, 1):
+                turn_c(3, H, a)
 
-            for i in range(CHUNKS - 1):
-                if i >= 1:
-                    interleave_on_gpsimd(i - 1, POST)
-                    for a in (0, 1):
-                        scale_h(i + 1, a)
-                    layer1(i, PRIOR)
-                if i == 1:
-                    spread_bias2()
+            for i in range(1, CHUNKS - 2):
+                interleave_on_gpsimd(i - 1, POST)
+                for a in (0, 1):
+                    scale_h(i + 2, a)
+                layer1(i + 1, PRIOR)
+                second(i - 1, PRIOR)
+                add_bias(i - 1, PRIOR)
                 if i >= 2:
-                    for head in HEADS:
-                        second(i - 2, head)
-                        add_bias(i - 2, head)
+                    second(i - 2, POST)
+                    add_bias(i - 2, POST)
+                for t in (0, 1):
+                    first(i, POST, t)
+                if i + 3 < CHUNKS:
+                    widen(nc.scalar.copy, i + 3)
                 for a in (0, 1):
                     turn_c(i + 1, E, a)
                     unload_e(nc.scalar.copy, i + 1, a)
-                if i + 2 < CHUNKS:
-                    widen(nc.scalar.copy, i + 2)
-                quantise_c(i + 1, H)
-                interleave(i, PRIOR)
-                if i == 0:
-                    turn_w2()
-                layer1(i, POST)
+                quantise_c(i + 2, H)
+                interleave(i + 1, PRIOR)
+                for t in (2, 3):
+                    first(i, POST, t)
+                for t in range(PACK):
+                    relu(i, POST, t)
                 quantise_c(i + 1, E)
-                if i == 0:
-                    quantise_w2()
-                else:
-                    quantise_a(i - 1, POST)
-                quantise_a(i, PRIOR)
-                if i + 2 < CHUNKS:
+                quantise_a(i - 1, POST)
+                quantise_a(i + 1, PRIOR)
+                if i + 3 < CHUNKS:
                     for a in (0, 1):
-                        turn_c(i + 2, H, a)
+                        turn_c(i + 3, H, a)
 
             last = CHUNKS - 1
+            for a in (0, 1):
+                turn_c(last, E, a)
+                unload_e(nc.scalar.copy, last, a)
+            interleave(last - 2, POST)
+            layer1(last, PRIOR)
+            second(last - 2, PRIOR)
+            add_bias(last - 2, PRIOR)
+            quantise_c(last, E)
+            quantise_a(last - 2, POST)
+            second(last - 3, POST)
+            add_bias(last - 3, POST)
+            layer1(last - 1, POST)
+            interleave(last, PRIOR)
+            second(last - 1, PRIOR)
+            add_bias(last - 1, PRIOR, (STD,))
+            quantise_a(last, PRIOR)
+            second(last - 2, POST)
             layer1(last, POST)
             interleave(last - 1, POST)
-            for head in HEADS:
-                second(last - 2, head)
-                add_bias(last - 2, head)
+            add_bias(last - 2, POST, (STD,))
+            second(last, PRIOR, tag="turned", bufs=TURNED)
             quantise_a(last - 1, POST)
-            layer1(last, PRIOR)
+            add_bias(last, PRIOR, (STD,))
             interleave(last, POST)
-            second(last - 1, PRIOR)
-            add_bias(last - 1, PRIOR)
+            second(last - 1, POST, tag="turned", bufs=TURNED)
+            add_bias(last - 1, POST, (STD,))
             quantise_a(last, POST)
-            interleave(last, PRIOR)
-            second(last - 1, POST)
-            add_bias(last - 1, POST)
-            quantise_a(last, PRIOR)
-            exp(0, last - 1)
-            exp(last - 1, last)
-            for head in (POST, PRIOR):
-                second(last, head)
-                add_bias(last, head)
-            exp(last, CHUNKS)
-            for i0, i1 in ((0, 1), (1, 3), (3, 5), (5, 7), (7, 8)):
-                log(i0, i1)
-                std(i0, i1)
+            add_bias(last - 1, PRIOR, (MEAN,))
+            add_bias(last - 2, POST, (MEAN,))
+            exp(BOTH, 0, (last - 1) * J)
+            exp(ONLY[PRIOR], (last - 1) * J, CHUNKS * J)
+            exp(ONLY[POST], (last - 1) * J, last * J)
+            second(last, POST, tag="acc", bufs=ACCS)
+            add_bias(last, POST, (STD,))
+            exp(ONLY[POST], last * J, CHUNKS * J)
+            add_bias(last, PRIOR, (MEAN,))
+            add_bias(last - 1, POST, (MEAN,))
+            add_bias(last, POST, (MEAN,))
+            for n0, n1 in ((0, 2), (2, 8), (8, 16), (16, 24), (24, 30), (30, 32)):
+                log(BOTH, n0, n1)
+                std(BOTH, n0, n1)

@@ -91,7 +91,7 @@ def tile_rssmcell_pb_t_kernel(
         def unload_w1(copy, head, a, g):
             if g == H:
                 w1_grouped[head, a] = work.tile(
-                    [P, CHUNK, PACK], BF16, name="w1_grouped", tag="a_grouped_%d" % (1 - a), bufs=1, align_bytes=64)
+                    [P, CHUNK, PACK], BF16, name="w1_grouped", tag="a_grouped_%d" % a, bufs=1, align_bytes=64)
             unload(copy, ("w", head, a, g), w1_grouped[head, a][:, g * HALF : (g + 1) * HALF])
 
         def quantise_w1(head, a):
@@ -109,12 +109,12 @@ def tile_rssmcell_pb_t_kernel(
             nc.sync.dma_start(out=h_raw[i][:], in_=h_bytes.rearrange("(p c j) k -> c p j k", p=P, j=J)[i])
 
         def load_embedding(i):
-            emb[i] = work.tile([P, J, KIN], BF16, name="emb", tag="emb", bufs=CHUNKS)
+            emb[i] = work.tile([P, J, KIN], BF16, name="emb", tag="emb", bufs=6)
             nc.sync.dma_start(out=emb[i][:], in_=embedding.rearrange("(p c j) k -> c p j k", p=P, j=J)[i])
 
         def widen(copy, i, j0=0, j1=J):
             if j0 == 0:
-                h_wide[i] = work.tile([P, J, KIN], BF16, name="h_wide", tag="h_wide", bufs=2, align_bytes=64)
+                h_wide[i] = work.tile([P, J, KIN], BF16, name="h_wide", tag="h_wide", bufs=5, align_bytes=64)
             copy(out=h_wide[i][:, j0:j1].rearrange("p j k -> p (j k)"),
                  in_=h_raw[i][:, j0:j1].rearrange("p j k -> p (j k)").bitcast(FP8))
 
@@ -173,17 +173,17 @@ def tile_rssmcell_pb_t_kernel(
         def new_grouped(i, head):
             a_grouped[i, head] = work.tile([P, CHUNK, PACK], BF16, name="a_grouped", tag="a_grouped_%d" % head, bufs=1, align_bytes=64)
 
-        def interleave(i, head, n0=0, n1=CHUNK):
-            if n0 == 0:
+        def interleave(i, head, n0=0, n1=CHUNK, copy=nc.vector.tensor_copy):
+            if (i, head) not in a_grouped:
                 new_grouped(i, head)
-            nc.vector.tensor_copy(
+            copy(
                 out=a_grouped[i, head][:, n0:n1].rearrange("p (c i) t -> p c t i", i=4),
                 in_=planes[i, head][:, :, n0:n1].rearrange("p t (c i) -> p c t i", i=4))
 
-        def interleave_on_gpsimd(i, head):
+        def interleave_on_gpsimd(i, head, n1=CHUNK):
             new_grouped(i, head)
             nc.gpsimd.tensor_scalar(
-                out=a_grouped[i, head][:], in0=planes[i, head][:].rearrange("p t n -> p n t"),
+                out=a_grouped[i, head][:, 0:n1], in0=planes[i, head][:, :, 0:n1].rearrange("p t n -> p n t"),
                 scalar1=1.0, scalar2=0.0, op0=ALU.mult, op1=ALU.add)
 
         def quantise_a(i, head, n0=0, n1=CHUNK):
@@ -261,39 +261,43 @@ def tile_rssmcell_pb_t_kernel(
             nc.scalar.dma_start(out=bias2_raw[POST][:], in_=bq2.unsqueeze(1))
             nc.scalar.activation(out=exp_tenth[:], in_=ones[:, 0:1], func=ACT.Exp, scale=0.1)
             load_h(0)
-            load_w1(PRIOR, 0)
-            load_w1(PRIOR, 1)
             load_h(1)
             load_h(2)
-            load_embedding(0)
+            load_w1(PRIOR, 0)
+            load_w1(PRIOR, 1)
+            load_h(3)
+            load_h(4)
             nc.sync.dma_start(out=bias1_raw[PRIOR][:], in_=bp1.rearrange("(m t) -> m t", t=PACK))
             nc.sync.dma_start(out=bias1_raw[POST][:], in_=bq1.rearrange("(m t) -> m t", t=PACK))
+            load_embedding(0)
             load_w1(POST, 0)
+            load_h(5)
             load_w1(POST, 1)
             load_embedding(1)
-            load_h(3)
             nc.sync.dma_start(out=w2_rows[:, PRIOR, :], in_=wp2)
             nc.sync.dma_start(out=w2_rows[:, POST, :], in_=wq2)
-            for i in range(2, CHUNKS):
+            load_h(6)
+            load_h(7)
+            for i in range(2, 6):
                 load_embedding(i)
-                if i + 2 < CHUNKS:
-                    load_h(i + 2)
 
             warm_up(4)
-            warm_up(2)
+            warm_up(4)
             widen(nc.vector.tensor_copy, 0, 0, 2)
+            widen(nc.scalar.copy, 0, 2, 4)
+            widen(nc.vector.tensor_copy, 1)
             for head in HEADS:
                 nc.vector.tensor_copy(out=bias2_column[:, head : head + 1], in_=bias2_raw[head][:])
-            widen(nc.scalar.copy, 0, 2, 4)
             for a in (0, 1):
                 turn_c(0, H, a)
                 scale_h(0, a)
             spread_bias2("result_0", 1)
-            widen(nc.scalar.copy, 1)
+            widen(nc.scalar.copy, 2)
+            widen(nc.scalar.copy, 3)
             for a in (0, 1):
                 turn_w1(PRIOR, a, H, "acc", ACCS)
                 unload_w1(nc.scalar.copy, PRIOR, a, H)
-            widen(nc.scalar.copy, 2)
+            widen(nc.scalar.copy, 4)
             warm_up(2)
             quantise_c(0, H)
             for a in (0, 1):
@@ -307,9 +311,11 @@ def tile_rssmcell_pb_t_kernel(
             for a in (0, 1):
                 turn_c(0, E, a, "result_%d" % a, 1)
                 unload_e(nc.scalar.copy, 0, a)
+            load_embedding(6)
             layer1(0, PRIOR, (2, 3))
             quantise_c(1, H)
             quantise_c(0, E)
+            widen(nc.vector.tensor_copy, 5)
             for g in (H, E):
                 turn_w1(POST, 0, g, "turned", TURNED)
                 unload_w1(nc.scalar.copy, POST, 0, g)
@@ -319,19 +325,23 @@ def tile_rssmcell_pb_t_kernel(
                 unload_w1(nc.vector.tensor_copy, POST, 1, g)
             quantise_w1(POST, 0)
             layer1(1, PRIOR, (2, 3))
+            widen(nc.scalar.copy, 6)
             for a in (0, 1):
                 turn_c(2, H, a)
             quantise_w1(POST, 1)
-            interleave_on_gpsimd(0, PRIOR)
+            interleave_on_gpsimd(0, PRIOR, 384)
             for a in (0, 1):
                 scale_h(2, a)
             layer1(0, POST, (0, 1))
-            widen(nc.scalar.copy, 3)
             for a in (0, 1):
                 turn_c(1, E, a, "result_%d" % a, 1)
-                unload_e((nc.scalar.copy, nc.vector.tensor_copy)[a], 1, a)
+                unload_e(nc.scalar.copy, 1, a)
+            load_embedding(7)
+            layer1(0, POST, (2,))
             turn_w2("acc", ACCS)
-            layer1(0, POST, (2, 3))
+            layer1(0, POST, (3,))
+            widen(nc.scalar.copy, 7)
+            interleave(0, PRIOR, 384, CHUNK)
             quantise_c(2, H)
             quantise_a(0, PRIOR)
             quantise_c(1, E)
@@ -346,20 +356,24 @@ def tile_rssmcell_pb_t_kernel(
                 for a in (0, 1):
                     scale_h(i + 2, a)
                 layer1(i + 1, PRIOR)
-                second(i - 1, PRIOR)
-                add_bias(i - 1, PRIOR)
+                if i == 1:
+                    second(0, PRIOR, tag="result_1")
+                    add_bias(0, PRIOR)
+                second(i, PRIOR)
+                add_bias(i, PRIOR)
                 if i >= 2:
                     second(i - 2, POST)
                     add_bias(i - 2, POST)
                 for t in (0, 1):
                     first(i, POST, t)
-                if i + 3 < CHUNKS:
-                    widen(nc.scalar.copy, i + 3)
+                if i >= 3:
+                    exp(BOTH, (i - 3) * J, (i - 2) * J)
+                interleave(i + 1, PRIOR, CHUNK - 64, CHUNK, nc.scalar.copy)
                 for a in (0, 1):
                     turn_c(i + 1, E, a)
                     unload_e(nc.scalar.copy, i + 1, a)
                 quantise_c(i + 2, H)
-                interleave(i + 1, PRIOR)
+                interleave(i + 1, PRIOR, 0, CHUNK - 64)
                 for t in (2, 3):
                     first(i, POST, t)
                 for t in range(PACK):
@@ -377,38 +391,36 @@ def tile_rssmcell_pb_t_kernel(
                 unload_e(nc.scalar.copy, last, a)
             interleave(last - 2, POST)
             layer1(last, PRIOR)
-            second(last - 2, PRIOR)
-            add_bias(last - 2, PRIOR)
+            second(last - 1, PRIOR)
+            add_bias(last - 1, PRIOR)
             quantise_c(last, E)
             quantise_a(last - 2, POST)
             second(last - 3, POST)
             add_bias(last - 3, POST)
-            layer1(last - 1, POST)
             interleave(last, PRIOR)
-            second(last - 1, PRIOR)
-            add_bias(last - 1, PRIOR, (STD,))
-            quantise_a(last, PRIOR)
+            layer1(last - 1, POST)
             second(last - 2, POST)
-            layer1(last, POST)
-            interleave(last - 1, POST)
             add_bias(last - 2, POST, (STD,))
-            second(last, PRIOR, tag="turned", bufs=TURNED)
-            quantise_a(last - 1, POST)
+            quantise_a(last, PRIOR)
+            interleave(last - 1, POST)
+            layer1(last, POST)
+            second(last, PRIOR)
             add_bias(last, PRIOR, (STD,))
-            interleave(last, POST)
+            quantise_a(last - 1, POST)
+            add_bias(last - 2, POST, (MEAN,))
+            interleave(last, POST, 0, CHUNK - 160)
+            interleave(last, POST, CHUNK - 160, CHUNK, nc.scalar.copy)
             second(last - 1, POST, tag="turned", bufs=TURNED)
             add_bias(last - 1, POST, (STD,))
             quantise_a(last, POST)
-            add_bias(last - 1, PRIOR, (MEAN,))
-            add_bias(last - 2, POST, (MEAN,))
-            exp(BOTH, 0, (last - 1) * J)
+            add_bias(last, PRIOR, (MEAN,))
+            add_bias(last - 1, POST, (MEAN,))
+            exp(BOTH, (last - 4) * J, (last - 1) * J)
             exp(ONLY[PRIOR], (last - 1) * J, CHUNKS * J)
             exp(ONLY[POST], (last - 1) * J, last * J)
             second(last, POST, tag="acc", bufs=ACCS)
             add_bias(last, POST, (STD,))
             exp(ONLY[POST], last * J, CHUNKS * J)
-            add_bias(last, PRIOR, (MEAN,))
-            add_bias(last - 1, POST, (MEAN,))
             add_bias(last, POST, (MEAN,))
             for n0, n1 in ((0, 2), (2, 8), (8, 16), (16, 24), (24, 30), (30, 32)):
                 log(BOTH, n0, n1)

@@ -173,12 +173,17 @@ def tile_rssmcell_pb_t_kernel(
         def new_grouped(i, head):
             a_grouped[i, head] = work.tile([P, CHUNK, PACK], BF16, name="a_grouped", tag="a_grouped_%d" % head, bufs=1, align_bytes=64)
 
-        def interleave(i, head, n0=0, n1=CHUNK, copy=nc.vector.tensor_copy):
+        def interleave(i, head, n0=0, n1=CHUNK):
             if (i, head) not in a_grouped:
                 new_grouped(i, head)
-            copy(
+            nc.vector.tensor_copy(
                 out=a_grouped[i, head][:, n0:n1].rearrange("p (c i) t -> p c t i", i=4),
                 in_=planes[i, head][:, :, n0:n1].rearrange("p t (c i) -> p c t i", i=4))
+
+        def interleave_on_scalar(i, head, n0):
+            if (i, head) not in a_grouped:
+                new_grouped(i, head)
+            nc.scalar.copy(out=a_grouped[i, head][:, n0:CHUNK], in_=planes[i, head][:, :, n0:CHUNK].rearrange("p t n -> p n t"))
 
         def interleave_on_gpsimd(i, head, n1=CHUNK):
             new_grouped(i, head)
@@ -368,7 +373,7 @@ def tile_rssmcell_pb_t_kernel(
                     first(i, POST, t)
                 if i >= 3:
                     exp(BOTH, (i - 3) * J, (i - 2) * J)
-                interleave(i + 1, PRIOR, CHUNK - 64, CHUNK, nc.scalar.copy)
+                interleave_on_scalar(i + 1, PRIOR, CHUNK - 64)
                 for a in (0, 1):
                     turn_c(i + 1, E, a)
                     unload_e(nc.scalar.copy, i + 1, a)
@@ -409,7 +414,7 @@ def tile_rssmcell_pb_t_kernel(
             quantise_a(last - 1, POST)
             add_bias(last - 2, POST, (MEAN,))
             interleave(last, POST, 0, CHUNK - 160)
-            interleave(last, POST, CHUNK - 160, CHUNK, nc.scalar.copy)
+            interleave_on_scalar(last, POST, CHUNK - 160)
             second(last - 1, POST, tag="turned", bufs=TURNED)
             add_bias(last - 1, POST, (STD,))
             quantise_a(last, POST)

@@ -23,7 +23,8 @@ FP8X4 = mybir.dt.float8_e4m3fn_x4
 ACT = mybir.ActivationFunctionType
 ALU = mybir.AluOpType
 
-TURNED, ACCS = 2, 4
+BANKS = 4
+LEAD = 1
 EXACT_ABOVE = 40.0
 PRIOR, POST = 0, 1
 HEADS = (PRIOR, POST)
@@ -65,14 +66,20 @@ def tile_rssmcell_pb_t_kernel(
         w2_scales = keep.tile([P, 2, DIST], U8, name="w2_scales", tag="w2_scales", align_bytes=64)
 
         h_raw, emb, h_wide, turned, c_grouped, c_codes, c_scales = {}, {}, {}, {}, {}, {}, {}
+        sorted_chunks = set()
         w1_grouped, acc, planes, a_grouped, a_codes, a_scales, result = {}, {}, {}, {}, {}, {}, {}
 
-        def turn(key, rows, tag="turned", bufs=TURNED):
-            turned[key] = psum.tile([P, 2, HALF], F32, name="turned", tag=tag, bufs=bufs)
+        def turn(key, words, bank):
+            turned[key] = bank
             for a in (0, 1):
-                words = rows[:, a, :].bitcast(F32)
                 for u in (0, 1):
-                    nc.tensor.transpose(turned[key][:, u, a * P : (a + 1) * P], words[:, u : KIN // 2 : 2], ident[:])
+                    nc.tensor.transpose(bank[:, u, a * P : (a + 1) * P], words(a, u), ident[:])
+
+        def every_second_word(rows):
+            return lambda a, u: rows[:, a, :].bitcast(F32)[:, u : KIN // 2 : 2]
+
+        def bank_of(tag):
+            return psum.tile([P, 2, HALF], F32, name="turned", tag=tag, bufs=BANKS)
 
         def unload(copy, key, dst):
             copy(out=dst.bitcast(F32), in_=turned[key][:].rearrange("p u n -> p n u"))
@@ -85,8 +92,8 @@ def tile_rssmcell_pb_t_kernel(
             rows = (wp1, wq1)[head].rearrange("(m t) k -> m t k", t=PACK)
             nc.sync.dma_start(out=w1_rows[head, a][:], in_=rows[:, 2 * a : 2 * a + 2])
 
-        def turn_w1(head, a, g, tag, bufs):
-            turn(("w", head, a, g), w1_rows[head, a][:, :, g * KIN : (g + 1) * KIN], tag, bufs)
+        def turn_w1(head, a, g, tag):
+            turn(("w", head, a, g), every_second_word(w1_rows[head, a][:, :, g * KIN : (g + 1) * KIN]), bank_of(tag))
 
         def unload_w1(copy, head, a, g):
             if g == H:
@@ -99,7 +106,7 @@ def tile_rssmcell_pb_t_kernel(
                      w1_grouped[head, a][:, 0 : (1 + head) * HALF])
 
         def warm_up(copies):
-            unread = psum.tile([P, copies, P], F32, name="unread", tag="acc", bufs=ACCS)
+            unread = psum.tile([P, copies, P], F32, name="unread", tag="acc", bufs=BANKS)
             nc.tensor.matmul(
                 out=unread[:], lhsT=ones[:], rhs=ones[:].unsqueeze(1).to_broadcast([P, copies, P]), start=True, stop=True)
 
@@ -118,8 +125,21 @@ def tile_rssmcell_pb_t_kernel(
             copy(out=h_wide[i][:, j0:j1].rearrange("p j k -> p (j k)"),
                  in_=h_raw[i][:, j0:j1].rearrange("p j k -> p (j k)").bitcast(FP8))
 
-        def turn_c(i, g, a, tag="turned", bufs=TURNED):
-            turn((i, g, a), (h_wide, emb)[g][i][:, 2 * a : 2 * a + 2], tag, bufs)
+        def widen_sorted(i, j0=0, j1=J):
+            if j0 == 0:
+                h_wide[i] = work.tile([P, 2, J * P, 2], BF16, name="h_wide", tag="h_wide", bufs=5, align_bytes=64)
+                sorted_chunks.add(i)
+            nc.vector.tensor_scalar(
+                out=h_wide[i][:, :, j0 * P : j1 * P].rearrange("p u q e -> p q u e"),
+                in0=h_raw[i][:, j0:j1].rearrange("p j k -> p (j k)").bitcast(FP8),
+                scalar1=ones[:, 0:1], scalar2=None, op0=ALU.mult)
+
+        def turn_c(i, g, a, tag="turned"):
+            if g == H and i in sorted_chunks:
+                pairs = h_wide[i][:, :, 2 * a * P : (2 * a + 2) * P].rearrange("p u q e -> p u (q e)").bitcast(F32)
+                turn((i, g, a), lambda b, u: pairs[:, u, b * P : (b + 1) * P], bank_of(tag))
+            else:
+                turn((i, g, a), every_second_word((h_wide, emb)[g][i][:, 2 * a : 2 * a + 2]), bank_of(tag))
 
         def grouped_half(i, g, a):
             if a == 0:
@@ -143,7 +163,7 @@ def tile_rssmcell_pb_t_kernel(
 
 
         def first(i, head, t, n0=0, n1=CHUNK):
-            acc[i, head, t] = psum.tile([P, n1 - n0], F32, name="acc", tag="acc", bufs=ACCS)
+            acc[i, head, t] = psum.tile([P, n1 - n0], F32, name="acc", tag="acc", bufs=BANKS)
             a, cols = t // 2, slice(t % 2 * P, (t % 2 + 1) * P)
             for g in range(1 + head):
                 nc.tensor.matmul_mx(
@@ -170,8 +190,10 @@ def tile_rssmcell_pb_t_kernel(
                 first(i, head, t, n0, n1)
                 (relu_on_vector if t in on_vector else relu)(i, head, t, n0, n1)
 
-        def new_grouped(i, head):
-            a_grouped[i, head] = work.tile([P, CHUNK, PACK], BF16, name="a_grouped", tag="a_grouped_%d" % head, bufs=1, align_bytes=64)
+        def new_grouped(i, head, slot=None):
+            a_grouped[i, head] = work.tile(
+                [P, CHUNK, PACK], BF16, name="a_grouped", tag="a_grouped_%d" % (head if slot is None else slot), bufs=1,
+                align_bytes=64)
 
         def interleave(i, head, n0=0, n1=CHUNK):
             if (i, head) not in a_grouped:
@@ -198,8 +220,8 @@ def tile_rssmcell_pb_t_kernel(
             quantise(a_codes[i, head][:, n0:n1], a_scales[i, head][:, n0:n1], a_grouped[i, head][:, n0:n1])
 
 
-        def second(i, head, j0=0, j1=J, tag=None, bufs=1):
-            result[i, head, j0] = psum.tile([P, j1 - j0, 2, LAT], F32, name="result", tag=tag or "result_%d" % head, bufs=bufs)
+        def second(i, head, j0=0, j1=J, tag="turned"):
+            result[i, head, j0] = psum.tile([P, j1 - j0, 2, LAT], F32, name="result", tag=tag, bufs=BANKS)
             for j in range(j0, j1):
                 cols = slice(j * P, (j + 1) * P)
                 nc.tensor.matmul_mx(
@@ -237,11 +259,9 @@ def tile_rssmcell_pb_t_kernel(
             nc.vector.scalar_tensor_tensor(
                 out=w_of(heads, n0, n1), in0=soft_of(heads, n0, n1), scalar=EXACT_ABOVE, in1=w_of(heads, n0, n1),
                 op0=ALU.min, op1=ALU.max)
-            for head in HEADS[heads]:
-                store(head, STD, n0, n1)
 
-        def turn_w2(tag, bufs):
-            turn("w2", w2_rows[:], tag, bufs)
+        def turn_w2(tag):
+            turn("w2", every_second_word(w2_rows[:]), bank_of(tag))
             new_grouped("w2", POST)
             unload(nc.scalar.copy, "w2", a_grouped["w2", POST][:, 0:HALF])
 
@@ -249,8 +269,8 @@ def tile_rssmcell_pb_t_kernel(
             quantise(w2_codes[:].rearrange("p e m -> p (e m)"), w2_scales[:].rearrange("p e m -> p (e m)"),
                      a_grouped["w2", POST][:, 0:HALF])
 
-        def spread_bias2(tag, bufs):
-            spread = psum.tile([P, 2, 2, LAT], F32, name="spread", tag=tag, bufs=bufs)
+        def spread_bias2(tag):
+            spread = psum.tile([P, 2, 2, LAT], F32, name="spread", tag=tag, bufs=BANKS)
             for head in HEADS:
                 nc.tensor.matmul(
                     out=spread[:, head].rearrange("p h c -> p (h c)"),
@@ -287,21 +307,21 @@ def tile_rssmcell_pb_t_kernel(
                 load_embedding(i)
 
             warm_up(4)
-            warm_up(4)
-            widen(nc.vector.tensor_copy, 0, 0, 2)
-            widen(nc.scalar.copy, 0, 2, 4)
-            widen(nc.vector.tensor_copy, 1)
+            warm_up(2)
+            widen_sorted(0, 0, 2)
+            widen_sorted(0, 2, 4)
+            widen(nc.scalar.copy, 1)
             for head in HEADS:
                 nc.vector.tensor_copy(out=bias2_column[:, head : head + 1], in_=bias2_raw[head][:])
             for a in (0, 1):
                 turn_c(0, H, a)
                 scale_h(0, a)
-            spread_bias2("result_0", 1)
+            spread_bias2("acc")
             widen(nc.scalar.copy, 2)
-            widen(nc.scalar.copy, 3)
             for a in (0, 1):
-                turn_w1(PRIOR, a, H, "acc", ACCS)
+                turn_w1(PRIOR, a, H, "acc")
                 unload_w1(nc.scalar.copy, PRIOR, a, H)
+            widen(nc.scalar.copy, 3)
             widen(nc.scalar.copy, 4)
             warm_up(2)
             quantise_c(0, H)
@@ -314,19 +334,19 @@ def tile_rssmcell_pb_t_kernel(
                 scale_h(1, a)
             layer1(0, PRIOR, (0, 1))
             for a in (0, 1):
-                turn_c(0, E, a, "result_%d" % a, 1)
+                turn_c(0, E, a)
                 unload_e(nc.scalar.copy, 0, a)
             load_embedding(6)
             layer1(0, PRIOR, (2, 3))
             quantise_c(1, H)
             quantise_c(0, E)
-            widen(nc.vector.tensor_copy, 5)
+            widen_sorted(5)
             for g in (H, E):
-                turn_w1(POST, 0, g, "turned", TURNED)
+                turn_w1(POST, 0, g, "turned")
                 unload_w1(nc.scalar.copy, POST, 0, g)
             layer1(1, PRIOR, (0, 1))
             for g in (H, E):
-                turn_w1(POST, 1, g, "result_%d" % g, 1)
+                turn_w1(POST, 1, g, "turned")
                 unload_w1(nc.vector.tensor_copy, POST, 1, g)
             quantise_w1(POST, 0)
             layer1(1, PRIOR, (2, 3))
@@ -339,11 +359,11 @@ def tile_rssmcell_pb_t_kernel(
                 scale_h(2, a)
             layer1(0, POST, (0, 1))
             for a in (0, 1):
-                turn_c(1, E, a, "result_%d" % a, 1)
+                turn_c(1, E, a)
                 unload_e(nc.scalar.copy, 1, a)
             load_embedding(7)
             layer1(0, POST, (2,))
-            turn_w2("acc", ACCS)
+            turn_w2("acc")
             layer1(0, POST, (3,))
             widen(nc.scalar.copy, 7)
             interleave(0, PRIOR, 384, CHUNK)
@@ -356,16 +376,15 @@ def tile_rssmcell_pb_t_kernel(
             for a in (0, 1):
                 turn_c(3, H, a)
 
-            for i in range(1, CHUNKS - 2):
+            for i in range(1, CHUNKS - 1 - LEAD):
+                ahead = i + LEAD
                 interleave_on_gpsimd(i - 1, POST)
                 for a in (0, 1):
-                    scale_h(i + 2, a)
-                layer1(i + 1, PRIOR)
-                if i == 1:
-                    second(0, PRIOR, tag="result_1")
-                    add_bias(0, PRIOR)
-                second(i, PRIOR)
-                add_bias(i, PRIOR)
+                    scale_h(ahead + 1, a)
+                layer1(ahead, PRIOR)
+                for done in range(0 if i == 1 else i, i + 1):
+                    second(done, PRIOR)
+                    add_bias(done, PRIOR)
                 if i >= 2:
                     second(i - 2, POST)
                     add_bias(i - 2, POST)
@@ -373,35 +392,35 @@ def tile_rssmcell_pb_t_kernel(
                     first(i, POST, t)
                 if i >= 3:
                     exp(BOTH, (i - 3) * J, (i - 2) * J)
-                interleave_on_scalar(i + 1, PRIOR, CHUNK - 64)
+                interleave_on_scalar(ahead, PRIOR, CHUNK - 64)
                 for a in (0, 1):
                     turn_c(i + 1, E, a)
                     unload_e(nc.scalar.copy, i + 1, a)
-                quantise_c(i + 2, H)
-                interleave(i + 1, PRIOR, 0, CHUNK - 64)
+                quantise_c(ahead + 1, H)
+                interleave(ahead, PRIOR, 0, CHUNK - 64)
                 for t in (2, 3):
                     first(i, POST, t)
                 for t in range(PACK):
                     relu(i, POST, t)
                 quantise_c(i + 1, E)
                 quantise_a(i - 1, POST)
-                quantise_a(i + 1, PRIOR)
-                if i + 3 < CHUNKS:
+                quantise_a(ahead, PRIOR)
+                if ahead + 2 < CHUNKS:
                     for a in (0, 1):
-                        turn_c(i + 3, H, a)
+                        turn_c(ahead + 2, H, a)
 
             last = CHUNKS - 1
             for a in (0, 1):
                 turn_c(last, E, a)
-                unload_e(nc.scalar.copy, last, a)
+                unload_e((nc.vector.tensor_copy, nc.scalar.copy)[a], last, a)
+            layer1(last, PRIOR, on_vector=())
             interleave(last - 2, POST)
-            layer1(last, PRIOR)
-            second(last - 1, PRIOR)
-            add_bias(last - 1, PRIOR)
             quantise_c(last, E)
+            second(last - 1, PRIOR)
+            add_bias(last - 1, PRIOR, (STD,))
             quantise_a(last - 2, POST)
             second(last - 3, POST)
-            add_bias(last - 3, POST)
+            add_bias(last - 3, POST, (STD,))
             interleave(last, PRIOR)
             layer1(last - 1, POST)
             second(last - 2, POST)
@@ -412,21 +431,27 @@ def tile_rssmcell_pb_t_kernel(
             second(last, PRIOR)
             add_bias(last, PRIOR, (STD,))
             quantise_a(last - 1, POST)
-            add_bias(last - 2, POST, (MEAN,))
-            interleave(last, POST, 0, CHUNK - 160)
-            interleave_on_scalar(last, POST, CHUNK - 160)
-            second(last - 1, POST, tag="turned", bufs=TURNED)
+            new_grouped(last, POST, PRIOR)
+            interleave(last, POST, 0, CHUNK - 192)
+            interleave_on_scalar(last, POST, CHUNK - 192)
+            second(last - 1, POST, tag="acc")
             add_bias(last - 1, POST, (STD,))
             quantise_a(last, POST)
+            add_bias(last - 1, PRIOR, (MEAN,))
+            add_bias(last - 3, POST, (MEAN,))
+            add_bias(last - 2, POST, (MEAN,))
             add_bias(last, PRIOR, (MEAN,))
-            add_bias(last - 1, POST, (MEAN,))
             exp(BOTH, (last - 4) * J, (last - 1) * J)
             exp(ONLY[PRIOR], (last - 1) * J, CHUNKS * J)
             exp(ONLY[POST], (last - 1) * J, last * J)
-            second(last, POST, tag="acc", bufs=ACCS)
+            second(last, POST, tag="acc")
             add_bias(last, POST, (STD,))
             exp(ONLY[POST], last * J, CHUNKS * J)
+            add_bias(last - 1, POST, (MEAN,))
             add_bias(last, POST, (MEAN,))
-            for n0, n1 in ((0, 2), (2, 8), (8, 16), (16, 24), (24, 30), (30, 32)):
-                log(BOTH, n0, n1)
-                std(BOTH, n0, n1)
+            for i in range(CHUNKS):
+                for n0 in range(i * J, (i + 1) * J, 2):
+                    log(BOTH, n0, n0 + 2)
+                    std(BOTH, n0, n0 + 2)
+                for head in HEADS:
+                    store(head, STD, i * J, (i + 1) * J)

@@ -48,8 +48,7 @@ def tile_rssmcell_pb_t_kernel(
         ones = keep.tile([P, P], F32, name="ones", tag="ones")
         ident = keep.tile([P, P], F32, name="ident", tag="ident")
         scale = keep.tile([P, PACK], F32, name="scale", tag="scale")
-        bias1_raw = [keep.tile([P, PACK], BF16, name="bias1_raw_%d" % e, tag="bias1_raw_%d" % e) for e in HEADS]
-        bias1 = [keep.tile([P, PACK], F32, name="bias1_%d" % e, tag="bias1_%d" % e) for e in HEADS]
+        bias1 = [keep.tile([P, PACK], BF16, name="bias1_%d" % e, tag="bias1_%d" % e) for e in HEADS]
         bias2 = keep.tile([P, 2, 2, LAT], F32, name="bias2", tag="bias2")
         exp_tenth = keep.tile([P, 1], F32, name="exp_tenth", tag="exp_tenth")
         w1_rows, w1_codes, w1_scales = {}, {}, {}
@@ -233,14 +232,14 @@ def tile_rssmcell_pb_t_kernel(
             dst = ((prior_mean, prior_std), (post_mean, post_std))[head][half]
             nc.sync.dma_start(out=dst.rearrange("(p n) d -> p n d", p=P)[:, n0:n1], in_=value[:, head, half, n0:n1])
 
-        def add_bias(i, head, halves=(MEAN, STD), j0=0, j1=J):
+        def add_bias(i, head, halves=(MEAN, STD), j0=0, j1=J, stored=True):
             part = slice(halves[0], halves[-1] + 1)
             nc.vector.tensor_tensor(
                 out=value[:, head, part, i * J + j0 : i * J + j1].rearrange("p h j c -> p j h c"),
                 in0=result[i, head, j0][:, :, part],
                 in1=bias2[:, head, part].unsqueeze(1).to_broadcast([P, j1 - j0, len(halves), LAT]),
                 op=ALU.add)
-            if MEAN in halves:
+            if MEAN in halves and stored:
                 store(head, MEAN, i * J + j0, i * J + j1)
 
         def w_of(heads, n0, n1):
@@ -292,8 +291,8 @@ def tile_rssmcell_pb_t_kernel(
             load_w1(PRIOR, 1)
             load_h(3)
             load_h(4)
-            nc.sync.dma_start(out=bias1_raw[PRIOR][:], in_=bp1.rearrange("(m t) -> m t", t=PACK))
-            nc.sync.dma_start(out=bias1_raw[POST][:], in_=bq1.rearrange("(m t) -> m t", t=PACK))
+            nc.sync.dma_start(out=bias1[PRIOR][:], in_=bp1.rearrange("(m t) -> m t", t=PACK))
+            nc.sync.dma_start(out=bias1[POST][:], in_=bq1.rearrange("(m t) -> m t", t=PACK))
             load_embedding(0)
             load_w1(POST, 0)
             load_h(5)
@@ -327,8 +326,6 @@ def tile_rssmcell_pb_t_kernel(
             quantise_c(0, H)
             for a in (0, 1):
                 quantise_w1(PRIOR, a)
-            for head in HEADS:
-                nc.vector.tensor_copy(out=bias1[head][:], in_=bias1_raw[head][:])
             for a in (0, 1):
                 turn_c(1, H, a)
                 scale_h(1, a)
@@ -378,6 +375,7 @@ def tile_rssmcell_pb_t_kernel(
 
             for i in range(1, CHUNKS - 1 - LEAD):
                 ahead = i + LEAD
+                share = 64 if i >= 3 else 64
                 interleave_on_gpsimd(i - 1, POST)
                 for a in (0, 1):
                     scale_h(ahead + 1, a)
@@ -392,12 +390,12 @@ def tile_rssmcell_pb_t_kernel(
                     first(i, POST, t)
                 if i >= 3:
                     exp(BOTH, (i - 3) * J, (i - 2) * J)
-                interleave_on_scalar(ahead, PRIOR, CHUNK - 64)
+                interleave_on_scalar(ahead, PRIOR, CHUNK - share)
                 for a in (0, 1):
                     turn_c(i + 1, E, a)
                     unload_e(nc.scalar.copy, i + 1, a)
                 quantise_c(ahead + 1, H)
-                interleave(ahead, PRIOR, 0, CHUNK - 64)
+                interleave(ahead, PRIOR, 0, CHUNK - share)
                 for t in (2, 3):
                     first(i, POST, t)
                 for t in range(PACK):
@@ -432,26 +430,29 @@ def tile_rssmcell_pb_t_kernel(
             add_bias(last, PRIOR, (STD,))
             quantise_a(last - 1, POST)
             new_grouped(last, POST, PRIOR)
-            interleave(last, POST, 0, CHUNK - 192)
-            interleave_on_scalar(last, POST, CHUNK - 192)
+            interleave(last, POST, 0, CHUNK - 128)
+            interleave_on_scalar(last, POST, CHUNK - 128)
             second(last - 1, POST, tag="acc")
             add_bias(last - 1, POST, (STD,))
             quantise_a(last, POST)
-            add_bias(last - 1, PRIOR, (MEAN,))
-            add_bias(last - 3, POST, (MEAN,))
-            add_bias(last - 2, POST, (MEAN,))
-            add_bias(last, PRIOR, (MEAN,))
+            for i in (last - 1, last):
+                add_bias(i, PRIOR, (MEAN,), stored=False)
+            store(PRIOR, MEAN, (last - 1) * J, CHUNKS * J)
+            for i in (last - 3, last - 2):
+                add_bias(i, POST, (MEAN,), stored=False)
+            store(POST, MEAN, (last - 3) * J, (last - 1) * J)
             exp(BOTH, (last - 4) * J, (last - 1) * J)
             exp(ONLY[PRIOR], (last - 1) * J, CHUNKS * J)
             exp(ONLY[POST], (last - 1) * J, last * J)
             second(last, POST, tag="acc")
             add_bias(last, POST, (STD,))
             exp(ONLY[POST], last * J, CHUNKS * J)
-            add_bias(last - 1, POST, (MEAN,))
-            add_bias(last, POST, (MEAN,))
-            for i in range(CHUNKS):
-                for n0 in range(i * J, (i + 1) * J, 2):
-                    log(BOTH, n0, n0 + 2)
-                    std(BOTH, n0, n0 + 2)
+            for i in (last - 1, last):
+                add_bias(i, POST, (MEAN,), stored=False)
+            store(POST, MEAN, (last - 1) * J, CHUNKS * J)
+            for pair in range(0, CHUNKS, 2):
                 for head in HEADS:
-                    store(head, STD, i * J, (i + 1) * J)
+                    for i in (pair, pair + 1):
+                        log(ONLY[head], i * J, (i + 1) * J)
+                        std(ONLY[head], i * J, (i + 1) * J)
+                    store(head, STD, pair * J, (pair + 2) * J)

@@ -25,6 +25,7 @@ ALU = mybir.AluOpType
 
 BANKS = 4
 LEAD = 1
+LATE = 4
 EXACT_ABOVE = 40.0
 PRIOR, POST = 0, 1
 HEADS = (PRIOR, POST)
@@ -48,6 +49,7 @@ def tile_rssmcell_pb_t_kernel(
         ones = keep.tile([P, P], F32, name="ones", tag="ones")
         ident = keep.tile([P, P], F32, name="ident", tag="ident")
         scale = keep.tile([P, PACK], F32, name="scale", tag="scale")
+        scale_wide = keep.tile([P, HALF, PACK], F32, name="scale_wide", tag="scale_wide")
         bias1 = [keep.tile([P, PACK], BF16, name="bias1_%d" % e, tag="bias1_%d" % e) for e in HEADS]
         bias2 = keep.tile([P, 2, 2, LAT], F32, name="bias2", tag="bias2")
         exp_tenth = keep.tile([P, 1], F32, name="exp_tenth", tag="exp_tenth")
@@ -149,7 +151,7 @@ def tile_rssmcell_pb_t_kernel(
             nc.vector.tensor_tensor(
                 out=grouped_half(i, H, a).rearrange("p n (u e) -> p n u e", u=2),
                 in0=turned[i, H, a][:].bitcast(BF16).rearrange("p u (n e) -> p n u e", e=2),
-                in1=scale[:].rearrange("p (u e) -> p u e", u=2).unsqueeze(1).to_broadcast([P, HALF, 2, 2]),
+                in1=scale_wide[:].rearrange("p n (u e) -> p n u e", u=2),
                 op=ALU.mult)
 
         def unload_e(copy, i, a):
@@ -214,8 +216,8 @@ def tile_rssmcell_pb_t_kernel(
 
         def quantise_a(i, head, n0=0, n1=CHUNK):
             if n0 == 0:
-                a_codes[i, head] = work.tile([P, CHUNK], U32, name="a_codes", tag="a_codes", bufs=4, align_bytes=64)
-                a_scales[i, head] = work.tile([P, CHUNK], U8, name="a_scales", tag="a_scales", bufs=4, align_bytes=64)
+                a_codes[i, head] = work.tile([P, CHUNK], U32, name="a_codes", tag="a_codes", bufs=10, align_bytes=64)
+                a_scales[i, head] = work.tile([P, CHUNK], U8, name="a_scales", tag="a_scales", bufs=10, align_bytes=64)
             quantise(a_codes[i, head][:, n0:n1], a_scales[i, head][:, n0:n1], a_grouped[i, head][:, n0:n1])
 
 
@@ -227,6 +229,23 @@ def tile_rssmcell_pb_t_kernel(
                     out=result[i, head, j0][:, j - j0, :, :].rearrange("p h c -> p (h c)"),
                     lhsT=a_codes[i, head][:, cols].bitcast(FP8X4), lhsT_scale=a_scales[i, head][:, cols],
                     rhs=w2_codes[:, head, :].bitcast(FP8X4), rhs_scale=w2_scales[:, head, :], start=True, stop=True)
+
+        def second_half(half, units, tag):
+            head, i0, i1 = units
+            bank = psum.tile([P, (i1 - i0) * J, LAT], F32, name="result", tag=tag, bufs=BANKS)
+            out = slice(half * LAT, (half + 1) * LAT)
+            for i in range(i0, i1):
+                for j in range(J):
+                    cols = slice(j * P, (j + 1) * P)
+                    nc.tensor.matmul_mx(
+                        out=bank[:, (i - i0) * J + j],
+                        lhsT=a_codes[i, head][:, cols].bitcast(FP8X4), lhsT_scale=a_scales[i, head][:, cols],
+                        rhs=w2_codes[:, head, out].bitcast(FP8X4), rhs_scale=w2_scales[:, head, out], start=True, stop=True)
+            nc.vector.tensor_tensor(
+                out=value[:, head, half, i0 * J : i1 * J], in0=bank[:],
+                in1=bias2[:, head, half].unsqueeze(1).to_broadcast([P, (i1 - i0) * J, LAT]), op=ALU.add)
+            if half == MEAN:
+                store(head, MEAN, i0 * J, i1 * J)
 
         def store(head, half, n0, n1):
             dst = ((prior_mean, prior_std), (post_mean, post_std))[head][half]
@@ -309,6 +328,7 @@ def tile_rssmcell_pb_t_kernel(
             warm_up(2)
             widen_sorted(0, 0, 2)
             widen_sorted(0, 2, 4)
+            nc.scalar.copy(out=scale_wide[:], in_=scale[:].unsqueeze(1).to_broadcast([P, HALF, PACK]))
             widen(nc.scalar.copy, 1)
             for head in HEADS:
                 nc.vector.tensor_copy(out=bias2_column[:, head : head + 1], in_=bias2_raw[head][:])
@@ -321,7 +341,6 @@ def tile_rssmcell_pb_t_kernel(
                 turn_w1(PRIOR, a, H, "acc")
                 unload_w1(nc.scalar.copy, PRIOR, a, H)
             widen(nc.scalar.copy, 3)
-            widen(nc.scalar.copy, 4)
             warm_up(2)
             quantise_c(0, H)
             for a in (0, 1):
@@ -336,8 +355,8 @@ def tile_rssmcell_pb_t_kernel(
             load_embedding(6)
             layer1(0, PRIOR, (2, 3))
             quantise_c(1, H)
+            widen_sorted(4)
             quantise_c(0, E)
-            widen_sorted(5)
             for g in (H, E):
                 turn_w1(POST, 0, g, "turned")
                 unload_w1(nc.scalar.copy, POST, 0, g)
@@ -347,11 +366,11 @@ def tile_rssmcell_pb_t_kernel(
                 unload_w1(nc.vector.tensor_copy, POST, 1, g)
             quantise_w1(POST, 0)
             layer1(1, PRIOR, (2, 3))
-            widen(nc.scalar.copy, 6)
+            widen(nc.scalar.copy, 5)
             for a in (0, 1):
                 turn_c(2, H, a)
             quantise_w1(POST, 1)
-            interleave_on_gpsimd(0, PRIOR, 384)
+            interleave_on_gpsimd(0, PRIOR, 448)
             for a in (0, 1):
                 scale_h(2, a)
             layer1(0, POST, (0, 1))
@@ -362,8 +381,7 @@ def tile_rssmcell_pb_t_kernel(
             layer1(0, POST, (2,))
             turn_w2("acc")
             layer1(0, POST, (3,))
-            widen(nc.scalar.copy, 7)
-            interleave(0, PRIOR, 384, CHUNK)
+            interleave(0, PRIOR, 448, CHUNK)
             quantise_c(2, H)
             quantise_a(0, PRIOR)
             quantise_c(1, E)
@@ -375,22 +393,29 @@ def tile_rssmcell_pb_t_kernel(
 
             for i in range(1, CHUNKS - 1 - LEAD):
                 ahead = i + LEAD
-                share = 64 if i >= 3 else 64
+                share = 32 if i >= 3 else 0
                 interleave_on_gpsimd(i - 1, POST)
                 for a in (0, 1):
                     scale_h(ahead + 1, a)
                 layer1(ahead, PRIOR)
-                for done in range(0 if i == 1 else i, i + 1):
-                    second(done, PRIOR)
-                    add_bias(done, PRIOR)
-                if i >= 2:
-                    second(i - 2, POST)
-                    add_bias(i - 2, POST)
+                if i >= LATE:
+                    second_half(STD, (PRIOR, i, i + 1), "turned")
+                    second_half(STD, (POST, i - 2, i - 1), "turned")
+                else:
+                    for done in range(0 if i == 1 else i, i + 1):
+                        second(done, PRIOR)
+                        add_bias(done, PRIOR)
+                    if i >= 2:
+                        second(i - 2, POST)
+                        add_bias(i - 2, POST)
                 for t in (0, 1):
                     first(i, POST, t)
                 if i >= 3:
                     exp(BOTH, (i - 3) * J, (i - 2) * J)
-                interleave_on_scalar(ahead, PRIOR, CHUNK - share)
+                else:
+                    widen(nc.scalar.copy, i + 5)
+                if share:
+                    interleave_on_scalar(ahead, PRIOR, CHUNK - share)
                 for a in (0, 1):
                     turn_c(i + 1, E, a)
                     unload_e(nc.scalar.copy, i + 1, a)
@@ -450,6 +475,8 @@ def tile_rssmcell_pb_t_kernel(
             for i in (last - 1, last):
                 add_bias(i, POST, (MEAN,), stored=False)
             store(POST, MEAN, (last - 1) * J, CHUNKS * J)
+            second_half(MEAN, (PRIOR, LATE, last - 1), "acc")
+            second_half(MEAN, (POST, LATE - 2, last - 3), "acc")
             for pair in range(0, CHUNKS, 2):
                 for head in HEADS:
                     for i in (pair, pair + 1):

@@ -49,7 +49,6 @@ def tile_rssmcell_pb_t_kernel(
         ones = keep.tile([P, P], F32, name="ones", tag="ones")
         ident = keep.tile([P, P], F32, name="ident", tag="ident")
         scale = keep.tile([P, PACK], F32, name="scale", tag="scale")
-        scale_wide = keep.tile([P, HALF, PACK], F32, name="scale_wide", tag="scale_wide")
         bias1 = [keep.tile([P, PACK], BF16, name="bias1_%d" % e, tag="bias1_%d" % e) for e in HEADS]
         bias2 = keep.tile([P, 2, 2, LAT], F32, name="bias2", tag="bias2")
         exp_tenth = keep.tile([P, 1], F32, name="exp_tenth", tag="exp_tenth")
@@ -151,7 +150,7 @@ def tile_rssmcell_pb_t_kernel(
             nc.vector.tensor_tensor(
                 out=grouped_half(i, H, a).rearrange("p n (u e) -> p n u e", u=2),
                 in0=turned[i, H, a][:].bitcast(BF16).rearrange("p u (n e) -> p n u e", e=2),
-                in1=scale_wide[:].rearrange("p n (u e) -> p n u e", u=2),
+                in1=scale[:].rearrange("p (u e) -> p u e", u=2).unsqueeze(1).to_broadcast([P, HALF, 2, 2]),
                 op=ALU.mult)
 
         def unload_e(copy, i, a):
@@ -208,10 +207,11 @@ def tile_rssmcell_pb_t_kernel(
                 new_grouped(i, head)
             nc.scalar.copy(out=a_grouped[i, head][:, n0:CHUNK], in_=planes[i, head][:, :, n0:CHUNK].rearrange("p t n -> p n t"))
 
-        def interleave_on_gpsimd(i, head, n1=CHUNK):
-            new_grouped(i, head)
+        def interleave_on_gpsimd(i, head, n1=CHUNK, n0=0):
+            if (i, head) not in a_grouped:
+                new_grouped(i, head)
             nc.gpsimd.tensor_scalar(
-                out=a_grouped[i, head][:, 0:n1], in0=planes[i, head][:, :, 0:n1].rearrange("p t n -> p n t"),
+                out=a_grouped[i, head][:, n0:n1], in0=planes[i, head][:, :, n0:n1].rearrange("p t n -> p n t"),
                 scalar1=1.0, scalar2=0.0, op0=ALU.mult, op1=ALU.add)
 
         def quantise_a(i, head, n0=0, n1=CHUNK):
@@ -230,19 +230,20 @@ def tile_rssmcell_pb_t_kernel(
                     lhsT=a_codes[i, head][:, cols].bitcast(FP8X4), lhsT_scale=a_scales[i, head][:, cols],
                     rhs=w2_codes[:, head, :].bitcast(FP8X4), rhs_scale=w2_scales[:, head, :], start=True, stop=True)
 
-        def second_half(half, units, tag):
-            head, i0, i1 = units
-            bank = psum.tile([P, (i1 - i0) * J, LAT], F32, name="result", tag=tag, bufs=BANKS)
+        def second_half(half, head, i0, i1, tag):
+            result[half, head, i0, i1] = psum.tile([P, (i1 - i0) * J, LAT], F32, name="result", tag=tag, bufs=BANKS)
             out = slice(half * LAT, (half + 1) * LAT)
             for i in range(i0, i1):
                 for j in range(J):
                     cols = slice(j * P, (j + 1) * P)
                     nc.tensor.matmul_mx(
-                        out=bank[:, (i - i0) * J + j],
+                        out=result[half, head, i0, i1][:, (i - i0) * J + j],
                         lhsT=a_codes[i, head][:, cols].bitcast(FP8X4), lhsT_scale=a_scales[i, head][:, cols],
                         rhs=w2_codes[:, head, out].bitcast(FP8X4), rhs_scale=w2_scales[:, head, out], start=True, stop=True)
+
+        def add_bias_half(half, head, i0, i1):
             nc.vector.tensor_tensor(
-                out=value[:, head, half, i0 * J : i1 * J], in0=bank[:],
+                out=value[:, head, half, i0 * J : i1 * J], in0=result[half, head, i0, i1][:],
                 in1=bias2[:, head, half].unsqueeze(1).to_broadcast([P, (i1 - i0) * J, LAT]), op=ALU.add)
             if half == MEAN:
                 store(head, MEAN, i0 * J, i1 * J)
@@ -328,7 +329,6 @@ def tile_rssmcell_pb_t_kernel(
             warm_up(2)
             widen_sorted(0, 0, 2)
             widen_sorted(0, 2, 4)
-            nc.scalar.copy(out=scale_wide[:], in_=scale[:].unsqueeze(1).to_broadcast([P, HALF, PACK]))
             widen(nc.scalar.copy, 1)
             for head in HEADS:
                 nc.vector.tensor_copy(out=bias2_column[:, head : head + 1], in_=bias2_raw[head][:])
@@ -393,14 +393,15 @@ def tile_rssmcell_pb_t_kernel(
 
             for i in range(1, CHUNKS - 1 - LEAD):
                 ahead = i + LEAD
-                share = 32 if i >= 3 else 0
+                share = 64 if i >= 3 else 0
                 interleave_on_gpsimd(i - 1, POST)
                 for a in (0, 1):
                     scale_h(ahead + 1, a)
                 layer1(ahead, PRIOR)
                 if i >= LATE:
-                    second_half(STD, (PRIOR, i, i + 1), "turned")
-                    second_half(STD, (POST, i - 2, i - 1), "turned")
+                    for head, done in ((PRIOR, i), (POST, i - 2)):
+                        second_half(STD, head, done, done + 1, "turned")
+                        add_bias_half(STD, head, done, done + 1)
                 else:
                     for done in range(0 if i == 1 else i, i + 1):
                         second(done, PRIOR)
@@ -414,13 +415,16 @@ def tile_rssmcell_pb_t_kernel(
                     exp(BOTH, (i - 3) * J, (i - 2) * J)
                 else:
                     widen(nc.scalar.copy, i + 5)
+                extra = 128 if i < LATE else 0
+                if extra:
+                    interleave_on_gpsimd(ahead, PRIOR, CHUNK - share, CHUNK - share - extra)
                 if share:
                     interleave_on_scalar(ahead, PRIOR, CHUNK - share)
                 for a in (0, 1):
                     turn_c(i + 1, E, a)
                     unload_e(nc.scalar.copy, i + 1, a)
                 quantise_c(ahead + 1, H)
-                interleave(ahead, PRIOR, 0, CHUNK - share)
+                interleave(ahead, PRIOR, 0, CHUNK - share - extra)
                 for t in (2, 3):
                     first(i, POST, t)
                 for t in range(PACK):
@@ -455,28 +459,30 @@ def tile_rssmcell_pb_t_kernel(
             add_bias(last, PRIOR, (STD,))
             quantise_a(last - 1, POST)
             new_grouped(last, POST, PRIOR)
-            interleave(last, POST, 0, CHUNK - 128)
-            interleave_on_scalar(last, POST, CHUNK - 128)
+            interleave(last, POST, 0, CHUNK - share)
+            interleave_on_scalar(last, POST, CHUNK - share)
+            second_half(MEAN, PRIOR, LATE, last - 1, "acc")
             second(last - 1, POST, tag="acc")
+            second_half(MEAN, POST, LATE - 2, last - 3, "acc")
             add_bias(last - 1, POST, (STD,))
             quantise_a(last, POST)
             for i in (last - 1, last):
                 add_bias(i, PRIOR, (MEAN,), stored=False)
             store(PRIOR, MEAN, (last - 1) * J, CHUNKS * J)
-            for i in (last - 3, last - 2):
-                add_bias(i, POST, (MEAN,), stored=False)
-            store(POST, MEAN, (last - 3) * J, (last - 1) * J)
             exp(BOTH, (last - 4) * J, (last - 1) * J)
             exp(ONLY[PRIOR], (last - 1) * J, CHUNKS * J)
             exp(ONLY[POST], (last - 1) * J, last * J)
             second(last, POST, tag="acc")
             add_bias(last, POST, (STD,))
             exp(ONLY[POST], last * J, CHUNKS * J)
+            for i in (last - 3, last - 2):
+                add_bias(i, POST, (MEAN,), stored=False)
+            store(POST, MEAN, (last - 3) * J, (last - 1) * J)
             for i in (last - 1, last):
                 add_bias(i, POST, (MEAN,), stored=False)
             store(POST, MEAN, (last - 1) * J, CHUNKS * J)
-            second_half(MEAN, (PRIOR, LATE, last - 1), "acc")
-            second_half(MEAN, (POST, LATE - 2, last - 3), "acc")
+            add_bias_half(MEAN, PRIOR, LATE, last - 1)
+            add_bias_half(MEAN, POST, LATE - 2, last - 3)
             for pair in range(0, CHUNKS, 2):
                 for head in HEADS:
                     for i in (pair, pair + 1):

@@ -1,4 +1,3 @@
-import math
 from contextlib import ExitStack
 
 import concourse.mybir as mybir
@@ -24,8 +23,14 @@ ACT = mybir.ActivationFunctionType
 ALU = mybir.AluOpType
 
 BANKS = 4
-LEAD = 1
-LATE = 4
+WIDE_BUFS = 5
+EMB_BUFS = 6
+A_BUFS = 10
+SCALAR_SHARE = 64
+LAST_SHARE = 128
+FIRST_GPSIMD = 384
+LATE = CHUNKS - 4
+EXP_LAG = 3
 EXACT_ABOVE = 40.0
 PRIOR, POST = 0, 1
 HEADS = (PRIOR, POST)
@@ -71,12 +76,12 @@ def tile_rssmcell_pb_t_kernel(
 
         def turn(key, words, bank):
             turned[key] = bank
-            for a in (0, 1):
+            for b in (0, 1):
                 for u in (0, 1):
-                    nc.tensor.transpose(bank[:, u, a * P : (a + 1) * P], words(a, u), ident[:])
+                    nc.tensor.transpose(bank[:, u, b * P : (b + 1) * P], words(b, u), ident[:])
 
         def every_second_word(rows):
-            return lambda a, u: rows[:, a, :].bitcast(F32)[:, u : KIN // 2 : 2]
+            return lambda b, u: rows[:, b, :].bitcast(F32)[:, u : KIN // 2 : 2]
 
         def bank_of(tag):
             return psum.tile([P, 2, HALF], F32, name="turned", tag=tag, bufs=BANKS)
@@ -116,30 +121,29 @@ def tile_rssmcell_pb_t_kernel(
             nc.sync.dma_start(out=h_raw[i][:], in_=h_bytes.rearrange("(p c j) k -> c p j k", p=P, j=J)[i])
 
         def load_embedding(i):
-            emb[i] = work.tile([P, J, KIN], BF16, name="emb", tag="emb", bufs=6)
+            emb[i] = work.tile([P, J, KIN], BF16, name="emb", tag="emb", bufs=EMB_BUFS)
             nc.sync.dma_start(out=emb[i][:], in_=embedding.rearrange("(p c j) k -> c p j k", p=P, j=J)[i])
 
-        def widen(copy, i, j0=0, j1=J):
-            if j0 == 0:
-                h_wide[i] = work.tile([P, J, KIN], BF16, name="h_wide", tag="h_wide", bufs=5, align_bytes=64)
-            copy(out=h_wide[i][:, j0:j1].rearrange("p j k -> p (j k)"),
-                 in_=h_raw[i][:, j0:j1].rearrange("p j k -> p (j k)").bitcast(FP8))
+        def widen(i):
+            h_wide[i] = work.tile([P, J, KIN], BF16, name="h_wide", tag="h_wide", bufs=WIDE_BUFS, align_bytes=64)
+            nc.scalar.copy(out=h_wide[i][:].rearrange("p j k -> p (j k)"),
+                           in_=h_raw[i][:].rearrange("p j k -> p (j k)").bitcast(FP8))
 
         def widen_sorted(i, j0=0, j1=J):
             if j0 == 0:
-                h_wide[i] = work.tile([P, 2, J * P, 2], BF16, name="h_wide", tag="h_wide", bufs=5, align_bytes=64)
+                h_wide[i] = work.tile([P, 2, J * P, 2], BF16, name="h_wide", tag="h_wide", bufs=WIDE_BUFS, align_bytes=64)
                 sorted_chunks.add(i)
             nc.vector.tensor_scalar(
                 out=h_wide[i][:, :, j0 * P : j1 * P].rearrange("p u q e -> p q u e"),
                 in0=h_raw[i][:, j0:j1].rearrange("p j k -> p (j k)").bitcast(FP8),
                 scalar1=ones[:, 0:1], scalar2=None, op0=ALU.mult)
 
-        def turn_c(i, g, a, tag="turned"):
+        def turn_c(i, g, a):
             if g == H and i in sorted_chunks:
                 pairs = h_wide[i][:, :, 2 * a * P : (2 * a + 2) * P].rearrange("p u q e -> p u (q e)").bitcast(F32)
-                turn((i, g, a), lambda b, u: pairs[:, u, b * P : (b + 1) * P], bank_of(tag))
+                turn((i, g, a), lambda b, u: pairs[:, u, b * P : (b + 1) * P], bank_of("turned"))
             else:
-                turn((i, g, a), every_second_word((h_wide, emb)[g][i][:, 2 * a : 2 * a + 2]), bank_of(tag))
+                turn((i, g, a), every_second_word((h_wide, emb)[g][i][:, 2 * a : 2 * a + 2]), bank_of("turned"))
 
         def grouped_half(i, g, a):
             if a == 0:
@@ -162,71 +166,61 @@ def tile_rssmcell_pb_t_kernel(
             quantise(c_codes[i, g][:], c_scales[i, g][:], c_grouped[i, g][:])
 
 
-        def first(i, head, t, n0=0, n1=CHUNK):
-            acc[i, head, t] = psum.tile([P, n1 - n0], F32, name="acc", tag="acc", bufs=BANKS)
+        def first(i, head, t):
+            acc[i, head, t] = psum.tile([P, CHUNK], F32, name="acc", tag="acc", bufs=BANKS)
             a, cols = t // 2, slice(t % 2 * P, (t % 2 + 1) * P)
             for g in range(1 + head):
                 nc.tensor.matmul_mx(
                     out=acc[i, head, t][:],
                     lhsT=w1_codes[head, a][:, g, cols].bitcast(FP8X4), lhsT_scale=w1_scales[head, a][:, g, cols],
-                    rhs=c_codes[i, g][:, n0:n1].bitcast(FP8X4), rhs_scale=c_scales[i, g][:, n0:n1],
+                    rhs=c_codes[i, g][:].bitcast(FP8X4), rhs_scale=c_scales[i, g][:],
                     start=(g == 0), stop=(g == head))
 
-        def plane(i, head, t, n0, n1):
-            if t == 0 and n0 == 0:
+        def relu(i, head, t):
+            if t == 0:
                 planes[i, head] = work.tile([P, PACK, CHUNK], BF16, name="planes", tag="planes_%d" % head, bufs=2, align_bytes=64)
-            return planes[i, head][:, t, n0:n1]
-
-        def relu(i, head, t, n0=0, n1=CHUNK):
             nc.scalar.activation(
-                out=plane(i, head, t, n0, n1), in_=acc[i, head, t][:], func=ACT.Relu, bias=bias1[head][:, t : t + 1])
+                out=planes[i, head][:, t], in_=acc[i, head, t][:], func=ACT.Relu, bias=bias1[head][:, t : t + 1])
 
-        def relu_on_vector(i, head, t, n0=0, n1=CHUNK):
-            nc.vector.tensor_scalar(out=plane(i, head, t, n0, n1), in0=acc[i, head, t][:], scalar1=bias1[head][:, t : t + 1],
-                                    scalar2=0.0, op0=ALU.add, op1=ALU.max)
-
-        def layer1(i, head, tiles=range(PACK), n0=0, n1=CHUNK, on_vector=()):
+        def layer1(i, head, tiles=range(PACK)):
             for t in tiles:
-                first(i, head, t, n0, n1)
-                (relu_on_vector if t in on_vector else relu)(i, head, t, n0, n1)
+                first(i, head, t)
+                relu(i, head, t)
 
-        def new_grouped(i, head, slot=None):
+        def new_grouped(i, head, buffer):
             a_grouped[i, head] = work.tile(
-                [P, CHUNK, PACK], BF16, name="a_grouped", tag="a_grouped_%d" % (head if slot is None else slot), bufs=1,
-                align_bytes=64)
+                [P, CHUNK, PACK], BF16, name="a_grouped", tag="a_grouped_%d" % buffer, bufs=1, align_bytes=64)
 
         def interleave(i, head, n0=0, n1=CHUNK):
             if (i, head) not in a_grouped:
-                new_grouped(i, head)
+                new_grouped(i, head, head)
             nc.vector.tensor_copy(
                 out=a_grouped[i, head][:, n0:n1].rearrange("p (c i) t -> p c t i", i=4),
                 in_=planes[i, head][:, :, n0:n1].rearrange("p t (c i) -> p c t i", i=4))
 
         def interleave_on_scalar(i, head, n0):
             if (i, head) not in a_grouped:
-                new_grouped(i, head)
+                new_grouped(i, head, head)
             nc.scalar.copy(out=a_grouped[i, head][:, n0:CHUNK], in_=planes[i, head][:, :, n0:CHUNK].rearrange("p t n -> p n t"))
 
-        def interleave_on_gpsimd(i, head, n1=CHUNK, n0=0):
-            if (i, head) not in a_grouped:
-                new_grouped(i, head)
+        def interleave_on_gpsimd(i, head, n1=CHUNK):
+            new_grouped(i, head, head)
             nc.gpsimd.tensor_scalar(
-                out=a_grouped[i, head][:, n0:n1], in0=planes[i, head][:, :, n0:n1].rearrange("p t n -> p n t"),
+                out=a_grouped[i, head][:, 0:n1], in0=planes[i, head][:, :, 0:n1].rearrange("p t n -> p n t"),
                 scalar1=1.0, scalar2=0.0, op0=ALU.mult, op1=ALU.add)
 
-        def quantise_a(i, head, n0=0, n1=CHUNK):
-            if n0 == 0:
-                a_codes[i, head] = work.tile([P, CHUNK], U32, name="a_codes", tag="a_codes", bufs=10, align_bytes=64)
-                a_scales[i, head] = work.tile([P, CHUNK], U8, name="a_scales", tag="a_scales", bufs=10, align_bytes=64)
-            quantise(a_codes[i, head][:, n0:n1], a_scales[i, head][:, n0:n1], a_grouped[i, head][:, n0:n1])
+        def quantise_a(i, head):
+            a_codes[i, head] = work.tile([P, CHUNK], U32, name="a_codes", tag="a_codes", bufs=A_BUFS, align_bytes=64)
+            a_scales[i, head] = work.tile([P, CHUNK], U8, name="a_scales", tag="a_scales", bufs=A_BUFS, align_bytes=64)
+            quantise(a_codes[i, head][:], a_scales[i, head][:], a_grouped[i, head][:])
 
 
-        def second(i, head, j0=0, j1=J, tag="turned"):
-            result[i, head, j0] = psum.tile([P, j1 - j0, 2, LAT], F32, name="result", tag=tag, bufs=BANKS)
-            for j in range(j0, j1):
+        def second(i, head, tag="turned"):
+            result[i, head] = psum.tile([P, J, 2, LAT], F32, name="result", tag=tag, bufs=BANKS)
+            for j in range(J):
                 cols = slice(j * P, (j + 1) * P)
                 nc.tensor.matmul_mx(
-                    out=result[i, head, j0][:, j - j0, :, :].rearrange("p h c -> p (h c)"),
+                    out=result[i, head][:, j, :, :].rearrange("p h c -> p (h c)"),
                     lhsT=a_codes[i, head][:, cols].bitcast(FP8X4), lhsT_scale=a_scales[i, head][:, cols],
                     rhs=w2_codes[:, head, :].bitcast(FP8X4), rhs_scale=w2_scales[:, head, :], start=True, stop=True)
 
@@ -245,51 +239,58 @@ def tile_rssmcell_pb_t_kernel(
             nc.vector.tensor_tensor(
                 out=value[:, head, half, i0 * J : i1 * J], in0=result[half, head, i0, i1][:],
                 in1=bias2[:, head, half].unsqueeze(1).to_broadcast([P, (i1 - i0) * J, LAT]), op=ALU.add)
-            if half == MEAN:
-                store(head, MEAN, i0 * J, i1 * J)
 
-        def store(head, half, n0, n1):
+        def store(head, half, i0, i1):
             dst = ((prior_mean, prior_std), (post_mean, post_std))[head][half]
-            nc.sync.dma_start(out=dst.rearrange("(p n) d -> p n d", p=P)[:, n0:n1], in_=value[:, head, half, n0:n1])
+            tokens = slice(i0 * J, i1 * J)
+            nc.sync.dma_start(out=dst.rearrange("(p n) d -> p n d", p=P)[:, tokens], in_=value[:, head, half, tokens])
 
-        def add_bias(i, head, halves=(MEAN, STD), j0=0, j1=J, stored=True):
+        def add_bias(i, head, halves):
             part = slice(halves[0], halves[-1] + 1)
             nc.vector.tensor_tensor(
-                out=value[:, head, part, i * J + j0 : i * J + j1].rearrange("p h j c -> p j h c"),
-                in0=result[i, head, j0][:, :, part],
-                in1=bias2[:, head, part].unsqueeze(1).to_broadcast([P, j1 - j0, len(halves), LAT]),
+                out=value[:, head, part, i * J : (i + 1) * J].rearrange("p h j c -> p j h c"),
+                in0=result[i, head][:, :, part],
+                in1=bias2[:, head, part].unsqueeze(1).to_broadcast([P, J, len(halves), LAT]),
                 op=ALU.add)
-            if MEAN in halves and stored:
-                store(head, MEAN, i * J + j0, i * J + j1)
 
-        def w_of(heads, n0, n1):
-            return value[:, heads, STD, n0:n1].rearrange("p e n c -> p e (n c)")
+        def layer2(i, head):
+            second(i, head)
+            add_bias(i, head, (MEAN, STD))
+            store(head, MEAN, i, i + 1)
 
-        def soft_of(heads, n0, n1):
-            return soft[:, heads, n0 * LAT : n1 * LAT]
+        def kept_means(head, i0):
+            for i in (i0, i0 + 1):
+                add_bias(i, head, (MEAN,))
+            store(head, MEAN, i0, i0 + 2)
 
-        def exp(heads, n0, n1):
-            nc.scalar.activation(out=soft_of(heads, n0, n1), in_=w_of(heads, n0, n1), func=ACT.Exp)
+        def w_of(heads, i0, i1):
+            return value[:, heads, STD, i0 * J : i1 * J].rearrange("p e n c -> p e (n c)")
 
-        def log(heads, n0, n1):
-            nc.scalar.activation(out=soft_of(heads, n0, n1), in_=soft_of(heads, n0, n1), func=ACT.Ln, bias=exp_tenth[:])
+        def soft_of(heads, i0, i1):
+            return soft[:, heads, i0 * J * LAT : i1 * J * LAT]
 
-        def std(heads, n0, n1):
+        def exp(heads, i0, i1):
+            nc.scalar.activation(out=soft_of(heads, i0, i1), in_=w_of(heads, i0, i1), func=ACT.Exp)
+
+        def log(heads, i0, i1):
+            nc.scalar.activation(out=soft_of(heads, i0, i1), in_=soft_of(heads, i0, i1), func=ACT.Ln, bias=exp_tenth[:])
+
+        def std(heads, i0, i1):
             nc.vector.scalar_tensor_tensor(
-                out=w_of(heads, n0, n1), in0=soft_of(heads, n0, n1), scalar=EXACT_ABOVE, in1=w_of(heads, n0, n1),
+                out=w_of(heads, i0, i1), in0=soft_of(heads, i0, i1), scalar=EXACT_ABOVE, in1=w_of(heads, i0, i1),
                 op0=ALU.min, op1=ALU.max)
 
-        def turn_w2(tag):
-            turn("w2", every_second_word(w2_rows[:]), bank_of(tag))
-            new_grouped("w2", POST)
+        def turn_w2():
+            turn("w2", every_second_word(w2_rows[:]), bank_of("acc"))
+            new_grouped("w2", POST, POST)
             unload(nc.scalar.copy, "w2", a_grouped["w2", POST][:, 0:HALF])
 
         def quantise_w2():
             quantise(w2_codes[:].rearrange("p e m -> p (e m)"), w2_scales[:].rearrange("p e m -> p (e m)"),
                      a_grouped["w2", POST][:, 0:HALF])
 
-        def spread_bias2(tag):
-            spread = psum.tile([P, 2, 2, LAT], F32, name="spread", tag=tag, bufs=BANKS)
+        def spread_bias2():
+            spread = psum.tile([P, 2, 2, LAT], F32, name="spread", tag="acc", bufs=BANKS)
             for head in HEADS:
                 nc.tensor.matmul(
                     out=spread[:, head].rearrange("p h c -> p (h c)"),
@@ -304,13 +305,12 @@ def tile_rssmcell_pb_t_kernel(
             nc.scalar.dma_start(out=bias2_raw[PRIOR][:], in_=bp2.unsqueeze(1))
             nc.scalar.dma_start(out=bias2_raw[POST][:], in_=bq2.unsqueeze(1))
             nc.scalar.activation(out=exp_tenth[:], in_=ones[:, 0:1], func=ACT.Exp, scale=0.1)
-            load_h(0)
-            load_h(1)
-            load_h(2)
-            load_w1(PRIOR, 0)
-            load_w1(PRIOR, 1)
-            load_h(3)
-            load_h(4)
+            for i in (0, 1, 2):
+                load_h(i)
+            for a in (0, 1):
+                load_w1(PRIOR, a)
+            for i in (3, 4):
+                load_h(i)
             nc.sync.dma_start(out=bias1[PRIOR][:], in_=bp1.rearrange("(m t) -> m t", t=PACK))
             nc.sync.dma_start(out=bias1[POST][:], in_=bq1.rearrange("(m t) -> m t", t=PACK))
             load_embedding(0)
@@ -320,27 +320,27 @@ def tile_rssmcell_pb_t_kernel(
             load_embedding(1)
             nc.sync.dma_start(out=w2_rows[:, PRIOR, :], in_=wp2)
             nc.sync.dma_start(out=w2_rows[:, POST, :], in_=wq2)
-            load_h(6)
-            load_h(7)
-            for i in range(2, 6):
+            for i in (6, 7):
+                load_h(i)
+            for i in range(2, EMB_BUFS):
                 load_embedding(i)
 
             warm_up(4)
             warm_up(2)
             widen_sorted(0, 0, 2)
             widen_sorted(0, 2, 4)
-            widen(nc.scalar.copy, 1)
+            widen(1)
             for head in HEADS:
                 nc.vector.tensor_copy(out=bias2_column[:, head : head + 1], in_=bias2_raw[head][:])
             for a in (0, 1):
                 turn_c(0, H, a)
                 scale_h(0, a)
-            spread_bias2("acc")
-            widen(nc.scalar.copy, 2)
+            spread_bias2()
+            widen(2)
             for a in (0, 1):
                 turn_w1(PRIOR, a, H, "acc")
                 unload_w1(nc.scalar.copy, PRIOR, a, H)
-            widen(nc.scalar.copy, 3)
+            widen(3)
             warm_up(2)
             quantise_c(0, H)
             for a in (0, 1):
@@ -352,7 +352,7 @@ def tile_rssmcell_pb_t_kernel(
             for a in (0, 1):
                 turn_c(0, E, a)
                 unload_e(nc.scalar.copy, 0, a)
-            load_embedding(6)
+            load_embedding(EMB_BUFS)
             layer1(0, PRIOR, (2, 3))
             quantise_c(1, H)
             widen_sorted(4)
@@ -366,22 +366,22 @@ def tile_rssmcell_pb_t_kernel(
                 unload_w1(nc.vector.tensor_copy, POST, 1, g)
             quantise_w1(POST, 0)
             layer1(1, PRIOR, (2, 3))
-            widen(nc.scalar.copy, 5)
+            widen(5)
             for a in (0, 1):
                 turn_c(2, H, a)
             quantise_w1(POST, 1)
-            interleave_on_gpsimd(0, PRIOR, 448)
+            interleave_on_gpsimd(0, PRIOR, FIRST_GPSIMD)
             for a in (0, 1):
                 scale_h(2, a)
             layer1(0, POST, (0, 1))
             for a in (0, 1):
                 turn_c(1, E, a)
                 unload_e(nc.scalar.copy, 1, a)
-            load_embedding(7)
+            load_embedding(EMB_BUFS + 1)
             layer1(0, POST, (2,))
-            turn_w2("acc")
+            turn_w2()
             layer1(0, POST, (3,))
-            interleave(0, PRIOR, 448, CHUNK)
+            interleave(0, PRIOR, FIRST_GPSIMD, CHUNK)
             quantise_c(2, H)
             quantise_a(0, PRIOR)
             quantise_c(1, E)
@@ -391,56 +391,49 @@ def tile_rssmcell_pb_t_kernel(
             for a in (0, 1):
                 turn_c(3, H, a)
 
-            for i in range(1, CHUNKS - 1 - LEAD):
-                ahead = i + LEAD
-                share = 64 if i >= 3 else 0
+            for i in range(1, CHUNKS - 2):
                 interleave_on_gpsimd(i - 1, POST)
                 for a in (0, 1):
-                    scale_h(ahead + 1, a)
-                layer1(ahead, PRIOR)
+                    scale_h(i + 2, a)
+                layer1(i + 1, PRIOR)
                 if i >= LATE:
                     for head, done in ((PRIOR, i), (POST, i - 2)):
                         second_half(STD, head, done, done + 1, "turned")
                         add_bias_half(STD, head, done, done + 1)
+                elif i == 1:
+                    layer2(0, PRIOR)
+                    layer2(1, PRIOR)
                 else:
-                    for done in range(0 if i == 1 else i, i + 1):
-                        second(done, PRIOR)
-                        add_bias(done, PRIOR)
-                    if i >= 2:
-                        second(i - 2, POST)
-                        add_bias(i - 2, POST)
+                    layer2(i, PRIOR)
+                    layer2(i - 2, POST)
                 for t in (0, 1):
                     first(i, POST, t)
-                if i >= 3:
-                    exp(BOTH, (i - 3) * J, (i - 2) * J)
+                if i >= EXP_LAG:
+                    exp(BOTH, i - EXP_LAG, i - EXP_LAG + 1)
                 else:
-                    widen(nc.scalar.copy, i + 5)
-                extra = 128 if i < LATE else 0
-                if extra:
-                    interleave_on_gpsimd(ahead, PRIOR, CHUNK - share, CHUNK - share - extra)
-                if share:
-                    interleave_on_scalar(ahead, PRIOR, CHUNK - share)
+                    widen(i + WIDE_BUFS)
+                interleave_on_scalar(i + 1, PRIOR, CHUNK - SCALAR_SHARE)
                 for a in (0, 1):
                     turn_c(i + 1, E, a)
                     unload_e(nc.scalar.copy, i + 1, a)
-                quantise_c(ahead + 1, H)
-                interleave(ahead, PRIOR, 0, CHUNK - share - extra)
+                quantise_c(i + 2, H)
+                interleave(i + 1, PRIOR, 0, CHUNK - SCALAR_SHARE)
                 for t in (2, 3):
                     first(i, POST, t)
                 for t in range(PACK):
                     relu(i, POST, t)
                 quantise_c(i + 1, E)
                 quantise_a(i - 1, POST)
-                quantise_a(ahead, PRIOR)
-                if ahead + 2 < CHUNKS:
+                quantise_a(i + 1, PRIOR)
+                if i + 3 < CHUNKS:
                     for a in (0, 1):
-                        turn_c(ahead + 2, H, a)
+                        turn_c(i + 3, H, a)
 
             last = CHUNKS - 1
             for a in (0, 1):
                 turn_c(last, E, a)
                 unload_e((nc.vector.tensor_copy, nc.scalar.copy)[a], last, a)
-            layer1(last, PRIOR, on_vector=())
+            layer1(last, PRIOR)
             interleave(last - 2, POST)
             quantise_c(last, E)
             second(last - 1, PRIOR)
@@ -459,33 +452,28 @@ def tile_rssmcell_pb_t_kernel(
             add_bias(last, PRIOR, (STD,))
             quantise_a(last - 1, POST)
             new_grouped(last, POST, PRIOR)
-            interleave(last, POST, 0, CHUNK - share)
-            interleave_on_scalar(last, POST, CHUNK - share)
-            second_half(MEAN, PRIOR, LATE, last - 1, "acc")
+            interleave(last, POST, 0, CHUNK - LAST_SHARE)
+            interleave_on_scalar(last, POST, CHUNK - LAST_SHARE)
+            second_half(MEAN, PRIOR, LATE, LATE + 2, "acc")
             second(last - 1, POST, tag="acc")
-            second_half(MEAN, POST, LATE - 2, last - 3, "acc")
+            second_half(MEAN, POST, LATE - 2, LATE, "acc")
             add_bias(last - 1, POST, (STD,))
             quantise_a(last, POST)
-            for i in (last - 1, last):
-                add_bias(i, PRIOR, (MEAN,), stored=False)
-            store(PRIOR, MEAN, (last - 1) * J, CHUNKS * J)
-            exp(BOTH, (last - 4) * J, (last - 1) * J)
-            exp(ONLY[PRIOR], (last - 1) * J, CHUNKS * J)
-            exp(ONLY[POST], (last - 1) * J, last * J)
+            kept_means(PRIOR, last - 1)
+            exp(BOTH, CHUNKS - 2 - EXP_LAG, last - 1)
+            exp(ONLY[PRIOR], last - 1, CHUNKS)
+            exp(ONLY[POST], last - 1, last)
             second(last, POST, tag="acc")
             add_bias(last, POST, (STD,))
-            exp(ONLY[POST], last * J, CHUNKS * J)
-            for i in (last - 3, last - 2):
-                add_bias(i, POST, (MEAN,), stored=False)
-            store(POST, MEAN, (last - 3) * J, (last - 1) * J)
-            for i in (last - 1, last):
-                add_bias(i, POST, (MEAN,), stored=False)
-            store(POST, MEAN, (last - 1) * J, CHUNKS * J)
-            add_bias_half(MEAN, PRIOR, LATE, last - 1)
-            add_bias_half(MEAN, POST, LATE - 2, last - 3)
+            exp(ONLY[POST], last, CHUNKS)
+            kept_means(POST, last - 3)
+            kept_means(POST, last - 1)
+            for head, i0 in ((PRIOR, LATE), (POST, LATE - 2)):
+                add_bias_half(MEAN, head, i0, i0 + 2)
+                store(head, MEAN, i0, i0 + 2)
             for pair in range(0, CHUNKS, 2):
                 for head in HEADS:
                     for i in (pair, pair + 1):
-                        log(ONLY[head], i * J, (i + 1) * J)
-                        std(ONLY[head], i * J, (i + 1) * J)
-                    store(head, STD, pair * J, (pair + 2) * J)
+                        log(ONLY[head], i, i + 1)
+                        std(ONLY[head], i, i + 1)
+                    store(head, STD, pair, pair + 2)

@@ -22,6 +22,7 @@ FP8X4 = mybir.dt.float8_e4m3fn_x4
 ACT = mybir.ActivationFunctionType
 ALU = mybir.AluOpType
 
+ALIGN = 256
 BANKS = 4
 WIDE_BUFS = 5
 EMB_BUFS = 6
@@ -62,13 +63,13 @@ def tile_rssmcell_pb_t_kernel(
             for a in (0, 1):
                 name = "w1_%d_%d" % (head, a)
                 w1_rows[head, a] = keep.tile([P, 2, (1 + head) * KIN], BF16, name=name, tag=name)
-                w1_codes[head, a] = keep.tile([P, 1 + head, HALF], U32, name=name + "c", tag=name + "c", align_bytes=64)
-                w1_scales[head, a] = keep.tile([P, 1 + head, HALF], U8, name=name + "s", tag=name + "s", align_bytes=64)
+                w1_codes[head, a] = keep.tile([P, 1 + head, HALF], U32, name=name + "c", tag=name + "c", align_bytes=ALIGN)
+                w1_scales[head, a] = keep.tile([P, 1 + head, HALF], U8, name=name + "s", tag=name + "s", align_bytes=ALIGN)
         w2_rows = keep.tile([P, 2, HID], BF16, name="w2_rows", tag="w2_rows")
         value = keep.tile([P, 2, 2, CHUNKS * J, LAT], F32, name="value", tag="value")
         soft = keep.tile([P, 2, CHUNKS * J * LAT], F32, name="soft", tag="soft")
-        w2_codes = keep.tile([P, 2, DIST], U32, name="w2_codes", tag="w2_codes", align_bytes=64)
-        w2_scales = keep.tile([P, 2, DIST], U8, name="w2_scales", tag="w2_scales", align_bytes=64)
+        w2_codes = keep.tile([P, 2, DIST], U32, name="w2_codes", tag="w2_codes", align_bytes=ALIGN)
+        w2_scales = keep.tile([P, 2, DIST], U8, name="w2_scales", tag="w2_scales", align_bytes=ALIGN)
 
         h_raw, emb, h_wide, turned, c_grouped, c_codes, c_scales = {}, {}, {}, {}, {}, {}, {}
         sorted_chunks = set()
@@ -103,7 +104,7 @@ def tile_rssmcell_pb_t_kernel(
         def unload_w1(copy, head, a, g):
             if g == H:
                 w1_grouped[head, a] = work.tile(
-                    [P, CHUNK, PACK], BF16, name="w1_grouped", tag="a_grouped_%d" % a, bufs=1, align_bytes=64)
+                    [P, CHUNK, PACK], BF16, name="w1_grouped", tag="a_grouped_%d" % a, bufs=1, align_bytes=ALIGN)
             unload(copy, ("w", head, a, g), w1_grouped[head, a][:, g * HALF : (g + 1) * HALF])
 
         def quantise_w1(head, a):
@@ -117,7 +118,7 @@ def tile_rssmcell_pb_t_kernel(
 
 
         def load_h(i):
-            h_raw[i] = work.tile([P, J, KIN], U8, name="h_raw", tag="h_raw", bufs=CHUNKS, align_bytes=64)
+            h_raw[i] = work.tile([P, J, KIN], U8, name="h_raw", tag="h_raw", bufs=CHUNKS, align_bytes=ALIGN)
             nc.sync.dma_start(out=h_raw[i][:], in_=h_bytes.rearrange("(p c j) k -> c p j k", p=P, j=J)[i])
 
         def load_embedding(i):
@@ -125,13 +126,13 @@ def tile_rssmcell_pb_t_kernel(
             nc.sync.dma_start(out=emb[i][:], in_=embedding.rearrange("(p c j) k -> c p j k", p=P, j=J)[i])
 
         def widen(i):
-            h_wide[i] = work.tile([P, J, KIN], BF16, name="h_wide", tag="h_wide", bufs=WIDE_BUFS, align_bytes=64)
+            h_wide[i] = work.tile([P, J, KIN], BF16, name="h_wide", tag="h_wide", bufs=WIDE_BUFS, align_bytes=ALIGN)
             nc.scalar.copy(out=h_wide[i][:].rearrange("p j k -> p (j k)"),
                            in_=h_raw[i][:].rearrange("p j k -> p (j k)").bitcast(FP8))
 
         def widen_sorted(i, j0=0, j1=J):
             if j0 == 0:
-                h_wide[i] = work.tile([P, 2, J * P, 2], BF16, name="h_wide", tag="h_wide", bufs=WIDE_BUFS, align_bytes=64)
+                h_wide[i] = work.tile([P, 2, J * P, 2], BF16, name="h_wide", tag="h_wide", bufs=WIDE_BUFS, align_bytes=ALIGN)
                 sorted_chunks.add(i)
             nc.vector.tensor_scalar(
                 out=h_wide[i][:, :, j0 * P : j1 * P].rearrange("p u q e -> p q u e"),
@@ -147,7 +148,7 @@ def tile_rssmcell_pb_t_kernel(
 
         def grouped_half(i, g, a):
             if a == 0:
-                c_grouped[i, g] = work.tile([P, CHUNK, PACK], BF16, name="c_grouped", tag="c_grouped_%d" % g, bufs=2, align_bytes=64)
+                c_grouped[i, g] = work.tile([P, CHUNK, PACK], BF16, name="c_grouped", tag="c_grouped_%d" % g, bufs=2, align_bytes=ALIGN)
             return c_grouped[i, g][:, a * HALF : (a + 1) * HALF]
 
         def scale_h(i, a):
@@ -161,8 +162,8 @@ def tile_rssmcell_pb_t_kernel(
             unload(copy, (i, E, a), grouped_half(i, E, a))
 
         def quantise_c(i, g):
-            c_codes[i, g] = work.tile([P, CHUNK], U32, name="c_codes", tag="c_codes_%d" % g, bufs=4 - g, align_bytes=64)
-            c_scales[i, g] = work.tile([P, CHUNK], U8, name="c_scales", tag="c_scales_%d" % g, bufs=4 - g, align_bytes=64)
+            c_codes[i, g] = work.tile([P, CHUNK], U32, name="c_codes", tag="c_codes_%d" % g, bufs=4 - g, align_bytes=ALIGN)
+            c_scales[i, g] = work.tile([P, CHUNK], U8, name="c_scales", tag="c_scales_%d" % g, bufs=4 - g, align_bytes=ALIGN)
             quantise(c_codes[i, g][:], c_scales[i, g][:], c_grouped[i, g][:])
 
 
@@ -178,7 +179,7 @@ def tile_rssmcell_pb_t_kernel(
 
         def relu(i, head, t):
             if t == 0:
-                planes[i, head] = work.tile([P, PACK, CHUNK], BF16, name="planes", tag="planes_%d" % head, bufs=2, align_bytes=64)
+                planes[i, head] = work.tile([P, PACK, CHUNK], BF16, name="planes", tag="planes_%d" % head, bufs=2, align_bytes=ALIGN)
             nc.scalar.activation(
                 out=planes[i, head][:, t], in_=acc[i, head, t][:], func=ACT.Relu, bias=bias1[head][:, t : t + 1])
 
@@ -189,7 +190,7 @@ def tile_rssmcell_pb_t_kernel(
 
         def new_grouped(i, head, buffer):
             a_grouped[i, head] = work.tile(
-                [P, CHUNK, PACK], BF16, name="a_grouped", tag="a_grouped_%d" % buffer, bufs=1, align_bytes=64)
+                [P, CHUNK, PACK], BF16, name="a_grouped", tag="a_grouped_%d" % buffer, bufs=1, align_bytes=ALIGN)
 
         def interleave(i, head, n0=0, n1=CHUNK):
             if (i, head) not in a_grouped:
@@ -210,8 +211,8 @@ def tile_rssmcell_pb_t_kernel(
                 scalar1=1.0, scalar2=0.0, op0=ALU.mult, op1=ALU.add)
 
         def quantise_a(i, head):
-            a_codes[i, head] = work.tile([P, CHUNK], U32, name="a_codes", tag="a_codes", bufs=A_BUFS, align_bytes=64)
-            a_scales[i, head] = work.tile([P, CHUNK], U8, name="a_scales", tag="a_scales", bufs=A_BUFS, align_bytes=64)
+            a_codes[i, head] = work.tile([P, CHUNK], U32, name="a_codes", tag="a_codes", bufs=A_BUFS, align_bytes=ALIGN)
+            a_scales[i, head] = work.tile([P, CHUNK], U8, name="a_scales", tag="a_scales", bufs=A_BUFS, align_bytes=ALIGN)
             quantise(a_codes[i, head][:], a_scales[i, head][:], a_grouped[i, head][:])
 
 

@@ -11,6 +11,7 @@ J = 4
 PACK = 4
 CHUNK = P * J
 CHUNKS = B // CHUNK
+GROUPS = CHUNKS + 1
 HALF = CHUNK // 2
 
 F32 = mybir.dt.float32
@@ -23,14 +24,21 @@ ACT = mybir.ActivationFunctionType
 ALU = mybir.AluOpType
 
 ALIGN = 256
-BANKS = 4
-WIDE_BUFS = 5
-EMB_BUFS = 6
-A_BUFS = 10
+BANKS = 8
+WIDE_BUFS = 6
+EMB_BUFS = 5
+GPSIMD_SHARE = 640
+N6 = 640
+L5 = ()
+S7 = 512
+VA = (3,)
+VB = (1, 3)
+VC = (1,)
+A_BUFS = 4
 SCALAR_SHARE = 64
-LAST_SHARE = 128
+LAST_SHARE = 192
 FIRST_GPSIMD = 384
-LATE = CHUNKS - 4
+LATE = CHUNKS - 3
 EXP_LAG = 3
 EXACT_ABOVE = 40.0
 PRIOR, POST = 0, 1
@@ -66,8 +74,8 @@ def tile_rssmcell_pb_t_kernel(
                 w1_codes[head, a] = keep.tile([P, 1 + head, HALF], U32, name=name + "c", tag=name + "c", align_bytes=ALIGN)
                 w1_scales[head, a] = keep.tile([P, 1 + head, HALF], U8, name=name + "s", tag=name + "s", align_bytes=ALIGN)
         w2_rows = keep.tile([P, 2, HID], BF16, name="w2_rows", tag="w2_rows")
-        value = keep.tile([P, 2, 2, CHUNKS * J, LAT], F32, name="value", tag="value")
-        soft = keep.tile([P, 2, CHUNKS * J * LAT], F32, name="soft", tag="soft")
+        value = keep.tile([P, 2, 2, GROUPS * J, LAT], F32, name="value", tag="value")
+        soft = keep.tile([P, 2, GROUPS * J * LAT], F32, name="soft", tag="soft")
         w2_codes = keep.tile([P, 2, DIST], U32, name="w2_codes", tag="w2_codes", align_bytes=ALIGN)
         w2_scales = keep.tile([P, 2, DIST], U8, name="w2_scales", tag="w2_scales", align_bytes=ALIGN)
 
@@ -85,7 +93,7 @@ def tile_rssmcell_pb_t_kernel(
             return lambda b, u: rows[:, b, :].bitcast(F32)[:, u : KIN // 2 : 2]
 
         def bank_of(tag):
-            return psum.tile([P, 2, HALF], F32, name="turned", tag=tag, bufs=BANKS)
+            return psum.tile([P, 2, HALF], F32, name="bank", tag=tag, bufs=BANKS)
 
         def unload(copy, key, dst):
             copy(out=dst.bitcast(F32), in_=turned[key][:].rearrange("p u n -> p n u"))
@@ -104,7 +112,8 @@ def tile_rssmcell_pb_t_kernel(
         def unload_w1(copy, head, a, g):
             if g == H:
                 w1_grouped[head, a] = work.tile(
-                    [P, CHUNK, PACK], BF16, name="w1_grouped", tag="a_grouped_%d" % a, bufs=1, align_bytes=ALIGN)
+                    [P, CHUNK, PACK], BF16, name="w1_grouped", tag="a_grouped" if (head, a) == (POST, 0) else "w_grouped",
+                    bufs=1 if (head, a) == (POST, 0) else 2, align_bytes=ALIGN)
             unload(copy, ("w", head, a, g), w1_grouped[head, a][:, g * HALF : (g + 1) * HALF])
 
         def quantise_w1(head, a):
@@ -112,7 +121,7 @@ def tile_rssmcell_pb_t_kernel(
                      w1_grouped[head, a][:, 0 : (1 + head) * HALF])
 
         def warm_up(copies):
-            unread = psum.tile([P, copies, P], F32, name="unread", tag="acc", bufs=BANKS)
+            unread = psum.tile([P, copies, P], F32, name="unread", tag="bank", bufs=BANKS)
             nc.tensor.matmul(
                 out=unread[:], lhsT=ones[:], rhs=ones[:].unsqueeze(1).to_broadcast([P, copies, P]), start=True, stop=True)
 
@@ -125,10 +134,11 @@ def tile_rssmcell_pb_t_kernel(
             emb[i] = work.tile([P, J, KIN], BF16, name="emb", tag="emb", bufs=EMB_BUFS)
             nc.sync.dma_start(out=emb[i][:], in_=embedding.rearrange("(p c j) k -> c p j k", p=P, j=J)[i])
 
-        def widen(i):
-            h_wide[i] = work.tile([P, J, KIN], BF16, name="h_wide", tag="h_wide", bufs=WIDE_BUFS, align_bytes=ALIGN)
-            nc.scalar.copy(out=h_wide[i][:].rearrange("p j k -> p (j k)"),
-                           in_=h_raw[i][:].rearrange("p j k -> p (j k)").bitcast(FP8))
+        def widen(i, j0=0, j1=J):
+            if j0 == 0:
+                h_wide[i] = work.tile([P, J, KIN], BF16, name="h_wide", tag="h_wide", bufs=WIDE_BUFS, align_bytes=ALIGN)
+            nc.scalar.copy(out=h_wide[i][:, j0:j1].rearrange("p j k -> p (j k)"),
+                           in_=h_raw[i][:, j0:j1].rearrange("p j k -> p (j k)").bitcast(FP8))
 
         def widen_sorted(i, j0=0, j1=J):
             if j0 == 0:
@@ -142,9 +152,9 @@ def tile_rssmcell_pb_t_kernel(
         def turn_c(i, g, a):
             if g == H and i in sorted_chunks:
                 pairs = h_wide[i][:, :, 2 * a * P : (2 * a + 2) * P].rearrange("p u q e -> p u (q e)").bitcast(F32)
-                turn((i, g, a), lambda b, u: pairs[:, u, b * P : (b + 1) * P], bank_of("turned"))
+                turn((i, g, a), lambda b, u: pairs[:, u, b * P : (b + 1) * P], bank_of("bank"))
             else:
-                turn((i, g, a), every_second_word((h_wide, emb)[g][i][:, 2 * a : 2 * a + 2]), bank_of("turned"))
+                turn((i, g, a), every_second_word((h_wide, emb)[g][i][:, 2 * a : 2 * a + 2]), bank_of("bank"))
 
         def grouped_half(i, g, a):
             if a == 0:
@@ -168,7 +178,7 @@ def tile_rssmcell_pb_t_kernel(
 
 
         def first(i, head, t):
-            acc[i, head, t] = psum.tile([P, CHUNK], F32, name="acc", tag="acc", bufs=BANKS)
+            acc[i, head, t] = psum.tile([P, CHUNK], F32, name="bank", tag="bank", bufs=BANKS)
             a, cols = t // 2, slice(t % 2 * P, (t % 2 + 1) * P)
             for g in range(1 + head):
                 nc.tensor.matmul_mx(
@@ -177,121 +187,125 @@ def tile_rssmcell_pb_t_kernel(
                     rhs=c_codes[i, g][:].bitcast(FP8X4), rhs_scale=c_scales[i, g][:],
                     start=(g == 0), stop=(g == head))
 
-        def relu(i, head, t):
-            if t == 0:
-                planes[i, head] = work.tile([P, PACK, CHUNK], BF16, name="planes", tag="planes_%d" % head, bufs=2, align_bytes=ALIGN)
-            nc.scalar.activation(
-                out=planes[i, head][:, t], in_=acc[i, head, t][:], func=ACT.Relu, bias=bias1[head][:, t : t + 1])
+        def plane(i, head, t):
+            s = i + head
+            if s not in planes:
+                planes[s] = work.tile([P, PACK, 2 * CHUNK], BF16, name="planes", tag="planes", bufs=3, align_bytes=ALIGN)
+            return planes[s][:, t, head * CHUNK : (head + 1) * CHUNK]
 
-        def layer1(i, head, tiles=range(PACK)):
+        def relu(i, head, t):
+            nc.scalar.activation(out=plane(i, head, t), in_=acc[i, head, t][:], func=ACT.Relu, bias=bias1[head][:, t : t + 1])
+
+        def relu_on_vector(i, head, t):
+            nc.vector.tensor_scalar(
+                out=plane(i, head, t), in0=acc[i, head, t][:], scalar1=bias1[head][:, t : t + 1], scalar2=0.0,
+                op0=ALU.add, op1=ALU.max)
+
+        def layer1(i, head, tiles=range(PACK), on_vector=()):
             for t in tiles:
                 first(i, head, t)
-                relu(i, head, t)
+                (relu_on_vector if t in on_vector else relu)(i, head, t)
 
-        def new_grouped(i, head, buffer):
-            a_grouped[i, head] = work.tile(
-                [P, CHUNK, PACK], BF16, name="a_grouped", tag="a_grouped_%d" % buffer, bufs=1, align_bytes=ALIGN)
+        def grouped(s, n0, n1):
+            if s >= CHUNKS - 1:
+                head = n0 // CHUNK
+                if (s, head) not in a_grouped:
+                    a_grouped[s, head] = work.tile([P, CHUNK, PACK], BF16, name="a_grouped", tag="c_grouped_%d" % head, bufs=2, align_bytes=ALIGN)
+                return a_grouped[s, head][:, n0 - head * CHUNK : n1 - head * CHUNK]
+            if s not in a_grouped:
+                a_grouped[s] = work.tile([P, 2 * CHUNK, PACK], BF16, name="a_grouped", tag="a_grouped", bufs=1, align_bytes=ALIGN)
+            return a_grouped[s][:, n0:n1]
 
-        def interleave(i, head, n0=0, n1=CHUNK):
-            if (i, head) not in a_grouped:
-                new_grouped(i, head, head)
+        def interleave(s, n0, n1):
             nc.vector.tensor_copy(
-                out=a_grouped[i, head][:, n0:n1].rearrange("p (c i) t -> p c t i", i=4),
-                in_=planes[i, head][:, :, n0:n1].rearrange("p t (c i) -> p c t i", i=4))
+                out=grouped(s, n0, n1).rearrange("p (c i) t -> p c t i", i=4),
+                in_=planes[s][:, :, n0:n1].rearrange("p t (c i) -> p c t i", i=4))
 
-        def interleave_on_scalar(i, head, n0):
-            if (i, head) not in a_grouped:
-                new_grouped(i, head, head)
-            nc.scalar.copy(out=a_grouped[i, head][:, n0:CHUNK], in_=planes[i, head][:, :, n0:CHUNK].rearrange("p t n -> p n t"))
+        def interleave_on_scalar(s, n0, n1):
+            nc.scalar.copy(out=grouped(s, n0, n1), in_=planes[s][:, :, n0:n1].rearrange("p t n -> p n t"))
 
-        def interleave_on_gpsimd(i, head, n1=CHUNK):
-            new_grouped(i, head, head)
+        def interleave_on_gpsimd(s, n0, n1):
             nc.gpsimd.tensor_scalar(
-                out=a_grouped[i, head][:, 0:n1], in0=planes[i, head][:, :, 0:n1].rearrange("p t n -> p n t"),
+                out=grouped(s, n0, n1), in0=planes[s][:, :, n0:n1].rearrange("p t n -> p n t"),
                 scalar1=1.0, scalar2=0.0, op0=ALU.mult, op1=ALU.add)
 
-        def quantise_a(i, head):
-            a_codes[i, head] = work.tile([P, CHUNK], U32, name="a_codes", tag="a_codes", bufs=A_BUFS, align_bytes=ALIGN)
-            a_scales[i, head] = work.tile([P, CHUNK], U8, name="a_scales", tag="a_scales", bufs=A_BUFS, align_bytes=ALIGN)
-            quantise(a_codes[i, head][:], a_scales[i, head][:], a_grouped[i, head][:])
+        def quantise_a(s, heads=BOTH):
+            if s not in a_codes:
+                a_codes[s] = work.tile([P, 2 * CHUNK], U32, name="a_codes", tag="a_codes", bufs=A_BUFS, align_bytes=ALIGN)
+                a_scales[s] = work.tile([P, 2 * CHUNK], U8, name="a_scales", tag="a_scales", bufs=A_BUFS, align_bytes=ALIGN)
+            cols = slice(heads.start * CHUNK, heads.stop * CHUNK)
+            quantise(a_codes[s][:, cols], a_scales[s][:, cols], grouped(s, cols.start, cols.stop))
 
 
-        def second(i, head, tag="turned"):
-            result[i, head] = psum.tile([P, J, 2, LAT], F32, name="result", tag=tag, bufs=BANKS)
+        def pass2(out, s, head, j, cols):
+            tokens = slice(head * CHUNK + j * P, head * CHUNK + (j + 1) * P)
+            nc.tensor.matmul_mx(
+                out=out, lhsT=a_codes[s][:, tokens].bitcast(FP8X4), lhsT_scale=a_scales[s][:, tokens],
+                rhs=w2_codes[:, head, cols].bitcast(FP8X4), rhs_scale=w2_scales[:, head, cols], start=True, stop=True)
+
+        def second(s, head, tag="bank"):
+            result[s, head] = psum.tile([P, J, 2, LAT], F32, name="result", tag=tag, bufs=BANKS)
             for j in range(J):
-                cols = slice(j * P, (j + 1) * P)
-                nc.tensor.matmul_mx(
-                    out=result[i, head][:, j, :, :].rearrange("p h c -> p (h c)"),
-                    lhsT=a_codes[i, head][:, cols].bitcast(FP8X4), lhsT_scale=a_scales[i, head][:, cols],
-                    rhs=w2_codes[:, head, :].bitcast(FP8X4), rhs_scale=w2_scales[:, head, :], start=True, stop=True)
+                pass2(result[s, head][:, j, :, :].rearrange("p h c -> p (h c)"), s, head, j, slice(0, DIST))
 
-        def second_half(half, head, i0, i1, tag):
-            result[half, head, i0, i1] = psum.tile([P, (i1 - i0) * J, LAT], F32, name="result", tag=tag, bufs=BANKS)
-            out = slice(half * LAT, (half + 1) * LAT)
-            for i in range(i0, i1):
+        def second_half(half, s, tag):
+            result["half", half, s] = psum.tile([P, 2, J, LAT], F32, name="result", tag=tag, bufs=BANKS)
+            for head in HEADS:
                 for j in range(J):
-                    cols = slice(j * P, (j + 1) * P)
-                    nc.tensor.matmul_mx(
-                        out=result[half, head, i0, i1][:, (i - i0) * J + j],
-                        lhsT=a_codes[i, head][:, cols].bitcast(FP8X4), lhsT_scale=a_scales[i, head][:, cols],
-                        rhs=w2_codes[:, head, out].bitcast(FP8X4), rhs_scale=w2_scales[:, head, out], start=True, stop=True)
+                    pass2(result["half", half, s][:, head, j], s, head, j, slice(half * LAT, (half + 1) * LAT))
 
-        def add_bias_half(half, head, i0, i1):
+        def add_bias_half(half, s):
             nc.vector.tensor_tensor(
-                out=value[:, head, half, i0 * J : i1 * J], in0=result[half, head, i0, i1][:],
-                in1=bias2[:, head, half].unsqueeze(1).to_broadcast([P, (i1 - i0) * J, LAT]), op=ALU.add)
+                out=value[:, :, half, s * J : (s + 1) * J], in0=result["half", half, s][:],
+                in1=bias2[:, :, half].unsqueeze(2).to_broadcast([P, 2, J, LAT]), op=ALU.add)
 
-        def store(head, half, i0, i1):
+        def store(head, half, s0, s1):
             dst = ((prior_mean, prior_std), (post_mean, post_std))[head][half]
-            tokens = slice(i0 * J, i1 * J)
-            nc.sync.dma_start(out=dst.rearrange("(p n) d -> p n d", p=P)[:, tokens], in_=value[:, head, half, tokens])
+            nc.sync.dma_start(
+                out=dst.rearrange("(p n) d -> p n d", p=P)[:, (s0 - head) * J : (s1 - head) * J],
+                in_=value[:, head, half, s0 * J : s1 * J])
 
-        def add_bias(i, head, halves):
+        def add_bias(s, head, halves):
             part = slice(halves[0], halves[-1] + 1)
             nc.vector.tensor_tensor(
-                out=value[:, head, part, i * J : (i + 1) * J].rearrange("p h j c -> p j h c"),
-                in0=result[i, head][:, :, part],
+                out=value[:, head, part, s * J : (s + 1) * J].rearrange("p h j c -> p j h c"),
+                in0=result[s, head][:, :, part],
                 in1=bias2[:, head, part].unsqueeze(1).to_broadcast([P, J, len(halves), LAT]),
                 op=ALU.add)
 
-        def layer2(i, head):
-            second(i, head)
-            add_bias(i, head, (MEAN, STD))
-            store(head, MEAN, i, i + 1)
+        def layer2(s, head):
+            second(s, head)
+            add_bias(s, head, (MEAN, STD))
+            store(head, MEAN, s, s + 1)
 
-        def kept_means(head, i0):
-            for i in (i0, i0 + 1):
-                add_bias(i, head, (MEAN,))
-            store(head, MEAN, i0, i0 + 2)
+        def w_of(heads, s0, s1):
+            return value[:, heads, STD, s0 * J : s1 * J].rearrange("p e n c -> p e (n c)")
 
-        def w_of(heads, i0, i1):
-            return value[:, heads, STD, i0 * J : i1 * J].rearrange("p e n c -> p e (n c)")
+        def soft_of(heads, s0, s1):
+            return soft[:, heads, s0 * J * LAT : s1 * J * LAT]
 
-        def soft_of(heads, i0, i1):
-            return soft[:, heads, i0 * J * LAT : i1 * J * LAT]
+        def exp(heads, s0, s1):
+            nc.scalar.activation(out=soft_of(heads, s0, s1), in_=w_of(heads, s0, s1), func=ACT.Exp)
 
-        def exp(heads, i0, i1):
-            nc.scalar.activation(out=soft_of(heads, i0, i1), in_=w_of(heads, i0, i1), func=ACT.Exp)
+        def log(heads, s0, s1):
+            nc.scalar.activation(out=soft_of(heads, s0, s1), in_=soft_of(heads, s0, s1), func=ACT.Ln, bias=exp_tenth[:])
 
-        def log(heads, i0, i1):
-            nc.scalar.activation(out=soft_of(heads, i0, i1), in_=soft_of(heads, i0, i1), func=ACT.Ln, bias=exp_tenth[:])
-
-        def std(heads, i0, i1):
+        def std(heads, s0, s1):
             nc.vector.scalar_tensor_tensor(
-                out=w_of(heads, i0, i1), in0=soft_of(heads, i0, i1), scalar=EXACT_ABOVE, in1=w_of(heads, i0, i1),
+                out=w_of(heads, s0, s1), in0=soft_of(heads, s0, s1), scalar=EXACT_ABOVE, in1=w_of(heads, s0, s1),
                 op0=ALU.min, op1=ALU.max)
 
         def turn_w2():
-            turn("w2", every_second_word(w2_rows[:]), bank_of("acc"))
-            new_grouped("w2", POST, POST)
-            unload(nc.scalar.copy, "w2", a_grouped["w2", POST][:, 0:HALF])
+            turn("w2", every_second_word(w2_rows[:]), bank_of("bank"))
+            w1_grouped["w2"] = work.tile([P, CHUNK, PACK], BF16, name="w2_grouped", tag="w_grouped", bufs=2, align_bytes=ALIGN)
+            unload(nc.scalar.copy, "w2", w1_grouped["w2"][:, 0:HALF])
 
         def quantise_w2():
             quantise(w2_codes[:].rearrange("p e m -> p (e m)"), w2_scales[:].rearrange("p e m -> p (e m)"),
-                     a_grouped["w2", POST][:, 0:HALF])
+                     w1_grouped["w2"][:, 0:HALF])
 
         def spread_bias2():
-            spread = psum.tile([P, 2, 2, LAT], F32, name="spread", tag="acc", bufs=BANKS)
+            spread = psum.tile([P, 2, 2, LAT], F32, name="spread", tag="bank", bufs=BANKS)
             for head in HEADS:
                 nc.tensor.matmul(
                     out=spread[:, head].rearrange("p h c -> p (h c)"),
@@ -306,23 +320,23 @@ def tile_rssmcell_pb_t_kernel(
             nc.scalar.dma_start(out=bias2_raw[PRIOR][:], in_=bp2.unsqueeze(1))
             nc.scalar.dma_start(out=bias2_raw[POST][:], in_=bq2.unsqueeze(1))
             nc.scalar.activation(out=exp_tenth[:], in_=ones[:, 0:1], func=ACT.Exp, scale=0.1)
-            for i in (0, 1, 2):
+            for i in (0, 1, 4):
                 load_h(i)
             for a in (0, 1):
                 load_w1(PRIOR, a)
-            for i in (3, 4):
+            for i in (5, 2):
                 load_h(i)
             nc.sync.dma_start(out=bias1[PRIOR][:], in_=bp1.rearrange("(m t) -> m t", t=PACK))
             nc.sync.dma_start(out=bias1[POST][:], in_=bq1.rearrange("(m t) -> m t", t=PACK))
             load_embedding(0)
             load_w1(POST, 0)
-            load_h(5)
+            load_h(3)
             load_w1(POST, 1)
             load_embedding(1)
+            load_h(6)
             nc.sync.dma_start(out=w2_rows[:, PRIOR, :], in_=wp2)
             nc.sync.dma_start(out=w2_rows[:, POST, :], in_=wq2)
-            for i in (6, 7):
-                load_h(i)
+            load_h(7)
             for i in range(2, EMB_BUFS):
                 load_embedding(i)
 
@@ -337,11 +351,11 @@ def tile_rssmcell_pb_t_kernel(
                 turn_c(0, H, a)
                 scale_h(0, a)
             spread_bias2()
-            widen(2)
+            widen(4)
             for a in (0, 1):
-                turn_w1(PRIOR, a, H, "acc")
+                turn_w1(PRIOR, a, H, "bank")
                 unload_w1(nc.scalar.copy, PRIOR, a, H)
-            widen(3)
+            widen(5)
             warm_up(2)
             quantise_c(0, H)
             for a in (0, 1):
@@ -356,125 +370,124 @@ def tile_rssmcell_pb_t_kernel(
             load_embedding(EMB_BUFS)
             layer1(0, PRIOR, (2, 3))
             quantise_c(1, H)
-            widen_sorted(4)
+            widen_sorted(2)
             quantise_c(0, E)
+            widen_sorted(3)
             for g in (H, E):
-                turn_w1(POST, 0, g, "turned")
+                turn_w1(POST, 0, g, "bank")
                 unload_w1(nc.scalar.copy, POST, 0, g)
             layer1(1, PRIOR, (0, 1))
             for g in (H, E):
-                turn_w1(POST, 1, g, "turned")
-                unload_w1(nc.vector.tensor_copy, POST, 1, g)
-            quantise_w1(POST, 0)
+                turn_w1(POST, 1, g, "bank")
+                unload_w1((nc.scalar.copy, nc.vector.tensor_copy)[g], POST, 1, g)
             layer1(1, PRIOR, (2, 3))
-            widen(5)
+            widen(6)
             for a in (0, 1):
                 turn_c(2, H, a)
+            quantise_w1(POST, 0)
             quantise_w1(POST, 1)
-            interleave_on_gpsimd(0, PRIOR, FIRST_GPSIMD)
+            interleave_on_gpsimd(0, 0, CHUNK)
             for a in (0, 1):
                 scale_h(2, a)
             layer1(0, POST, (0, 1))
             for a in (0, 1):
                 turn_c(1, E, a)
-                unload_e(nc.scalar.copy, 1, a)
+                unload_e(nc.vector.tensor_copy if a == 0 else nc.scalar.copy, 1, a)
             load_embedding(EMB_BUFS + 1)
-            layer1(0, POST, (2,))
             turn_w2()
-            layer1(0, POST, (3,))
-            interleave(0, PRIOR, FIRST_GPSIMD, CHUNK)
+            layer1(0, POST, (2, 3))
             quantise_c(2, H)
-            quantise_a(0, PRIOR)
             quantise_c(1, E)
-            interleave(1, PRIOR)
             quantise_w2()
-            quantise_a(1, PRIOR)
             for a in (0, 1):
                 turn_c(3, H, a)
-
-            for i in range(1, CHUNKS - 2):
-                interleave_on_gpsimd(i - 1, POST)
-                for a in (0, 1):
-                    scale_h(i + 2, a)
-                layer1(i + 1, PRIOR)
-                if i >= LATE:
-                    for head, done in ((PRIOR, i), (POST, i - 2)):
-                        second_half(STD, head, done, done + 1, "turned")
-                        add_bias_half(STD, head, done, done + 1)
-                elif i == 1:
-                    layer2(0, PRIOR)
-                    layer2(1, PRIOR)
-                else:
-                    layer2(i, PRIOR)
-                    layer2(i - 2, POST)
-                for t in (0, 1):
-                    first(i, POST, t)
-                if i >= EXP_LAG:
-                    exp(BOTH, i - EXP_LAG, i - EXP_LAG + 1)
-                else:
-                    widen(i + WIDE_BUFS)
-                interleave_on_scalar(i + 1, PRIOR, CHUNK - SCALAR_SHARE)
-                for a in (0, 1):
-                    turn_c(i + 1, E, a)
-                    unload_e(nc.scalar.copy, i + 1, a)
-                quantise_c(i + 2, H)
-                interleave(i + 1, PRIOR, 0, CHUNK - SCALAR_SHARE)
-                for t in (2, 3):
-                    first(i, POST, t)
-                for t in range(PACK):
-                    relu(i, POST, t)
-                quantise_c(i + 1, E)
-                quantise_a(i - 1, POST)
-                quantise_a(i + 1, PRIOR)
-                if i + 3 < CHUNKS:
-                    for a in (0, 1):
-                        turn_c(i + 3, H, a)
+            widen(7)
+            for a in (0, 1):
+                turn_c(2, E, a)
+            unload_e(nc.scalar.copy, 2, 0)
+            quantise_a(0, ONLY[PRIOR])
 
             last = CHUNKS - 1
-            for a in (0, 1):
-                turn_c(last, E, a)
-                unload_e((nc.vector.tensor_copy, nc.scalar.copy)[a], last, a)
-            layer1(last, PRIOR)
-            interleave(last - 2, POST)
-            quantise_c(last, E)
-            second(last - 1, PRIOR)
-            add_bias(last - 1, PRIOR, (STD,))
-            quantise_a(last - 2, POST)
-            second(last - 3, POST)
-            add_bias(last - 3, POST, (STD,))
-            interleave(last, PRIOR)
-            layer1(last - 1, POST)
-            second(last - 2, POST)
-            add_bias(last - 2, POST, (STD,))
-            quantise_a(last, PRIOR)
-            interleave(last - 1, POST)
-            layer1(last, POST)
+            for s in range(1, CHUNKS - 2):
+                interleave_on_gpsimd(s, 0, GPSIMD_SHARE)
+                for a in (0, 1):
+                    scale_h(s + 2, a)
+                if s == 1:
+                    unload_e(nc.vector.tensor_copy, 2, 1)
+                    load_embedding(EMB_BUFS + 2)
+                if s > 1:
+                    exp(BOTH if s > 2 else ONLY[PRIOR], s - 2, s - 1)
+                layer1(s, POST, (0, 1))
+                for head in HEADS[: min(s, 2)]:
+                    layer2(s - 1, head)
+                layer1(s, POST, (2, 3))
+                if s + 2 == last:
+                    for a in (0, 1):
+                        turn_c(s + 2, E, a)
+                        unload_e(nc.scalar.copy, s + 2, a)
+                layer1(s + 1, PRIOR)
+                interleave(s, GPSIMD_SHARE, 2 * CHUNK)
+                quantise_c(s + 1, E)
+                if s + 2 < last:
+                    quantise_a(s)
+                    quantise_c(s + 2, H)
+                    for a in (0, 1):
+                        turn_c(s + 2, E, a)
+                        unload_e(nc.scalar.copy, s + 2, a)
+                    for a in (0, 1):
+                        turn_c(s + 3, H, a)
+                else:
+                    quantise_c(s + 2, H)
+                    quantise_a(s)
+                    quantise_c(s + 2, E)
+
+            s = last - 1
+            interleave_on_gpsimd(s, 0, N6)
+            layer1(s, POST, on_vector=VA)
+            for head in HEADS:
+                second(s - 1, head)
+                add_bias(s - 1, head, (STD,) if head in L5 else (MEAN, STD))
+                if head not in L5:
+                    store(head, MEAN, s - 1, s)
+            layer1(last, PRIOR, on_vector=VB)
+            layer1(last, POST, on_vector=VC)
+            interleave(s, N6, 2 * CHUNK)
+            interleave_on_scalar(last, 2 * CHUNK - S7, 2 * CHUNK)
+            interleave(last, 0, CHUNK)
+            quantise_a(s)
+            if S7 < CHUNK:
+                interleave(last, CHUNK, 2 * CHUNK - S7)
+            quantise_a(last, ONLY[PRIOR])
+            for head in HEADS:
+                second(s, head)
             second(last, PRIOR)
-            add_bias(last, PRIOR, (STD,))
-            quantise_a(last - 1, POST)
-            new_grouped(last, POST, PRIOR)
-            interleave(last, POST, 0, CHUNK - LAST_SHARE)
-            interleave_on_scalar(last, POST, CHUNK - LAST_SHARE)
-            second_half(MEAN, PRIOR, LATE, LATE + 2, "acc")
-            second(last - 1, POST, tag="acc")
-            second_half(MEAN, POST, LATE - 2, LATE, "acc")
-            add_bias(last - 1, POST, (STD,))
-            quantise_a(last, POST)
-            kept_means(PRIOR, last - 1)
-            exp(BOTH, CHUNKS - 2 - EXP_LAG, last - 1)
-            exp(ONLY[PRIOR], last - 1, CHUNKS)
-            exp(ONLY[POST], last - 1, last)
-            second(last, POST, tag="acc")
-            add_bias(last, POST, (STD,))
-            exp(ONLY[POST], last, CHUNKS)
-            kept_means(POST, last - 3)
-            kept_means(POST, last - 1)
-            for head, i0 in ((PRIOR, LATE), (POST, LATE - 2)):
-                add_bias_half(MEAN, head, i0, i0 + 2)
-                store(head, MEAN, i0, i0 + 2)
+            s = CHUNKS
+            interleave_on_scalar(s, 2 * CHUNK - LAST_SHARE, 2 * CHUNK)
+            exp(BOTH, s - 4, s - 2)
+            interleave(s, CHUNK, 2 * CHUNK - LAST_SHARE)
+            quantise_a(last, ONLY[POST])
+            second(last, POST)
+            add_bias(s - 2, PRIOR, (STD,))
+            quantise_a(s, ONLY[POST])
+            add_bias(s - 2, POST, (STD,))
+            exp(BOTH, s - 2, last)
+            second(s, POST)
+            for head in HEADS:
+                add_bias(last, head, (STD,))
+                exp(ONLY[head], last, s)
+            add_bias(s, POST, (STD,))
+            exp(ONLY[POST], s, s + 1)
+            for head in HEADS:
+                s0 = last - 2 if head in L5 else last - 1
+                for late in range(s0, s + head):
+                    add_bias(late, head, (MEAN,))
+                    if late == s0 + 1:
+                        store(head, MEAN, s0, s0 + 2)
+                if s0 + 2 < s + head:
+                    store(head, MEAN, s0 + 2, s + head)
             for pair in range(0, CHUNKS, 2):
                 for head in HEADS:
-                    for i in (pair, pair + 1):
-                        log(ONLY[head], i, i + 1)
-                        std(ONLY[head], i, i + 1)
-                    store(head, STD, pair, pair + 2)
+                    for s in (pair + head, pair + head + 1):
+                        log(ONLY[head], s, s + 1)
+                        std(ONLY[head], s, s + 1)
+                    store(head, STD, pair + head, pair + head + 2)

@@ -27,9 +27,14 @@ ALIGN = 256
 BANKS = 8
 WIDE_BUFS = 6
 EMB_BUFS = 5
-GPSIMD_SHARE = 640
-N6 = 640
-L5 = ()
+GPSIMD_SHARE = 672
+C3 = 1
+W11 = 1
+E10 = 1
+E21 = 1
+SS = 64
+N6 = 576
+L5 = 1
 S7 = 512
 VA = (3,)
 VB = (1, 3)
@@ -126,9 +131,11 @@ def tile_rssmcell_pb_t_kernel(
                 out=unread[:], lhsT=ones[:], rhs=ones[:].unsqueeze(1).to_broadcast([P, copies, P]), start=True, stop=True)
 
 
-        def load_h(i):
+        def load_h(i, pieces=((0, J),)):
             h_raw[i] = work.tile([P, J, KIN], U8, name="h_raw", tag="h_raw", bufs=CHUNKS, align_bytes=ALIGN)
-            nc.sync.dma_start(out=h_raw[i][:], in_=h_bytes.rearrange("(p c j) k -> c p j k", p=P, j=J)[i])
+            rows = h_bytes.rearrange("(p c j) k -> c p j k", p=P, j=J)[i]
+            for j0, j1 in pieces:
+                nc.sync.dma_start(out=h_raw[i][:, j0:j1], in_=rows[:, j0:j1])
 
         def load_embedding(i):
             emb[i] = work.tile([P, J, KIN], BF16, name="emb", tag="emb", bufs=EMB_BUFS)
@@ -320,7 +327,8 @@ def tile_rssmcell_pb_t_kernel(
             nc.scalar.dma_start(out=bias2_raw[PRIOR][:], in_=bp2.unsqueeze(1))
             nc.scalar.dma_start(out=bias2_raw[POST][:], in_=bq2.unsqueeze(1))
             nc.scalar.activation(out=exp_tenth[:], in_=ones[:, 0:1], func=ACT.Exp, scale=0.1)
-            for i in (0, 1, 4):
+            load_h(0, ((0, 2), (2, J)))
+            for i in (1, 4):
                 load_h(i)
             for a in (0, 1):
                 load_w1(PRIOR, a)
@@ -372,14 +380,14 @@ def tile_rssmcell_pb_t_kernel(
             quantise_c(1, H)
             widen_sorted(2)
             quantise_c(0, E)
-            widen_sorted(3)
+            (widen_sorted if C3 else widen)(3)
             for g in (H, E):
                 turn_w1(POST, 0, g, "bank")
                 unload_w1(nc.scalar.copy, POST, 0, g)
             layer1(1, PRIOR, (0, 1))
             for g in (H, E):
                 turn_w1(POST, 1, g, "bank")
-                unload_w1((nc.scalar.copy, nc.vector.tensor_copy)[g], POST, 1, g)
+                unload_w1((nc.scalar.copy, nc.vector.tensor_copy)[g * W11], POST, 1, g)
             layer1(1, PRIOR, (2, 3))
             widen(6)
             for a in (0, 1):
@@ -392,7 +400,7 @@ def tile_rssmcell_pb_t_kernel(
             layer1(0, POST, (0, 1))
             for a in (0, 1):
                 turn_c(1, E, a)
-                unload_e(nc.vector.tensor_copy if a == 0 else nc.scalar.copy, 1, a)
+                unload_e(nc.vector.tensor_copy if a == 0 and E10 else nc.scalar.copy, 1, a)
             load_embedding(EMB_BUFS + 1)
             turn_w2()
             layer1(0, POST, (2, 3))
@@ -413,7 +421,7 @@ def tile_rssmcell_pb_t_kernel(
                 for a in (0, 1):
                     scale_h(s + 2, a)
                 if s == 1:
-                    unload_e(nc.vector.tensor_copy, 2, 1)
+                    unload_e(nc.vector.tensor_copy if E21 else nc.scalar.copy, 2, 1)
                     load_embedding(EMB_BUFS + 2)
                 if s > 1:
                     exp(BOTH if s > 2 else ONLY[PRIOR], s - 2, s - 1)
@@ -421,12 +429,14 @@ def tile_rssmcell_pb_t_kernel(
                 for head in HEADS[: min(s, 2)]:
                     layer2(s - 1, head)
                 layer1(s, POST, (2, 3))
+                if SS:
+                    interleave_on_scalar(s, 2 * CHUNK - SS, 2 * CHUNK)
                 if s + 2 == last:
                     for a in (0, 1):
                         turn_c(s + 2, E, a)
                         unload_e(nc.scalar.copy, s + 2, a)
                 layer1(s + 1, PRIOR)
-                interleave(s, GPSIMD_SHARE, 2 * CHUNK)
+                interleave(s, GPSIMD_SHARE, 2 * CHUNK - SS)
                 quantise_c(s + 1, E)
                 if s + 2 < last:
                     quantise_a(s)
@@ -444,13 +454,16 @@ def tile_rssmcell_pb_t_kernel(
             s = last - 1
             interleave_on_gpsimd(s, 0, N6)
             layer1(s, POST, on_vector=VA)
-            for head in HEADS:
-                second(s - 1, head)
-                add_bias(s - 1, head, (STD,) if head in L5 else (MEAN, STD))
-                if head not in L5:
-                    store(head, MEAN, s - 1, s)
+            if L5:
+                second_half(STD, s - 1, "bank")
+                add_bias_half(STD, s - 1)
+            else:
+                for head in HEADS:
+                    layer2(s - 1, head)
             layer1(last, PRIOR, on_vector=VB)
             layer1(last, POST, on_vector=VC)
+            if L5:
+                second_half(MEAN, s - 1, "bank")
             interleave(s, N6, 2 * CHUNK)
             interleave_on_scalar(last, 2 * CHUNK - S7, 2 * CHUNK)
             interleave(last, 0, CHUNK)
@@ -477,9 +490,11 @@ def tile_rssmcell_pb_t_kernel(
                 exp(ONLY[head], last, s)
             add_bias(s, POST, (STD,))
             exp(ONLY[POST], s, s + 1)
+            s0 = last - 2 if L5 else last - 1
+            if L5:
+                add_bias_half(MEAN, s0)
             for head in HEADS:
-                s0 = last - 2 if head in L5 else last - 1
-                for late in range(s0, s + head):
+                for late in range(last - 1, s + head):
                     add_bias(late, head, (MEAN,))
                     if late == s0 + 1:
                         store(head, MEAN, s0, s0 + 2)
@@ -487,7 +502,11 @@ def tile_rssmcell_pb_t_kernel(
                     store(head, MEAN, s0 + 2, s + head)
             for pair in range(0, CHUNKS, 2):
                 for head in HEADS:
+                    final = pair + 2 == CHUNKS and head == POST
                     for s in (pair + head, pair + head + 1):
                         log(ONLY[head], s, s + 1)
                         std(ONLY[head], s, s + 1)
-                    store(head, STD, pair + head, pair + head + 2)
+                        if final:
+                            store(head, STD, s, s + 1)
+                    if not final:
+                        store(head, STD, pair + head, pair + head + 2)

@@ -125,11 +125,6 @@ def tile_rssmcell_pb_t_kernel(
             quantise(w1_codes[head, a][:].rearrange("p g m -> p (g m)"), w1_scales[head, a][:].rearrange("p g m -> p (g m)"),
                      w1_grouped[head, a][:, 0 : (1 + head) * HALF])
 
-        def warm_up(copies):
-            unread = psum.tile([P, copies, P], F32, name="unread", tag="bank", bufs=BANKS)
-            nc.tensor.matmul(
-                out=unread[:], lhsT=ones[:], rhs=ones[:].unsqueeze(1).to_broadcast([P, copies, P]), start=True, stop=True)
-
 
         def load_h(i, pieces=((0, J),)):
             h_raw[i] = work.tile([P, J, KIN], U8, name="h_raw", tag="h_raw", bufs=CHUNKS, align_bytes=ALIGN)
@@ -348,8 +343,6 @@ def tile_rssmcell_pb_t_kernel(
             for i in range(2, EMB_BUFS):
                 load_embedding(i)
 
-            warm_up(4)
-            warm_up(2)
             widen_sorted(0, 0, 2)
             widen_sorted(0, 2, 4)
             widen(1)
@@ -364,7 +357,6 @@ def tile_rssmcell_pb_t_kernel(
                 turn_w1(PRIOR, a, H, "bank")
                 unload_w1(nc.scalar.copy, PRIOR, a, H)
             widen(5)
-            warm_up(2)
             quantise_c(0, H)
             for a in (0, 1):
                 quantise_w1(PRIOR, a)

@@ -33,15 +33,16 @@ W11 = 1
 E10 = 1
 E21 = 1
 SS = 64
+T8 = 256
 N6 = 576
 L5 = 1
-S7 = 512
+S7 = 256
 VA = (3,)
 VB = (1, 3)
 VC = (1,)
 A_BUFS = 4
 SCALAR_SHARE = 64
-LAST_SHARE = 192
+LAST_SHARE = 0
 FIRST_GPSIMD = 384
 LATE = CHUNKS - 3
 EXP_LAG = 3
@@ -67,6 +68,7 @@ def tile_rssmcell_pb_t_kernel(
         bias2_column = keep.tile([P, 2], F32, name="bias2_column", tag="bias2_column")
         ones = keep.tile([P, P], F32, name="ones", tag="ones")
         ident = keep.tile([P, P], F32, name="ident", tag="ident")
+        ident16 = keep.tile([P, P], BF16, name="ident16", tag="ident16")
         scale = keep.tile([P, PACK], F32, name="scale", tag="scale")
         bias1 = [keep.tile([P, PACK], BF16, name="bias1_%d" % e, tag="bias1_%d" % e) for e in HEADS]
         bias2 = keep.tile([P, 2, 2, LAT], F32, name="bias2", tag="bias2")
@@ -85,6 +87,7 @@ def tile_rssmcell_pb_t_kernel(
         w2_scales = keep.tile([P, 2, DIST], U8, name="w2_scales", tag="w2_scales", align_bytes=ALIGN)
 
         h_raw, emb, h_wide, turned, c_grouped, c_codes, c_scales = {}, {}, {}, {}, {}, {}, {}
+        mixed = {}
         sorted_chunks = set()
         w1_grouped, acc, planes, a_grouped, a_codes, a_scales, result = {}, {}, {}, {}, {}, {}, {}
 
@@ -231,6 +234,16 @@ def tile_rssmcell_pb_t_kernel(
                 out=grouped(s, n0, n1), in0=planes[s][:, :, n0:n1].rearrange("p t n -> p n t"),
                 scalar1=1.0, scalar2=0.0, op0=ALU.mult, op1=ALU.add)
 
+        def interleave_on_tensor(s, n0):
+            mixed[s, n0] = psum.tile([P, HALF, PACK], BF16, name="mixed", tag="bank", bufs=BANKS)
+            for m in (0, P):
+                nc.tensor.matmul(
+                    out=mixed[s, n0][:, m : m + P].rearrange("p n t -> p t n"), lhsT=ident16[:],
+                    rhs=planes[s][:, :, n0 + m : n0 + m + P], start=True, stop=True)
+
+        def unload_mixed(s, n0):
+            nc.scalar.copy(out=grouped(s, n0, n0 + HALF).bitcast(F32), in_=mixed[s, n0][:].bitcast(F32))
+
         def quantise_a(s, heads=BOTH):
             if s not in a_codes:
                 a_codes[s] = work.tile([P, 2 * CHUNK], U32, name="a_codes", tag="a_codes", bufs=A_BUFS, align_bytes=ALIGN)
@@ -318,6 +331,7 @@ def tile_rssmcell_pb_t_kernel(
         with tc.manual_schedule():
             nc.vector.memset(ones[:], 1.0)
             make_identity(nc, ident[:])
+            make_identity(nc, ident16[:])
             nc.scalar.dma_start(out=scale[:], in_=h_scale.rearrange("o (p t) -> p (o t)", t=PACK))
             nc.scalar.dma_start(out=bias2_raw[PRIOR][:], in_=bp2.unsqueeze(1))
             nc.scalar.dma_start(out=bias2_raw[POST][:], in_=bq2.unsqueeze(1))
@@ -454,22 +468,29 @@ def tile_rssmcell_pb_t_kernel(
                     layer2(s - 1, head)
             layer1(last, PRIOR, on_vector=VB)
             layer1(last, POST, on_vector=VC)
-            if L5:
-                second_half(MEAN, s - 1, "bank")
             interleave(s, N6, 2 * CHUNK)
-            interleave_on_scalar(last, 2 * CHUNK - S7, 2 * CHUNK)
-            interleave(last, 0, CHUNK)
+            for n0 in (CHUNK, CHUNK + HALF):
+                interleave_on_tensor(last, n0)
+            for n0 in range(2 * CHUNK - T8, 2 * CHUNK, HALF):
+                interleave_on_tensor(CHUNKS, n0)
+            if S7:
+                interleave_on_scalar(last, CHUNK - S7, CHUNK)
+            for n0 in (CHUNK, CHUNK + HALF):
+                unload_mixed(last, n0)
+            interleave(last, 0, CHUNK - S7)
             quantise_a(s)
-            if S7 < CHUNK:
-                interleave(last, CHUNK, 2 * CHUNK - S7)
             quantise_a(last, ONLY[PRIOR])
             for head in HEADS:
                 second(s, head)
             second(last, PRIOR)
             s = CHUNKS
-            interleave_on_scalar(s, 2 * CHUNK - LAST_SHARE, 2 * CHUNK)
+            if LAST_SHARE:
+                interleave_on_scalar(s, 2 * CHUNK - T8 - LAST_SHARE, 2 * CHUNK - T8)
+            for n0 in range(2 * CHUNK - T8, 2 * CHUNK, HALF):
+                unload_mixed(CHUNKS, n0)
             exp(BOTH, s - 4, s - 2)
-            interleave(s, CHUNK, 2 * CHUNK - LAST_SHARE)
+            if T8 + LAST_SHARE < CHUNK:
+                interleave(s, CHUNK, 2 * CHUNK - T8 - LAST_SHARE)
             quantise_a(last, ONLY[POST])
             second(last, POST)
             add_bias(s - 2, PRIOR, (STD,))
@@ -477,6 +498,7 @@ def tile_rssmcell_pb_t_kernel(
             add_bias(s - 2, POST, (STD,))
             exp(BOTH, s - 2, last)
             second(s, POST)
+            second_half(MEAN, s - 3, "bank")
             for head in HEADS:
                 add_bias(last, head, (STD,))
                 exp(ONLY[head], last, s)

@@ -64,9 +64,12 @@ def tile_rssmcell_pb_t_kernel(
         work = ctx.enter_context(tc.tile_pool(name="work", bufs=2))
         psum = ctx.enter_context(tc.psum_pool(name="psum", bufs=1))
 
+        def shifted(pool, columns, dtype, skip, **kw):
+            return pool.tile([P, skip + columns], dtype, align_bytes=ALIGN, **kw)[:, skip : skip + columns]
+
         bias2_raw = [keep.tile([P, 1], BF16, name="bias2_raw_%d" % e, tag="bias2_raw_%d" % e) for e in HEADS]
         bias2_column = keep.tile([P, 2], F32, name="bias2_column", tag="bias2_column")
-        ones = keep.tile([P, P], F32, name="ones", tag="ones")
+        ones = keep.tile([P, 1], F32, name="ones", tag="ones")
         ident = keep.tile([P, P], F32, name="ident", tag="ident")
         ident16 = keep.tile([P, P], BF16, name="ident16", tag="ident16")
         scale = keep.tile([P, PACK], F32, name="scale", tag="scale")
@@ -79,12 +82,13 @@ def tile_rssmcell_pb_t_kernel(
                 name = "w1_%d_%d" % (head, a)
                 w1_rows[head, a] = keep.tile([P, 2, (1 + head) * KIN], BF16, name=name, tag=name)
                 w1_codes[head, a] = keep.tile([P, 1 + head, HALF], U32, name=name + "c", tag=name + "c", align_bytes=ALIGN)
-                w1_scales[head, a] = keep.tile([P, 1 + head, HALF], U8, name=name + "s", tag=name + "s", align_bytes=ALIGN)
+                w1_scales[head, a] = shifted(keep, (1 + head) * HALF, U8, 64, name=name + "s", tag=name + "s").rearrange(
+                    "p (g m) -> p g m", m=HALF)
         w2_rows = keep.tile([P, 2, HID], BF16, name="w2_rows", tag="w2_rows")
         value = keep.tile([P, 2, 2, GROUPS * J, LAT], F32, name="value", tag="value")
         soft = keep.tile([P, 2, GROUPS * J * LAT], F32, name="soft", tag="soft")
-        w2_codes = keep.tile([P, 2, DIST], U32, name="w2_codes", tag="w2_codes", align_bytes=ALIGN)
-        w2_scales = keep.tile([P, 2, DIST], U8, name="w2_scales", tag="w2_scales", align_bytes=ALIGN)
+        w2_codes = shifted(keep, 2 * DIST, U32, 32, name="w2_codes", tag="w2_codes").rearrange("p (e m) -> p e m", e=2)
+        w2_scales = shifted(keep, 2 * DIST, U8, 64, name="w2_scales", tag="w2_scales").rearrange("p (e m) -> p e m", e=2)
 
         h_raw, emb, h_wide, turned, c_grouped, c_codes, c_scales = {}, {}, {}, {}, {}, {}, {}
         mixed = {}
@@ -177,8 +181,8 @@ def tile_rssmcell_pb_t_kernel(
             unload(copy, (i, E, a), grouped_half(i, E, a))
 
         def quantise_c(i, g):
-            c_codes[i, g] = work.tile([P, CHUNK], U32, name="c_codes", tag="c_codes_%d" % g, bufs=4 - g, align_bytes=ALIGN)
-            c_scales[i, g] = work.tile([P, CHUNK], U8, name="c_scales", tag="c_scales_%d" % g, bufs=4 - g, align_bytes=ALIGN)
+            c_codes[i, g] = shifted(work, CHUNK, U32, 32, name="c_codes", tag="c_codes_%d" % g, bufs=3)
+            c_scales[i, g] = shifted(work, CHUNK, U8, 192, name="c_scales", tag="c_scales_%d" % g, bufs=3)
             quantise(c_codes[i, g][:], c_scales[i, g][:], c_grouped[i, g][:])
 
 

@@ -27,11 +27,18 @@ ALIGN = 256
 BANKS = 8
 WIDE_BUFS = 6
 EMB_BUFS = 5
+A_BUFS = 4
+EXACT_ABOVE = 40.0
+PRIOR, POST = 0, 1
+HEADS = (PRIOR, POST)
+BOTH, ONLY = slice(0, 2), (slice(0, 1), slice(1, 2))
+MEAN, STD = 0, 1
+H, E = 0, 1
 GPSIMD_SHARE = 672
 C3 = 1
 W11 = 1
 E10 = 1
-E21 = 1
+E21 = 0
 SS = 64
 T8 = 256
 N6 = 576
@@ -40,18 +47,20 @@ S7 = 256
 VA = (3,)
 VB = (1, 3)
 VC = (1,)
-A_BUFS = 4
-SCALAR_SHARE = 64
 LAST_SHARE = 0
-FIRST_GPSIMD = 384
-LATE = CHUNKS - 3
-EXP_LAG = 3
-EXACT_ABOVE = 40.0
-PRIOR, POST = 0, 1
-HEADS = (PRIOR, POST)
-BOTH, ONLY = slice(0, 2), (slice(0, 1), slice(1, 2))
-MEAN, STD = 0, 1
-H, E = 0, 1
+GATE = 1
+FIRST_TAG = ("a_grouped", 1)
+W_TAGS = {(0, 0): ("w_grouped", 2), (0, 1): ("late_wide", 1), (1, GATE): ("a_grouped", 1), (1, 1 - GATE): ("w_grouped", 2)}
+WIDE_BUFS = 5
+D6 = 0
+GJ = 4
+E01 = 1
+C5 = 1
+C6 = 0
+DIRECT = (0, 2, 2, 0, 0, 0, 0, 0)
+GP = (0, 768, 768, 672, 672, 672)
+SP = (0, 64, 64, 64, 64, 64)
+CASTS = {1: 6, 2: 7}
 
 
 def tile_rssmcell_pb_t_kernel(
@@ -91,7 +100,7 @@ def tile_rssmcell_pb_t_kernel(
         w2_scales = shifted(keep, 2 * DIST, U8, 64, name="w2_scales", tag="w2_scales").rearrange("p (e m) -> p e m", e=2)
 
         h_raw, emb, h_wide, turned, c_grouped, c_codes, c_scales = {}, {}, {}, {}, {}, {}, {}
-        mixed = {}
+        mixed, quads = {}, {}
         sorted_chunks = set()
         w1_grouped, acc, planes, a_grouped, a_codes, a_scales, result = {}, {}, {}, {}, {}, {}, {}
 
@@ -104,8 +113,14 @@ def tile_rssmcell_pb_t_kernel(
         def every_second_word(rows):
             return lambda b, u: rows[:, b, :].bitcast(F32)[:, u : KIN // 2 : 2]
 
+        taken = []
+
+        def next_bank(shape, dtype=F32):
+            taken.append(len(taken) % BANKS)
+            return psum.tile(shape, dtype, name="bank", tag="bank_%d" % taken[-1])
+
         def bank_of(tag):
-            return psum.tile([P, 2, HALF], F32, name="bank", tag=tag, bufs=BANKS)
+            return next_bank([P, 2, HALF])
 
         def unload(copy, key, dst):
             copy(out=dst.bitcast(F32), in_=turned[key][:].rearrange("p u n -> p n u"))
@@ -124,8 +139,7 @@ def tile_rssmcell_pb_t_kernel(
         def unload_w1(copy, head, a, g):
             if g == H:
                 w1_grouped[head, a] = work.tile(
-                    [P, CHUNK, PACK], BF16, name="w1_grouped", tag="a_grouped" if (head, a) == (POST, 0) else "w_grouped",
-                    bufs=1 if (head, a) == (POST, 0) else 2, align_bytes=ALIGN)
+                    [P, CHUNK, PACK], BF16, name="w1_grouped", tag=W_TAGS[head, a][0], bufs=W_TAGS[head, a][1], align_bytes=ALIGN)
             unload(copy, ("w", head, a, g), w1_grouped[head, a][:, g * HALF : (g + 1) * HALF])
 
         def quantise_w1(head, a):
@@ -134,7 +148,8 @@ def tile_rssmcell_pb_t_kernel(
 
 
         def load_h(i, pieces=((0, J),)):
-            h_raw[i] = work.tile([P, J, KIN], U8, name="h_raw", tag="h_raw", bufs=CHUNKS, align_bytes=ALIGN)
+            if pieces[0][0] == 0:
+                h_raw[i] = work.tile([P, J, KIN], U8, name="h_raw", tag="h_raw", bufs=CHUNKS, align_bytes=ALIGN)
             rows = h_bytes.rearrange("(p c j) k -> c p j k", p=P, j=J)[i]
             for j0, j1 in pieces:
                 nc.sync.dma_start(out=h_raw[i][:, j0:j1], in_=rows[:, j0:j1])
@@ -148,6 +163,11 @@ def tile_rssmcell_pb_t_kernel(
                 h_wide[i] = work.tile([P, J, KIN], BF16, name="h_wide", tag="h_wide", bufs=WIDE_BUFS, align_bytes=ALIGN)
             nc.scalar.copy(out=h_wide[i][:, j0:j1].rearrange("p j k -> p (j k)"),
                            in_=h_raw[i][:, j0:j1].rearrange("p j k -> p (j k)").bitcast(FP8))
+
+        def widen_on_gpsimd(i, tag, bufs, j1=J):
+            h_wide[i] = work.tile([P, J, KIN], BF16, name="h_wide", tag=tag, bufs=bufs, align_bytes=ALIGN)
+            nc.gpsimd.tensor_copy(out=h_wide[i][:, 0:j1].rearrange("p j k -> p (j k)"),
+                                  in_=h_raw[i][:, 0:j1].rearrange("p j k -> p (j k)").bitcast(FP8))
 
         def widen_sorted(i, j0=0, j1=J):
             if j0 == 0:
@@ -186,36 +206,58 @@ def tile_rssmcell_pb_t_kernel(
             quantise(c_codes[i, g][:], c_scales[i, g][:], c_grouped[i, g][:])
 
 
-        def first(i, head, t):
-            acc[i, head, t] = psum.tile([P, CHUNK], F32, name="bank", tag="bank", bufs=BANKS)
+        def passes(out, i, head, t, n0, n1):
             a, cols = t // 2, slice(t % 2 * P, (t % 2 + 1) * P)
             for g in range(1 + head):
                 nc.tensor.matmul_mx(
-                    out=acc[i, head, t][:],
-                    lhsT=w1_codes[head, a][:, g, cols].bitcast(FP8X4), lhsT_scale=w1_scales[head, a][:, g, cols],
-                    rhs=c_codes[i, g][:].bitcast(FP8X4), rhs_scale=c_scales[i, g][:],
+                    out=out, lhsT=w1_codes[head, a][:, g, cols].bitcast(FP8X4), lhsT_scale=w1_scales[head, a][:, g, cols],
+                    rhs=c_codes[i, g][:, n0:n1].bitcast(FP8X4), rhs_scale=c_scales[i, g][:, n0:n1],
                     start=(g == 0), stop=(g == head))
 
-        def plane(i, head, t):
+        def plane(i, head, t, n0, n1):
             s = i + head
             if s not in planes:
                 planes[s] = work.tile([P, PACK, 2 * CHUNK], BF16, name="planes", tag="planes", bufs=3, align_bytes=ALIGN)
-            return planes[s][:, t, head * CHUNK : (head + 1) * CHUNK]
+            return planes[s][:, t, head * CHUNK + n0 : head * CHUNK + n1]
 
-        def relu(i, head, t):
-            nc.scalar.activation(out=plane(i, head, t), in_=acc[i, head, t][:], func=ACT.Relu, bias=bias1[head][:, t : t + 1])
+        def relu(i, head, t, n0, n1):
+            nc.scalar.activation(out=plane(i, head, t, n0, n1), in_=acc[i, head, t], func=ACT.Relu, bias=bias1[head][:, t : t + 1])
 
-        def relu_on_vector(i, head, t):
+        def relu_on_vector(i, head, t, n0, n1):
             nc.vector.tensor_scalar(
-                out=plane(i, head, t), in0=acc[i, head, t][:], scalar1=bias1[head][:, t : t + 1], scalar2=0.0,
+                out=plane(i, head, t, n0, n1), in0=acc[i, head, t], scalar1=bias1[head][:, t : t + 1], scalar2=0.0,
                 op0=ALU.add, op1=ALU.max)
 
-        def layer1(i, head, tiles=range(PACK), on_vector=()):
-            for t in tiles:
-                first(i, head, t)
-                (relu_on_vector if t in on_vector else relu)(i, head, t)
+        def layer1(i, head, tiles=range(PACK), on_vector=(), n0=0, n1=CHUNK):
+            fit = CHUNK // (n1 - n0)
+            for t0 in tiles[::fit]:
+                bank = next_bank([P, fit, n1 - n0])
+                for t in range(t0, t0 + fit):
+                    acc[i, head, t] = bank[:, t - t0]
+                    passes(acc[i, head, t], i, head, t, n0, n1)
+                for t in range(t0, t0 + fit):
+                    (relu_on_vector if t in on_vector else relu)(i, head, t, n0, n1)
+
+        def quad(i, head, j):
+            quads[i, head, j] = next_bank([P, PACK, P])
+            for t in range(PACK):
+                passes(quads[i, head, j][:, t], i, head, t, j * P, (j + 1) * P)
+
+        def add_quad(i, head, j):
+            n0 = head * CHUNK + j * P
+            nc.vector.tensor_tensor(
+                out=grouped(i + head, n0, n0 + P), in0=quads[i, head, j][:].rearrange("p t n -> p n t"),
+                in1=bias1[head][:].unsqueeze(1).to_broadcast([P, P, PACK]), op=ALU.add)
+
+        def relu_grouped(s, n0, n1):
+            part = grouped(s, n0, n1).rearrange("p n t -> p (n t)")
+            nc.vector.tensor_scalar(out=part, in0=part, scalar1=0.0, scalar2=None, op0=ALU.max)
 
         def grouped(s, n0, n1):
+            if s == 0:
+                if s not in a_grouped:
+                    a_grouped[s] = work.tile([P, CHUNK, PACK], BF16, name="a_grouped", tag=FIRST_TAG[0], bufs=FIRST_TAG[1], align_bytes=ALIGN)
+                return a_grouped[s][:, n0:n1]
             if s >= CHUNKS - 1:
                 head = n0 // CHUNK
                 if (s, head) not in a_grouped:
@@ -239,7 +281,7 @@ def tile_rssmcell_pb_t_kernel(
                 scalar1=1.0, scalar2=0.0, op0=ALU.mult, op1=ALU.add)
 
         def interleave_on_tensor(s, n0):
-            mixed[s, n0] = psum.tile([P, HALF, PACK], BF16, name="mixed", tag="bank", bufs=BANKS)
+            mixed[s, n0] = next_bank([P, HALF, PACK], BF16)
             for m in (0, P):
                 nc.tensor.matmul(
                     out=mixed[s, n0][:, m : m + P].rearrange("p n t -> p t n"), lhsT=ident16[:],
@@ -263,12 +305,12 @@ def tile_rssmcell_pb_t_kernel(
                 rhs=w2_codes[:, head, cols].bitcast(FP8X4), rhs_scale=w2_scales[:, head, cols], start=True, stop=True)
 
         def second(s, head, tag="bank"):
-            result[s, head] = psum.tile([P, J, 2, LAT], F32, name="result", tag=tag, bufs=BANKS)
+            result[s, head] = next_bank([P, J, 2, LAT])
             for j in range(J):
                 pass2(result[s, head][:, j, :, :].rearrange("p h c -> p (h c)"), s, head, j, slice(0, DIST))
 
         def second_half(half, s, tag):
-            result["half", half, s] = psum.tile([P, 2, J, LAT], F32, name="result", tag=tag, bufs=BANKS)
+            result["half", half, s] = next_bank([P, 2, J, LAT])
             for head in HEADS:
                 for j in range(J):
                     pass2(result["half", half, s][:, head, j], s, head, j, slice(half * LAT, (half + 1) * LAT))
@@ -324,13 +366,22 @@ def tile_rssmcell_pb_t_kernel(
                      w1_grouped["w2"][:, 0:HALF])
 
         def spread_bias2():
-            spread = psum.tile([P, 2, 2, LAT], F32, name="spread", tag="bank", bufs=BANKS)
+            spread = next_bank([P, 2, 2, LAT])
             for head in HEADS:
                 nc.tensor.matmul(
                     out=spread[:, head].rearrange("p h c -> p (h c)"),
                     lhsT=bias2_column[:, head : head + 1].to_broadcast([P, P]), rhs=ident[:], start=True, stop=True)
             nc.vector.tensor_copy(out=bias2[:, :, MEAN], in_=spread[:, :, MEAN])
             nc.vector.tensor_scalar(out=bias2[:, :, STD], in0=spread[:, :, STD], scalar1=0.1, scalar2=None, op0=ALU.add)
+
+        def spread_bias16():
+            spread = next_bank([P, 2, 2, LAT])
+            for head in HEADS:
+                nc.tensor.matmul(
+                    out=spread[:, head].rearrange("p h c -> p (h c)"),
+                    lhsT=bias2_raw[head][:].to_broadcast([P, P]), rhs=ident16[:], start=True, stop=True)
+            nc.scalar.copy(out=bias2[:, :, MEAN], in_=spread[:, :, MEAN])
+            nc.scalar.activation(out=bias2[:, :, STD], in_=spread[:, :, STD], func=ACT.Copy, bias=0.1)
 
         with tc.manual_schedule():
             nc.vector.memset(ones[:], 1.0)
@@ -341,18 +392,18 @@ def tile_rssmcell_pb_t_kernel(
             nc.scalar.dma_start(out=bias2_raw[POST][:], in_=bq2.unsqueeze(1))
             nc.scalar.activation(out=exp_tenth[:], in_=ones[:, 0:1], func=ACT.Exp, scale=0.1)
             load_h(0, ((0, 2), (2, J)))
-            for i in (1, 4):
-                load_h(i)
+            load_h(1)
             for a in (0, 1):
                 load_w1(PRIOR, a)
-            for i in (5, 2):
-                load_h(i)
-            nc.sync.dma_start(out=bias1[PRIOR][:], in_=bp1.rearrange("(m t) -> m t", t=PACK))
-            nc.sync.dma_start(out=bias1[POST][:], in_=bq1.rearrange("(m t) -> m t", t=PACK))
+            load_h(4)
             load_embedding(0)
+            nc.sync.dma_start(out=bias1[PRIOR][:], in_=bp1.rearrange("(m t) -> m t", t=PACK))
+            load_h(2)
+            load_h(5)
             load_w1(POST, 0)
             load_h(3)
             load_w1(POST, 1)
+            nc.sync.dma_start(out=bias1[POST][:], in_=bq1.rearrange("(m t) -> m t", t=PACK))
             load_embedding(1)
             load_h(6)
             nc.sync.dma_start(out=w2_rows[:, PRIOR, :], in_=wp2)
@@ -364,42 +415,41 @@ def tile_rssmcell_pb_t_kernel(
             widen_sorted(0, 0, 2)
             widen_sorted(0, 2, 4)
             widen(1)
-            for head in HEADS:
-                nc.vector.tensor_copy(out=bias2_column[:, head : head + 1], in_=bias2_raw[head][:])
             for a in (0, 1):
                 turn_c(0, H, a)
                 scale_h(0, a)
-            spread_bias2()
-            widen(4)
             for a in (0, 1):
                 turn_w1(PRIOR, a, H, "bank")
                 unload_w1(nc.scalar.copy, PRIOR, a, H)
-            widen(5)
+            widen(4)
+            quantise_w1(PRIOR, 0)
             quantise_c(0, H)
-            for a in (0, 1):
-                quantise_w1(PRIOR, a)
+            quantise_w1(PRIOR, 1)
+            widen_on_gpsimd(2, "late_wide", 1, GJ)
             for a in (0, 1):
                 turn_c(1, H, a)
                 scale_h(1, a)
-            layer1(0, PRIOR, (0, 1))
             for a in (0, 1):
                 turn_c(0, E, a)
-                unload_e(nc.scalar.copy, 0, a)
+                unload_e(nc.vector.tensor_copy if a == 1 and E01 else nc.scalar.copy, 0, a)
             load_embedding(EMB_BUFS)
-            layer1(0, PRIOR, (2, 3))
+            if C5:
+                widen(5)
+            layer1(0, PRIOR)
+            if GJ < J:
+                widen(2, GJ, J)
             quantise_c(1, H)
-            widen_sorted(2)
             quantise_c(0, E)
-            (widen_sorted if C3 else widen)(3)
+            widen_sorted(3)
             for g in (H, E):
                 turn_w1(POST, 0, g, "bank")
                 unload_w1(nc.scalar.copy, POST, 0, g)
-            layer1(1, PRIOR, (0, 1))
             for g in (H, E):
                 turn_w1(POST, 1, g, "bank")
                 unload_w1((nc.scalar.copy, nc.vector.tensor_copy)[g * W11], POST, 1, g)
-            layer1(1, PRIOR, (2, 3))
-            widen(6)
+            layer1(1, PRIOR, n0=DIRECT[1] * P)
+            if C6:
+                widen(6)
             for a in (0, 1):
                 turn_c(2, H, a)
             quantise_w1(POST, 0)
@@ -407,27 +457,29 @@ def tile_rssmcell_pb_t_kernel(
             interleave_on_gpsimd(0, 0, CHUNK)
             for a in (0, 1):
                 scale_h(2, a)
-            layer1(0, POST, (0, 1))
+            layer1(0, POST, range(0, 2))
             for a in (0, 1):
                 turn_c(1, E, a)
                 unload_e(nc.vector.tensor_copy if a == 0 and E10 else nc.scalar.copy, 1, a)
             load_embedding(EMB_BUFS + 1)
             turn_w2()
-            layer1(0, POST, (2, 3))
+            layer1(0, POST, range(2, 4))
+            spread_bias16()
             quantise_c(2, H)
             quantise_c(1, E)
             quantise_w2()
             for a in (0, 1):
                 turn_c(3, H, a)
-            widen(7)
             for a in (0, 1):
                 turn_c(2, E, a)
             unload_e(nc.scalar.copy, 2, 0)
             quantise_a(0, ONLY[PRIOR])
-
             last = CHUNKS - 1
             for s in range(1, CHUNKS - 2):
-                interleave_on_gpsimd(s, 0, GPSIMD_SHARE)
+                n0 = DIRECT[s] * P
+                n1 = min(n0 + GP[s], 2 * CHUNK)
+                n2 = max(n1, 2 * CHUNK - SP[s])
+                interleave_on_gpsimd(s, n0, n1)
                 for a in (0, 1):
                     scale_h(s + 2, a)
                 if s == 1:
@@ -435,32 +487,39 @@ def tile_rssmcell_pb_t_kernel(
                     load_embedding(EMB_BUFS + 2)
                 if s > 1:
                     exp(BOTH if s > 2 else ONLY[PRIOR], s - 2, s - 1)
-                layer1(s, POST, (0, 1))
+                layer1(s, POST, range(0, 2))
+                for j in range(DIRECT[s]):
+                    quad(s, PRIOR, j)
+                    add_quad(s, PRIOR, j)
                 for head in HEADS[: min(s, 2)]:
                     layer2(s - 1, head)
-                layer1(s, POST, (2, 3))
-                if SS:
-                    interleave_on_scalar(s, 2 * CHUNK - SS, 2 * CHUNK)
+                if s in CASTS:
+                    widen(CASTS[s])
+                layer1(s, POST, range(2, 4))
+                if n2 < 2 * CHUNK:
+                    interleave_on_scalar(s, n2, 2 * CHUNK)
                 if s + 2 == last:
                     for a in (0, 1):
-                        turn_c(s + 2, E, a)
-                        unload_e(nc.scalar.copy, s + 2, a)
-                layer1(s + 1, PRIOR)
-                interleave(s, GPSIMD_SHARE, 2 * CHUNK - SS)
+                        turn_c(last, E, a)
+                        unload_e(nc.scalar.copy, last, a)
+                layer1(s + 1, PRIOR, n0=DIRECT[s + 1] * P)
+                if n0:
+                    relu_grouped(s, 0, n0)
+                if n1 < n2:
+                    interleave(s, n1, n2)
                 quantise_c(s + 1, E)
                 if s + 2 < last:
                     quantise_a(s)
                     quantise_c(s + 2, H)
-                    for a in (0, 1):
-                        turn_c(s + 2, E, a)
-                        unload_e(nc.scalar.copy, s + 2, a)
-                    for a in (0, 1):
-                        turn_c(s + 3, H, a)
+                    for g in (E, H):
+                        for a in (0, 1):
+                            turn_c(s + 3 - g, g, a)
+                            if g == E:
+                                unload_e(nc.scalar.copy, s + 2, a)
                 else:
                     quantise_c(s + 2, H)
                     quantise_a(s)
                     quantise_c(s + 2, E)
-
             s = last - 1
             interleave_on_gpsimd(s, 0, N6)
             layer1(s, POST, on_vector=VA)

@@ -61,6 +61,7 @@ DIRECT = (0, 2, 2, 0, 0, 0, 0, 0)
 GP = (0, 768, 768, 672, 672, 672)
 SP = (0, 64, 64, 64, 64, 64)
 CASTS = {1: 6, 2: 7}
+WARM = 6
 
 
 def tile_rssmcell_pb_t_kernel(
@@ -374,6 +375,22 @@ def tile_rssmcell_pb_t_kernel(
             nc.vector.tensor_copy(out=bias2[:, :, MEAN], in_=spread[:, :, MEAN])
             nc.vector.tensor_scalar(out=bias2[:, :, STD], in0=spread[:, :, STD], scalar1=0.1, scalar2=None, op0=ALU.add)
 
+        def warm_up(count):
+            idle = work.tile([P, CHUNK], BF16, name="idle", tag="planes", bufs=3, align_bytes=ALIGN)
+            nc.vector.memset(idle[:], 0.0)
+            bank = next_bank([P, CHUNK])
+            for n in range(count):
+                nc.tensor.matmul(out=bank[:], lhsT=idle[:, 0:P], rhs=idle[:], start=True, stop=True)
+
+        def spread_bias32():
+            spread = next_bank([P, 2, 2, LAT])
+            for head in HEADS:
+                nc.tensor.matmul(
+                    out=spread[:, head].rearrange("p h c -> p (h c)"),
+                    lhsT=bias2_column[:, head : head + 1].to_broadcast([P, P]), rhs=ident[:], start=True, stop=True)
+            nc.scalar.copy(out=bias2[:, :, MEAN], in_=spread[:, :, MEAN])
+            nc.scalar.activation(out=bias2[:, :, STD], in_=spread[:, :, STD], func=ACT.Copy, bias=0.1)
+
         def spread_bias16():
             spread = next_bank([P, 2, 2, LAT])
             for head in HEADS:
@@ -412,6 +429,7 @@ def tile_rssmcell_pb_t_kernel(
             for i in range(2, EMB_BUFS):
                 load_embedding(i)
 
+            warm_up(WARM)
             widen_sorted(0, 0, 2)
             widen_sorted(0, 2, 4)
             widen(1)

@@ -36,7 +36,7 @@ MEAN, STD = 0, 1
 H, E = 0, 1
 GPSIMD_SHARE = 672
 C3 = 1
-W11 = 1
+W11 = 0
 E10 = 1
 E21 = 0
 SS = 64
@@ -47,7 +47,7 @@ S7 = 256
 VA = (3,)
 VB = (1, 3)
 VC = (1,)
-LAST_SHARE = 0
+LAST_SHARE = 64
 GATE = 1
 FIRST_TAG = ("a_grouped", 1)
 W_TAGS = {(0, 0): ("w_grouped", 2), (0, 1): ("late_wide", 1), (1, GATE): ("a_grouped", 1), (1, 1 - GATE): ("w_grouped", 2)}
@@ -56,12 +56,18 @@ D6 = 0
 GJ = 4
 E01 = 1
 C5 = 1
-C6 = 0
-DIRECT = (0, 2, 2, 0, 0, 0, 0, 0)
-GP = (0, 768, 768, 672, 672, 672)
+C6 = 1
+DIRECT = (0, 2, 0, 0, 0, 0, 0, 0)
+GP = (0, 768, 640, 640, 640, 640)
 SP = (0, 64, 64, 64, 64, 64)
-CASTS = {1: 6, 2: 7}
-WARM = 6
+CASTS = {1: 7}
+LATE = 5
+S8 = 0
+SPLIT0 = 0
+PAIRS = 0
+T7 = 512
+WARM = 4
+P0 = 4
 
 
 def tile_rssmcell_pb_t_kernel(
@@ -101,7 +107,7 @@ def tile_rssmcell_pb_t_kernel(
         w2_scales = shifted(keep, 2 * DIST, U8, 64, name="w2_scales", tag="w2_scales").rearrange("p (e m) -> p e m", e=2)
 
         h_raw, emb, h_wide, turned, c_grouped, c_codes, c_scales = {}, {}, {}, {}, {}, {}, {}
-        mixed, quads = {}, {}
+        mixed, quads, second_half_wide = {}, {}, []
         sorted_chunks = set()
         w1_grouped, acc, planes, a_grouped, a_codes, a_scales, result = {}, {}, {}, {}, {}, {}, {}
 
@@ -179,8 +185,16 @@ def tile_rssmcell_pb_t_kernel(
                 in0=h_raw[i][:, j0:j1].rearrange("p j k -> p (j k)").bitcast(FP8),
                 scalar1=ones[:, 0:1], scalar2=None, op0=ALU.mult)
 
+        def widen_first():
+            widen_sorted(0, 0, 2)
+            second_half_wide.append(work.tile([P, 2, KIN], BF16, name="h_wide", tag="h_wide", bufs=WIDE_BUFS, align_bytes=ALIGN))
+            nc.scalar.copy(out=second_half_wide[0][:].rearrange("p j k -> p (j k)"),
+                           in_=h_raw[0][:, 2:J].rearrange("p j k -> p (j k)").bitcast(FP8))
+
         def turn_c(i, g, a):
-            if g == H and i in sorted_chunks:
+            if (i, g, a) == (0, H, 1) and second_half_wide:
+                turn((i, g, a), every_second_word(second_half_wide[0][:]), bank_of("bank"))
+            elif g == H and i in sorted_chunks:
                 pairs = h_wide[i][:, :, 2 * a * P : (2 * a + 2) * P].rearrange("p u q e -> p u (q e)").bitcast(F32)
                 turn((i, g, a), lambda b, u: pairs[:, u, b * P : (b + 1) * P], bank_of("bank"))
             else:
@@ -391,6 +405,17 @@ def tile_rssmcell_pb_t_kernel(
             nc.scalar.copy(out=bias2[:, :, MEAN], in_=spread[:, :, MEAN])
             nc.scalar.activation(out=bias2[:, :, STD], in_=spread[:, :, STD], func=ACT.Copy, bias=0.1)
 
+        def spread_early():
+            for head in HEADS:
+                nc.scalar.copy(out=bias2_column[:, head : head + 1], in_=bias2_raw[head][:])
+            spread = next_bank([P, 2, 2, LAT])
+            for head in HEADS:
+                nc.tensor.matmul(
+                    out=spread[:, head].rearrange("p h c -> p (h c)"),
+                    lhsT=bias2_column[:, head : head + 1].to_broadcast([P, P]), rhs=ident[:], start=True, stop=True)
+            nc.scalar.copy(out=bias2[:, :, MEAN], in_=spread[:, :, MEAN])
+            nc.scalar.activation(out=bias2[:, :, STD], in_=spread[:, :, STD], func=ACT.Copy, bias=0.1)
+
         def spread_bias16():
             spread = next_bank([P, 2, 2, LAT])
             for head in HEADS:
@@ -405,8 +430,6 @@ def tile_rssmcell_pb_t_kernel(
             make_identity(nc, ident[:])
             make_identity(nc, ident16[:])
             nc.scalar.dma_start(out=scale[:], in_=h_scale.rearrange("o (p t) -> p (o t)", t=PACK))
-            nc.scalar.dma_start(out=bias2_raw[PRIOR][:], in_=bp2.unsqueeze(1))
-            nc.scalar.dma_start(out=bias2_raw[POST][:], in_=bq2.unsqueeze(1))
             nc.scalar.activation(out=exp_tenth[:], in_=ones[:, 0:1], func=ACT.Exp, scale=0.1)
             load_h(0, ((0, 2), (2, J)))
             load_h(1)
@@ -422,6 +445,8 @@ def tile_rssmcell_pb_t_kernel(
             load_w1(POST, 1)
             nc.sync.dma_start(out=bias1[POST][:], in_=bq1.rearrange("(m t) -> m t", t=PACK))
             load_embedding(1)
+            nc.sync.dma_start(out=bias2_raw[PRIOR][:], in_=bp2.unsqueeze(1))
+            nc.sync.dma_start(out=bias2_raw[POST][:], in_=bq2.unsqueeze(1))
             load_h(6)
             nc.sync.dma_start(out=w2_rows[:, PRIOR, :], in_=wp2)
             nc.sync.dma_start(out=w2_rows[:, POST, :], in_=wq2)
@@ -429,9 +454,13 @@ def tile_rssmcell_pb_t_kernel(
             for i in range(2, EMB_BUFS):
                 load_embedding(i)
 
-            warm_up(WARM)
-            widen_sorted(0, 0, 2)
-            widen_sorted(0, 2, 4)
+            if WARM:
+                warm_up(WARM)
+            if SPLIT0:
+                widen_first()
+            else:
+                widen_sorted(0, 0, 2)
+                widen_sorted(0, 2, 4)
             widen(1)
             for a in (0, 1):
                 turn_c(0, H, a)
@@ -453,15 +482,17 @@ def tile_rssmcell_pb_t_kernel(
             load_embedding(EMB_BUFS)
             if C5:
                 widen(5)
-            layer1(0, PRIOR)
+            layer1(0, PRIOR, range(0, P0))
             if GJ < J:
                 widen(2, GJ, J)
             quantise_c(1, H)
             quantise_c(0, E)
-            widen_sorted(3)
+            (widen_sorted if C3 else widen)(3)
             for g in (H, E):
                 turn_w1(POST, 0, g, "bank")
                 unload_w1(nc.scalar.copy, POST, 0, g)
+            if P0 < PACK:
+                layer1(0, PRIOR, range(P0, PACK))
             for g in (H, E):
                 turn_w1(POST, 1, g, "bank")
                 unload_w1((nc.scalar.copy, nc.vector.tensor_copy)[g * W11], POST, 1, g)
@@ -509,8 +540,12 @@ def tile_rssmcell_pb_t_kernel(
                 for j in range(DIRECT[s]):
                     quad(s, PRIOR, j)
                     add_quad(s, PRIOR, j)
-                for head in HEADS[: min(s, 2)]:
-                    layer2(s - 1, head)
+                if s - 1 >= LATE:
+                    second_half(STD, s - 1, "bank")
+                    add_bias_half(STD, s - 1)
+                else:
+                    for head in HEADS[: min(s, 2)]:
+                        layer2(s - 1, head)
                 if s in CASTS:
                     widen(CASTS[s])
                 layer1(s, POST, range(2, 4))
@@ -597,11 +632,13 @@ def tile_rssmcell_pb_t_kernel(
                     store(head, MEAN, s0 + 2, s + head)
             for pair in range(0, CHUNKS, 2):
                 for head in HEADS:
+                    s0 = pair + head
                     final = pair + 2 == CHUNKS and head == POST
-                    for s in (pair + head, pair + head + 1):
-                        log(ONLY[head], s, s + 1)
-                        std(ONLY[head], s, s + 1)
+                    single = final or (pair == 0 and head == PRIOR) or not PAIRS
+                    for s in (s0, s0 + 1) if single else (s0,):
+                        log(ONLY[head], s, s + (1 if single else 2))
+                        std(ONLY[head], s, s + (1 if single else 2))
                         if final:
                             store(head, STD, s, s + 1)
                     if not final:
-                        store(head, STD, pair + head, pair + head + 2)
+                        store(head, STD, s0, s0 + 2)

@@ -36,7 +36,7 @@ MEAN, STD = 0, 1
 H, E = 0, 1
 GPSIMD_SHARE = 672
 C3 = 1
-W11 = 0
+W11 = 1
 E10 = 1
 E21 = 0
 SS = 64
@@ -59,7 +59,7 @@ C5 = 1
 C6 = 1
 DIRECT = (0, 2, 0, 0, 0, 0, 0, 0)
 GP = (0, 768, 640, 640, 640, 640)
-SP = (0, 64, 64, 64, 64, 64)
+SP = (0, 0, 48, 48, 48, 48)
 CASTS = {1: 7}
 LATE = 5
 S8 = 0
@@ -68,6 +68,8 @@ PAIRS = 0
 T7 = 512
 WARM = 4
 P0 = 4
+G1 = 0
+G1J = 4
 
 
 def tile_rssmcell_pb_t_kernel(
@@ -291,9 +293,7 @@ def tile_rssmcell_pb_t_kernel(
             nc.scalar.copy(out=grouped(s, n0, n1), in_=planes[s][:, :, n0:n1].rearrange("p t n -> p n t"))
 
         def interleave_on_gpsimd(s, n0, n1):
-            nc.gpsimd.tensor_scalar(
-                out=grouped(s, n0, n1), in0=planes[s][:, :, n0:n1].rearrange("p t n -> p n t"),
-                scalar1=1.0, scalar2=0.0, op0=ALU.mult, op1=ALU.add)
+            nc.gpsimd.tensor_copy(out=grouped(s, n0, n1), in_=planes[s][:, :, n0:n1].rearrange("p t n -> p n t"))
 
         def interleave_on_tensor(s, n0):
             mixed[s, n0] = next_bank([P, HALF, PACK], BF16)
@@ -433,13 +433,16 @@ def tile_rssmcell_pb_t_kernel(
             nc.scalar.activation(out=exp_tenth[:], in_=ones[:, 0:1], func=ACT.Exp, scale=0.1)
             load_h(0, ((0, 2), (2, J)))
             load_h(1)
+            if G1:
+                load_h(G1)
             for a in (0, 1):
                 load_w1(PRIOR, a)
             load_h(4)
             load_embedding(0)
             nc.sync.dma_start(out=bias1[PRIOR][:], in_=bp1.rearrange("(m t) -> m t", t=PACK))
             load_h(2)
-            load_h(5)
+            if G1 != 5:
+                load_h(5)
             load_w1(POST, 0)
             load_h(3)
             load_w1(POST, 1)
@@ -462,6 +465,8 @@ def tile_rssmcell_pb_t_kernel(
                 widen_sorted(0, 0, 2)
                 widen_sorted(0, 2, 4)
             widen(1)
+            if G1:
+                widen_on_gpsimd(G1, "h_wide", WIDE_BUFS, G1J)
             for a in (0, 1):
                 turn_c(0, H, a)
                 scale_h(0, a)
@@ -469,8 +474,11 @@ def tile_rssmcell_pb_t_kernel(
                 turn_w1(PRIOR, a, H, "bank")
                 unload_w1(nc.scalar.copy, PRIOR, a, H)
             widen(4)
+            if G1:
+                quantise_c(0, H)
             quantise_w1(PRIOR, 0)
-            quantise_c(0, H)
+            if not G1:
+                quantise_c(0, H)
             quantise_w1(PRIOR, 1)
             widen_on_gpsimd(2, "late_wide", 1, GJ)
             for a in (0, 1):
@@ -480,8 +488,10 @@ def tile_rssmcell_pb_t_kernel(
                 turn_c(0, E, a)
                 unload_e(nc.vector.tensor_copy if a == 1 and E01 else nc.scalar.copy, 0, a)
             load_embedding(EMB_BUFS)
-            if C5:
+            if G1 != 5:
                 widen(5)
+            elif G1J < J:
+                widen(5, G1J, J)
             layer1(0, PRIOR, range(0, P0))
             if GJ < J:
                 widen(2, GJ, J)

@@ -25,51 +25,23 @@ ALU = mybir.AluOpType
 
 ALIGN = 256
 BANKS = 8
-WIDE_BUFS = 6
+WIDE_BUFS = 5
 EMB_BUFS = 5
+CODE_BUFS = 3
+PLANE_BUFS = 3
 A_BUFS = 4
+GPSIMD_SHARE = 640
+SCALAR_SHARE = 48
+END_GPSIMD_SHARE = 576
+END_SCALAR_SHARE = 256
+LAST_SCALAR_SHARE = 64
+END_VECTOR_TILES = ((3,), (1, 3), (1,))
 EXACT_ABOVE = 40.0
 PRIOR, POST = 0, 1
 HEADS = (PRIOR, POST)
 BOTH, ONLY = slice(0, 2), (slice(0, 1), slice(1, 2))
 MEAN, STD = 0, 1
 H, E = 0, 1
-GPSIMD_SHARE = 672
-C3 = 1
-W11 = 1
-E10 = 1
-E21 = 0
-SS = 64
-T8 = 256
-N6 = 576
-L5 = 1
-S7 = 256
-VA = (3,)
-VB = (1, 3)
-VC = (1,)
-LAST_SHARE = 64
-GATE = 1
-FIRST_TAG = ("a_grouped", 1)
-W_TAGS = {(0, 0): ("w_grouped", 2), (0, 1): ("late_wide", 1), (1, GATE): ("a_grouped", 1), (1, 1 - GATE): ("w_grouped", 2)}
-WIDE_BUFS = 5
-D6 = 0
-GJ = 4
-E01 = 1
-C5 = 1
-C6 = 1
-DIRECT = (0, 2, 0, 0, 0, 0, 0, 0)
-GP = (0, 768, 640, 640, 640, 640)
-SP = (0, 0, 48, 48, 48, 48)
-CASTS = {1: 7}
-LATE = 5
-S8 = 0
-SPLIT0 = 0
-PAIRS = 0
-T7 = 512
-WARM = 4
-P0 = 4
-G1 = 0
-G1J = 4
 
 
 def tile_rssmcell_pb_t_kernel(
@@ -86,7 +58,6 @@ def tile_rssmcell_pb_t_kernel(
             return pool.tile([P, skip + columns], dtype, align_bytes=ALIGN, **kw)[:, skip : skip + columns]
 
         bias2_raw = [keep.tile([P, 1], BF16, name="bias2_raw_%d" % e, tag="bias2_raw_%d" % e) for e in HEADS]
-        bias2_column = keep.tile([P, 2], F32, name="bias2_column", tag="bias2_column")
         ones = keep.tile([P, 1], F32, name="ones", tag="ones")
         ident = keep.tile([P, P], F32, name="ident", tag="ident")
         ident16 = keep.tile([P, P], BF16, name="ident16", tag="ident16")
@@ -109,18 +80,9 @@ def tile_rssmcell_pb_t_kernel(
         w2_scales = shifted(keep, 2 * DIST, U8, 64, name="w2_scales", tag="w2_scales").rearrange("p (e m) -> p e m", e=2)
 
         h_raw, emb, h_wide, turned, c_grouped, c_codes, c_scales = {}, {}, {}, {}, {}, {}, {}
-        mixed, quads, second_half_wide = {}, {}, []
+        mixed = {}
         sorted_chunks = set()
         w1_grouped, acc, planes, a_grouped, a_codes, a_scales, result = {}, {}, {}, {}, {}, {}, {}
-
-        def turn(key, words, bank):
-            turned[key] = bank
-            for b in (0, 1):
-                for u in (0, 1):
-                    nc.tensor.transpose(bank[:, u, b * P : (b + 1) * P], words(b, u), ident[:])
-
-        def every_second_word(rows):
-            return lambda b, u: rows[:, b, :].bitcast(F32)[:, u : KIN // 2 : 2]
 
         taken = []
 
@@ -128,8 +90,15 @@ def tile_rssmcell_pb_t_kernel(
             taken.append(len(taken) % BANKS)
             return psum.tile(shape, dtype, name="bank", tag="bank_%d" % taken[-1])
 
-        def bank_of(tag):
-            return next_bank([P, 2, HALF])
+        def turn(key, words):
+            bank = next_bank([P, 2, HALF])
+            turned[key] = bank
+            for b in (0, 1):
+                for u in (0, 1):
+                    nc.tensor.transpose(bank[:, u, b * P : (b + 1) * P], words(b, u), ident[:])
+
+        def every_second_word(rows):
+            return lambda b, u: rows[:, b, :].bitcast(F32)[:, u : KIN // 2 : 2]
 
         def unload(copy, key, dst):
             copy(out=dst.bitcast(F32), in_=turned[key][:].rearrange("p u n -> p n u"))
@@ -142,13 +111,13 @@ def tile_rssmcell_pb_t_kernel(
             rows = (wp1, wq1)[head].rearrange("(m t) k -> m t k", t=PACK)
             nc.sync.dma_start(out=w1_rows[head, a][:], in_=rows[:, 2 * a : 2 * a + 2])
 
-        def turn_w1(head, a, g, tag):
-            turn(("w", head, a, g), every_second_word(w1_rows[head, a][:, :, g * KIN : (g + 1) * KIN]), bank_of(tag))
+        def turn_w1(head, a, g):
+            turn(("w", head, a, g), every_second_word(w1_rows[head, a][:, :, g * KIN : (g + 1) * KIN]))
 
         def unload_w1(copy, head, a, g):
             if g == H:
-                w1_grouped[head, a] = work.tile(
-                    [P, CHUNK, PACK], BF16, name="w1_grouped", tag=W_TAGS[head, a][0], bufs=W_TAGS[head, a][1], align_bytes=ALIGN)
+                tag, bufs = (("w_grouped", 2), (("gpsimd_wide", "a_grouped")[head], 1))[a]
+                w1_grouped[head, a] = work.tile([P, CHUNK, PACK], BF16, name="w1_grouped", tag=tag, bufs=bufs, align_bytes=ALIGN)
             unload(copy, ("w", head, a, g), w1_grouped[head, a][:, g * HALF : (g + 1) * HALF])
 
         def quantise_w1(head, a):
@@ -157,8 +126,7 @@ def tile_rssmcell_pb_t_kernel(
 
 
         def load_h(i, pieces=((0, J),)):
-            if pieces[0][0] == 0:
-                h_raw[i] = work.tile([P, J, KIN], U8, name="h_raw", tag="h_raw", bufs=CHUNKS, align_bytes=ALIGN)
+            h_raw[i] = work.tile([P, J, KIN], U8, name="h_raw", tag="h_raw", bufs=CHUNKS, align_bytes=ALIGN)
             rows = h_bytes.rearrange("(p c j) k -> c p j k", p=P, j=J)[i]
             for j0, j1 in pieces:
                 nc.sync.dma_start(out=h_raw[i][:, j0:j1], in_=rows[:, j0:j1])
@@ -167,16 +135,16 @@ def tile_rssmcell_pb_t_kernel(
             emb[i] = work.tile([P, J, KIN], BF16, name="emb", tag="emb", bufs=EMB_BUFS)
             nc.sync.dma_start(out=emb[i][:], in_=embedding.rearrange("(p c j) k -> c p j k", p=P, j=J)[i])
 
-        def widen(i, j0=0, j1=J):
-            if j0 == 0:
-                h_wide[i] = work.tile([P, J, KIN], BF16, name="h_wide", tag="h_wide", bufs=WIDE_BUFS, align_bytes=ALIGN)
-            nc.scalar.copy(out=h_wide[i][:, j0:j1].rearrange("p j k -> p (j k)"),
-                           in_=h_raw[i][:, j0:j1].rearrange("p j k -> p (j k)").bitcast(FP8))
+        def raw_values(i, j0=0, j1=J):
+            return h_raw[i][:, j0:j1].rearrange("p j k -> p (j k)").bitcast(FP8)
 
-        def widen_on_gpsimd(i, tag, bufs, j1=J):
-            h_wide[i] = work.tile([P, J, KIN], BF16, name="h_wide", tag=tag, bufs=bufs, align_bytes=ALIGN)
-            nc.gpsimd.tensor_copy(out=h_wide[i][:, 0:j1].rearrange("p j k -> p (j k)"),
-                                  in_=h_raw[i][:, 0:j1].rearrange("p j k -> p (j k)").bitcast(FP8))
+        def widen(i):
+            h_wide[i] = work.tile([P, J, KIN], BF16, name="h_wide", tag="h_wide", bufs=WIDE_BUFS, align_bytes=ALIGN)
+            nc.scalar.copy(out=h_wide[i][:].rearrange("p j k -> p (j k)"), in_=raw_values(i))
+
+        def widen_on_gpsimd(i):
+            h_wide[i] = work.tile([P, J, KIN], BF16, name="h_wide", tag="gpsimd_wide", bufs=1, align_bytes=ALIGN)
+            nc.gpsimd.tensor_copy(out=h_wide[i][:].rearrange("p j k -> p (j k)"), in_=raw_values(i))
 
         def widen_sorted(i, j0=0, j1=J):
             if j0 == 0:
@@ -184,23 +152,14 @@ def tile_rssmcell_pb_t_kernel(
                 sorted_chunks.add(i)
             nc.vector.tensor_scalar(
                 out=h_wide[i][:, :, j0 * P : j1 * P].rearrange("p u q e -> p q u e"),
-                in0=h_raw[i][:, j0:j1].rearrange("p j k -> p (j k)").bitcast(FP8),
-                scalar1=ones[:, 0:1], scalar2=None, op0=ALU.mult)
-
-        def widen_first():
-            widen_sorted(0, 0, 2)
-            second_half_wide.append(work.tile([P, 2, KIN], BF16, name="h_wide", tag="h_wide", bufs=WIDE_BUFS, align_bytes=ALIGN))
-            nc.scalar.copy(out=second_half_wide[0][:].rearrange("p j k -> p (j k)"),
-                           in_=h_raw[0][:, 2:J].rearrange("p j k -> p (j k)").bitcast(FP8))
+                in0=raw_values(i, j0, j1), scalar1=ones[:, 0:1], scalar2=None, op0=ALU.mult)
 
         def turn_c(i, g, a):
-            if (i, g, a) == (0, H, 1) and second_half_wide:
-                turn((i, g, a), every_second_word(second_half_wide[0][:]), bank_of("bank"))
-            elif g == H and i in sorted_chunks:
+            if g == H and i in sorted_chunks:
                 pairs = h_wide[i][:, :, 2 * a * P : (2 * a + 2) * P].rearrange("p u q e -> p u (q e)").bitcast(F32)
-                turn((i, g, a), lambda b, u: pairs[:, u, b * P : (b + 1) * P], bank_of("bank"))
+                turn((i, g, a), lambda b, u: pairs[:, u, b * P : (b + 1) * P])
             else:
-                turn((i, g, a), every_second_word((h_wide, emb)[g][i][:, 2 * a : 2 * a + 2]), bank_of("bank"))
+                turn((i, g, a), every_second_word((h_wide, emb)[g][i][:, 2 * a : 2 * a + 2]))
 
         def grouped_half(i, g, a):
             if a == 0:
@@ -218,8 +177,8 @@ def tile_rssmcell_pb_t_kernel(
             unload(copy, (i, E, a), grouped_half(i, E, a))
 
         def quantise_c(i, g):
-            c_codes[i, g] = shifted(work, CHUNK, U32, 32, name="c_codes", tag="c_codes_%d" % g, bufs=3)
-            c_scales[i, g] = shifted(work, CHUNK, U8, 192, name="c_scales", tag="c_scales_%d" % g, bufs=3)
+            c_codes[i, g] = shifted(work, CHUNK, U32, 32, name="c_codes", tag="c_codes_%d" % g, bufs=CODE_BUFS)
+            c_scales[i, g] = shifted(work, CHUNK, U8, 192, name="c_scales", tag="c_scales_%d" % g, bufs=CODE_BUFS)
             quantise(c_codes[i, g][:], c_scales[i, g][:], c_grouped[i, g][:])
 
 
@@ -234,7 +193,7 @@ def tile_rssmcell_pb_t_kernel(
         def plane(i, head, t, n0, n1):
             s = i + head
             if s not in planes:
-                planes[s] = work.tile([P, PACK, 2 * CHUNK], BF16, name="planes", tag="planes", bufs=3, align_bytes=ALIGN)
+                planes[s] = work.tile([P, PACK, 2 * CHUNK], BF16, name="planes", tag="planes", bufs=PLANE_BUFS, align_bytes=ALIGN)
             return planes[s][:, t, head * CHUNK + n0 : head * CHUNK + n1]
 
         def relu(i, head, t, n0, n1):
@@ -245,7 +204,8 @@ def tile_rssmcell_pb_t_kernel(
                 out=plane(i, head, t, n0, n1), in0=acc[i, head, t], scalar1=bias1[head][:, t : t + 1], scalar2=0.0,
                 op0=ALU.add, op1=ALU.max)
 
-        def layer1(i, head, tiles=range(PACK), on_vector=(), n0=0, n1=CHUNK):
+        def layer1(i, head, tiles=range(PACK), on_vector=(), n0=0):
+            n1 = CHUNK
             fit = CHUNK // (n1 - n0)
             for t0 in tiles[::fit]:
                 bank = next_bank([P, fit, n1 - n0])
@@ -255,15 +215,13 @@ def tile_rssmcell_pb_t_kernel(
                 for t in range(t0, t0 + fit):
                     (relu_on_vector if t in on_vector else relu)(i, head, t, n0, n1)
 
-        def quad(i, head, j):
-            quads[i, head, j] = next_bank([P, PACK, P])
+        def layer1_grouped(i, head, j):
+            bank = next_bank([P, PACK, P])
             for t in range(PACK):
-                passes(quads[i, head, j][:, t], i, head, t, j * P, (j + 1) * P)
-
-        def add_quad(i, head, j):
+                passes(bank[:, t], i, head, t, j * P, (j + 1) * P)
             n0 = head * CHUNK + j * P
             nc.vector.tensor_tensor(
-                out=grouped(i + head, n0, n0 + P), in0=quads[i, head, j][:].rearrange("p t n -> p n t"),
+                out=grouped(i + head, n0, n0 + P), in0=bank[:].rearrange("p t n -> p n t"),
                 in1=bias1[head][:].unsqueeze(1).to_broadcast([P, P, PACK]), op=ALU.add)
 
         def relu_grouped(s, n0, n1):
@@ -271,17 +229,14 @@ def tile_rssmcell_pb_t_kernel(
             nc.vector.tensor_scalar(out=part, in0=part, scalar1=0.0, scalar2=None, op0=ALU.max)
 
         def grouped(s, n0, n1):
-            if s == 0:
-                if s not in a_grouped:
-                    a_grouped[s] = work.tile([P, CHUNK, PACK], BF16, name="a_grouped", tag=FIRST_TAG[0], bufs=FIRST_TAG[1], align_bytes=ALIGN)
-                return a_grouped[s][:, n0:n1]
             if s >= CHUNKS - 1:
                 head = n0 // CHUNK
                 if (s, head) not in a_grouped:
                     a_grouped[s, head] = work.tile([P, CHUNK, PACK], BF16, name="a_grouped", tag="c_grouped_%d" % head, bufs=2, align_bytes=ALIGN)
                 return a_grouped[s, head][:, n0 - head * CHUNK : n1 - head * CHUNK]
             if s not in a_grouped:
-                a_grouped[s] = work.tile([P, 2 * CHUNK, PACK], BF16, name="a_grouped", tag="a_grouped", bufs=1, align_bytes=ALIGN)
+                columns = 2 * CHUNK if s else CHUNK
+                a_grouped[s] = work.tile([P, columns, PACK], BF16, name="a_grouped", tag="a_grouped", bufs=1, align_bytes=ALIGN)
             return a_grouped[s][:, n0:n1]
 
         def interleave(s, n0, n1):
@@ -319,12 +274,12 @@ def tile_rssmcell_pb_t_kernel(
                 out=out, lhsT=a_codes[s][:, tokens].bitcast(FP8X4), lhsT_scale=a_scales[s][:, tokens],
                 rhs=w2_codes[:, head, cols].bitcast(FP8X4), rhs_scale=w2_scales[:, head, cols], start=True, stop=True)
 
-        def second(s, head, tag="bank"):
+        def second(s, head):
             result[s, head] = next_bank([P, J, 2, LAT])
             for j in range(J):
                 pass2(result[s, head][:, j, :, :].rearrange("p h c -> p (h c)"), s, head, j, slice(0, DIST))
 
-        def second_half(half, s, tag):
+        def second_half(half, s):
             result["half", half, s] = next_bank([P, 2, J, LAT])
             for head in HEADS:
                 for j in range(J):
@@ -372,7 +327,7 @@ def tile_rssmcell_pb_t_kernel(
                 op0=ALU.min, op1=ALU.max)
 
         def turn_w2():
-            turn("w2", every_second_word(w2_rows[:]), bank_of("bank"))
+            turn("w2", every_second_word(w2_rows[:]))
             w1_grouped["w2"] = work.tile([P, CHUNK, PACK], BF16, name="w2_grouped", tag="w_grouped", bufs=2, align_bytes=ALIGN)
             unload(nc.scalar.copy, "w2", w1_grouped["w2"][:, 0:HALF])
 
@@ -385,45 +340,19 @@ def tile_rssmcell_pb_t_kernel(
             for head in HEADS:
                 nc.tensor.matmul(
                     out=spread[:, head].rearrange("p h c -> p (h c)"),
-                    lhsT=bias2_column[:, head : head + 1].to_broadcast([P, P]), rhs=ident[:], start=True, stop=True)
-            nc.vector.tensor_copy(out=bias2[:, :, MEAN], in_=spread[:, :, MEAN])
-            nc.vector.tensor_scalar(out=bias2[:, :, STD], in0=spread[:, :, STD], scalar1=0.1, scalar2=None, op0=ALU.add)
-
-        def warm_up(count):
-            idle = work.tile([P, CHUNK], BF16, name="idle", tag="planes", bufs=3, align_bytes=ALIGN)
-            nc.vector.memset(idle[:], 0.0)
-            bank = next_bank([P, CHUNK])
-            for n in range(count):
-                nc.tensor.matmul(out=bank[:], lhsT=idle[:, 0:P], rhs=idle[:], start=True, stop=True)
-
-        def spread_bias32():
-            spread = next_bank([P, 2, 2, LAT])
-            for head in HEADS:
-                nc.tensor.matmul(
-                    out=spread[:, head].rearrange("p h c -> p (h c)"),
-                    lhsT=bias2_column[:, head : head + 1].to_broadcast([P, P]), rhs=ident[:], start=True, stop=True)
-            nc.scalar.copy(out=bias2[:, :, MEAN], in_=spread[:, :, MEAN])
-            nc.scalar.activation(out=bias2[:, :, STD], in_=spread[:, :, STD], func=ACT.Copy, bias=0.1)
-
-        def spread_early():
-            for head in HEADS:
-                nc.scalar.copy(out=bias2_column[:, head : head + 1], in_=bias2_raw[head][:])
-            spread = next_bank([P, 2, 2, LAT])
-            for head in HEADS:
-                nc.tensor.matmul(
-                    out=spread[:, head].rearrange("p h c -> p (h c)"),
-                    lhsT=bias2_column[:, head : head + 1].to_broadcast([P, P]), rhs=ident[:], start=True, stop=True)
-            nc.scalar.copy(out=bias2[:, :, MEAN], in_=spread[:, :, MEAN])
-            nc.scalar.activation(out=bias2[:, :, STD], in_=spread[:, :, STD], func=ACT.Copy, bias=0.1)
-
-        def spread_bias16():
-            spread = next_bank([P, 2, 2, LAT])
-            for head in HEADS:
-                nc.tensor.matmul(
-                    out=spread[:, head].rearrange("p h c -> p (h c)"),
                     lhsT=bias2_raw[head][:].to_broadcast([P, P]), rhs=ident16[:], start=True, stop=True)
             nc.scalar.copy(out=bias2[:, :, MEAN], in_=spread[:, :, MEAN])
             nc.scalar.activation(out=bias2[:, :, STD], in_=spread[:, :, STD], func=ACT.Copy, bias=0.1)
+
+        def turn_and_scale(i):
+            for a in (0, 1):
+                turn_c(i, H, a)
+                scale_h(i, a)
+
+        def turn_embedding(i, copies=(nc.scalar.copy, nc.scalar.copy)):
+            for a in (0, 1):
+                turn_c(i, E, a)
+                unload_e(copies[a], i, a)
 
         with tc.manual_schedule():
             nc.vector.memset(ones[:], 1.0)
@@ -433,16 +362,13 @@ def tile_rssmcell_pb_t_kernel(
             nc.scalar.activation(out=exp_tenth[:], in_=ones[:, 0:1], func=ACT.Exp, scale=0.1)
             load_h(0, ((0, 2), (2, J)))
             load_h(1)
-            if G1:
-                load_h(G1)
             for a in (0, 1):
                 load_w1(PRIOR, a)
             load_h(4)
             load_embedding(0)
             nc.sync.dma_start(out=bias1[PRIOR][:], in_=bp1.rearrange("(m t) -> m t", t=PACK))
             load_h(2)
-            if G1 != 5:
-                load_h(5)
+            load_h(5)
             load_w1(POST, 0)
             load_h(3)
             load_w1(POST, 1)
@@ -457,73 +383,45 @@ def tile_rssmcell_pb_t_kernel(
             for i in range(2, EMB_BUFS):
                 load_embedding(i)
 
-            if WARM:
-                warm_up(WARM)
-            if SPLIT0:
-                widen_first()
-            else:
-                widen_sorted(0, 0, 2)
-                widen_sorted(0, 2, 4)
+            widen_sorted(0, 0, 2)
+            widen_sorted(0, 2, J)
             widen(1)
-            if G1:
-                widen_on_gpsimd(G1, "h_wide", WIDE_BUFS, G1J)
+            turn_and_scale(0)
             for a in (0, 1):
-                turn_c(0, H, a)
-                scale_h(0, a)
-            for a in (0, 1):
-                turn_w1(PRIOR, a, H, "bank")
+                turn_w1(PRIOR, a, H)
                 unload_w1(nc.scalar.copy, PRIOR, a, H)
             widen(4)
-            if G1:
-                quantise_c(0, H)
             quantise_w1(PRIOR, 0)
-            if not G1:
-                quantise_c(0, H)
+            quantise_c(0, H)
             quantise_w1(PRIOR, 1)
-            widen_on_gpsimd(2, "late_wide", 1, GJ)
-            for a in (0, 1):
-                turn_c(1, H, a)
-                scale_h(1, a)
-            for a in (0, 1):
-                turn_c(0, E, a)
-                unload_e(nc.vector.tensor_copy if a == 1 and E01 else nc.scalar.copy, 0, a)
+            widen_on_gpsimd(2)
+            turn_and_scale(1)
+            turn_embedding(0, (nc.scalar.copy, nc.vector.tensor_copy))
             load_embedding(EMB_BUFS)
-            if G1 != 5:
-                widen(5)
-            elif G1J < J:
-                widen(5, G1J, J)
-            layer1(0, PRIOR, range(0, P0))
-            if GJ < J:
-                widen(2, GJ, J)
+            widen(5)
+            layer1(0, PRIOR)
             quantise_c(1, H)
             quantise_c(0, E)
-            (widen_sorted if C3 else widen)(3)
-            for g in (H, E):
-                turn_w1(POST, 0, g, "bank")
-                unload_w1(nc.scalar.copy, POST, 0, g)
-            if P0 < PACK:
-                layer1(0, PRIOR, range(P0, PACK))
-            for g in (H, E):
-                turn_w1(POST, 1, g, "bank")
-                unload_w1((nc.scalar.copy, nc.vector.tensor_copy)[g * W11], POST, 1, g)
-            layer1(1, PRIOR, n0=DIRECT[1] * P)
-            if C6:
-                widen(6)
+            widen_sorted(3)
+            for a in (0, 1):
+                for g in (H, E):
+                    turn_w1(POST, a, g)
+                    unload_w1(nc.vector.tensor_copy if (a, g) == (1, E) else nc.scalar.copy, POST, a, g)
+            layer1(1, PRIOR, n0=HALF)
+            widen(6)
             for a in (0, 1):
                 turn_c(2, H, a)
-            quantise_w1(POST, 0)
-            quantise_w1(POST, 1)
+            for a in (0, 1):
+                quantise_w1(POST, a)
             interleave_on_gpsimd(0, 0, CHUNK)
             for a in (0, 1):
                 scale_h(2, a)
             layer1(0, POST, range(0, 2))
-            for a in (0, 1):
-                turn_c(1, E, a)
-                unload_e(nc.vector.tensor_copy if a == 0 and E10 else nc.scalar.copy, 1, a)
+            turn_embedding(1, (nc.vector.tensor_copy, nc.scalar.copy))
             load_embedding(EMB_BUFS + 1)
             turn_w2()
-            layer1(0, POST, range(2, 4))
-            spread_bias16()
+            layer1(0, POST, range(2, PACK))
+            spread_bias2()
             quantise_c(2, H)
             quantise_c(1, E)
             quantise_w2()
@@ -533,122 +431,105 @@ def tile_rssmcell_pb_t_kernel(
                 turn_c(2, E, a)
             unload_e(nc.scalar.copy, 2, 0)
             quantise_a(0, ONLY[PRIOR])
+
             last = CHUNKS - 1
-            for s in range(1, CHUNKS - 2):
-                n0 = DIRECT[s] * P
-                n1 = min(n0 + GP[s], 2 * CHUNK)
-                n2 = max(n1, 2 * CHUNK - SP[s])
-                interleave_on_gpsimd(s, n0, n1)
+            for s in range(1, last - 1):
+                first_step, final_step = s == 1, s + 2 == last
+                if first_step:
+                    interleave_on_gpsimd(s, HALF, 2 * CHUNK)
+                else:
+                    interleave_on_gpsimd(s, 0, GPSIMD_SHARE)
                 for a in (0, 1):
                     scale_h(s + 2, a)
-                if s == 1:
-                    unload_e(nc.vector.tensor_copy if E21 else nc.scalar.copy, 2, 1)
+                if first_step:
+                    unload_e(nc.scalar.copy, 2, 1)
                     load_embedding(EMB_BUFS + 2)
-                if s > 1:
+                else:
                     exp(BOTH if s > 2 else ONLY[PRIOR], s - 2, s - 1)
                 layer1(s, POST, range(0, 2))
-                for j in range(DIRECT[s]):
-                    quad(s, PRIOR, j)
-                    add_quad(s, PRIOR, j)
-                if s - 1 >= LATE:
-                    second_half(STD, s - 1, "bank")
-                    add_bias_half(STD, s - 1)
+                if first_step:
+                    for j in (0, 1):
+                        layer1_grouped(s, PRIOR, j)
+                    layer2(0, PRIOR)
+                    widen(last)
                 else:
-                    for head in HEADS[: min(s, 2)]:
+                    for head in HEADS:
                         layer2(s - 1, head)
-                if s in CASTS:
-                    widen(CASTS[s])
-                layer1(s, POST, range(2, 4))
-                if n2 < 2 * CHUNK:
-                    interleave_on_scalar(s, n2, 2 * CHUNK)
-                if s + 2 == last:
-                    for a in (0, 1):
-                        turn_c(last, E, a)
-                        unload_e(nc.scalar.copy, last, a)
-                layer1(s + 1, PRIOR, n0=DIRECT[s + 1] * P)
-                if n0:
-                    relu_grouped(s, 0, n0)
-                if n1 < n2:
-                    interleave(s, n1, n2)
-                quantise_c(s + 1, E)
-                if s + 2 < last:
-                    quantise_a(s)
-                    quantise_c(s + 2, H)
-                    for g in (E, H):
-                        for a in (0, 1):
-                            turn_c(s + 3 - g, g, a)
-                            if g == E:
-                                unload_e(nc.scalar.copy, s + 2, a)
+                layer1(s, POST, range(2, PACK))
+                if not first_step:
+                    interleave_on_scalar(s, 2 * CHUNK - SCALAR_SHARE, 2 * CHUNK)
+                if final_step:
+                    turn_embedding(last)
+                layer1(s + 1, PRIOR)
+                if first_step:
+                    relu_grouped(s, 0, HALF)
                 else:
-                    quantise_c(s + 2, H)
+                    interleave(s, GPSIMD_SHARE, 2 * CHUNK - SCALAR_SHARE)
+                quantise_c(s + 1, E)
+                if final_step:
+                    quantise_c(last, H)
                     quantise_a(s)
-                    quantise_c(s + 2, E)
-            s = last - 1
-            interleave_on_gpsimd(s, 0, N6)
-            layer1(s, POST, on_vector=VA)
-            if L5:
-                second_half(STD, s - 1, "bank")
-                add_bias_half(STD, s - 1)
-            else:
-                for head in HEADS:
-                    layer2(s - 1, head)
-            layer1(last, PRIOR, on_vector=VB)
-            layer1(last, POST, on_vector=VC)
-            interleave(s, N6, 2 * CHUNK)
+                    quantise_c(last, E)
+                else:
+                    quantise_a(s)
+                    quantise_c(s + 2, H)
+                    turn_embedding(s + 2)
+                    for a in (0, 1):
+                        turn_c(s + 3, H, a)
+
+            g6, g7, g8 = last - 1, last, CHUNKS
+            late = g6 - 1
+            interleave_on_gpsimd(g6, 0, END_GPSIMD_SHARE)
+            layer1(last - 1, POST, on_vector=END_VECTOR_TILES[0])
+            second_half(STD, late)
+            add_bias_half(STD, late)
+            layer1(last, PRIOR, on_vector=END_VECTOR_TILES[1])
+            layer1(last, POST, on_vector=END_VECTOR_TILES[2])
+            interleave(g6, END_GPSIMD_SHARE, 2 * CHUNK)
             for n0 in (CHUNK, CHUNK + HALF):
-                interleave_on_tensor(last, n0)
-            for n0 in range(2 * CHUNK - T8, 2 * CHUNK, HALF):
-                interleave_on_tensor(CHUNKS, n0)
-            if S7:
-                interleave_on_scalar(last, CHUNK - S7, CHUNK)
+                interleave_on_tensor(g7, n0)
+            interleave_on_tensor(g8, CHUNK + HALF)
+            interleave_on_scalar(g7, CHUNK - END_SCALAR_SHARE, CHUNK)
             for n0 in (CHUNK, CHUNK + HALF):
-                unload_mixed(last, n0)
-            interleave(last, 0, CHUNK - S7)
-            quantise_a(s)
-            quantise_a(last, ONLY[PRIOR])
+                unload_mixed(g7, n0)
+            interleave(g7, 0, CHUNK - END_SCALAR_SHARE)
+            quantise_a(g6)
+            quantise_a(g7, ONLY[PRIOR])
             for head in HEADS:
-                second(s, head)
-            second(last, PRIOR)
-            s = CHUNKS
-            if LAST_SHARE:
-                interleave_on_scalar(s, 2 * CHUNK - T8 - LAST_SHARE, 2 * CHUNK - T8)
-            for n0 in range(2 * CHUNK - T8, 2 * CHUNK, HALF):
-                unload_mixed(CHUNKS, n0)
-            exp(BOTH, s - 4, s - 2)
-            if T8 + LAST_SHARE < CHUNK:
-                interleave(s, CHUNK, 2 * CHUNK - T8 - LAST_SHARE)
-            quantise_a(last, ONLY[POST])
-            second(last, POST)
-            add_bias(s - 2, PRIOR, (STD,))
-            quantise_a(s, ONLY[POST])
-            add_bias(s - 2, POST, (STD,))
-            exp(BOTH, s - 2, last)
-            second(s, POST)
-            second_half(MEAN, s - 3, "bank")
+                second(g6, head)
+            second(g7, PRIOR)
+            interleave_on_scalar(g8, CHUNK + HALF - LAST_SCALAR_SHARE, CHUNK + HALF)
+            unload_mixed(g8, CHUNK + HALF)
+            exp(BOTH, late - 1, g6)
+            interleave(g8, CHUNK, CHUNK + HALF - LAST_SCALAR_SHARE)
+            quantise_a(g7, ONLY[POST])
+            second(g7, POST)
+            add_bias(g6, PRIOR, (STD,))
+            quantise_a(g8, ONLY[POST])
+            add_bias(g6, POST, (STD,))
+            exp(BOTH, g6, g7)
+            second(g8, POST)
+            second_half(MEAN, late)
             for head in HEADS:
-                add_bias(last, head, (STD,))
-                exp(ONLY[head], last, s)
-            add_bias(s, POST, (STD,))
-            exp(ONLY[POST], s, s + 1)
-            s0 = last - 2 if L5 else last - 1
-            if L5:
-                add_bias_half(MEAN, s0)
+                add_bias(g7, head, (STD,))
+                exp(ONLY[head], g7, g8)
+            add_bias(g8, POST, (STD,))
+            exp(ONLY[POST], g8, g8 + 1)
+
+            add_bias_half(MEAN, late)
             for head in HEADS:
-                for late in range(last - 1, s + head):
-                    add_bias(late, head, (MEAN,))
-                    if late == s0 + 1:
-                        store(head, MEAN, s0, s0 + 2)
-                if s0 + 2 < s + head:
-                    store(head, MEAN, s0 + 2, s + head)
+                add_bias(g6, head, (MEAN,))
+                store(head, MEAN, late, g7)
+                for s in range(g7, g8 + head):
+                    add_bias(s, head, (MEAN,))
+                store(head, MEAN, g7, g8 + head)
             for pair in range(0, CHUNKS, 2):
                 for head in HEADS:
-                    s0 = pair + head
                     final = pair + 2 == CHUNKS and head == POST
-                    single = final or (pair == 0 and head == PRIOR) or not PAIRS
-                    for s in (s0, s0 + 1) if single else (s0,):
-                        log(ONLY[head], s, s + (1 if single else 2))
-                        std(ONLY[head], s, s + (1 if single else 2))
+                    for s in (pair + head, pair + head + 1):
+                        log(ONLY[head], s, s + 1)
+                        std(ONLY[head], s, s + 1)
                         if final:
                             store(head, STD, s, s + 1)
                     if not final:
-                        store(head, STD, s0, s0 + 2)
+                        store(head, STD, pair + head, pair + head + 2)

@@ -139,8 +139,10 @@ def tile_rssmcell_pb_t_kernel(
             return h_raw[i][:, j0:j1].rearrange("p j k -> p (j k)").bitcast(FP8)
 
         def widen(i):
-            h_wide[i] = work.tile([P, J, KIN], BF16, name="h_wide", tag="h_wide", bufs=WIDE_BUFS, align_bytes=ALIGN)
-            nc.scalar.copy(out=h_wide[i][:].rearrange("p j k -> p (j k)"), in_=raw_values(i))
+            h_wide[i] = work.tile([P, 2, J * P, 2], BF16, name="h_wide", tag="h_wide", bufs=WIDE_BUFS, align_bytes=ALIGN)
+            sorted_chunks.add(i)
+            nc.scalar.copy(out=h_wide[i][:].rearrange("p u q e -> p (u q e)"),
+                           in_=raw_values(i).rearrange("p (q u e) -> p u q e", u=2, e=2))
 
         def widen_on_gpsimd(i):
             h_wide[i] = work.tile([P, J, KIN], BF16, name="h_wide", tag="gpsimd_wide", bufs=1, align_bytes=ALIGN)

@@ -23,25 +23,24 @@ FP8X4 = mybir.dt.float8_e4m3fn_x4
 ACT = mybir.ActivationFunctionType
 ALU = mybir.AluOpType
 
-ALIGN = 256
+ALIGN = 64
 BANKS = 8
-WIDE_BUFS = 5
-EMB_BUFS = 5
-CODE_BUFS = 3
-PLANE_BUFS = 3
-A_BUFS = 4
-GPSIMD_SHARE = 640
-SCALAR_SHARE = 48
-END_GPSIMD_SHARE = 576
-END_SCALAR_SHARE = 256
-LAST_SCALAR_SHARE = 64
-END_VECTOR_TILES = ((3,), (1, 3), (1,))
 EXACT_ABOVE = 40.0
 PRIOR, POST = 0, 1
 HEADS = (PRIOR, POST)
 BOTH, ONLY = slice(0, 2), (slice(0, 1), slice(1, 2))
 MEAN, STD = 0, 1
 H, E = 0, 1
+GPSIMD_SHARE = 640
+SCALAR_SHARE = 48
+FINAL_SHARE = 736
+G6_FROM = 0
+
+WIDE_BUFS = 5
+PAIR_BUFS = 3
+EMB_BUFS = 5
+PLANE_BUFS = 3
+A_BUFS = 4
 
 
 def tile_rssmcell_pb_t_kernel(
@@ -53,9 +52,6 @@ def tile_rssmcell_pb_t_kernel(
         keep = ctx.enter_context(tc.tile_pool(name="keep", bufs=1))
         work = ctx.enter_context(tc.tile_pool(name="work", bufs=2))
         psum = ctx.enter_context(tc.psum_pool(name="psum", bufs=1))
-
-        def shifted(pool, columns, dtype, skip, **kw):
-            return pool.tile([P, skip + columns], dtype, align_bytes=ALIGN, **kw)[:, skip : skip + columns]
 
         bias2_raw = [keep.tile([P, 1], BF16, name="bias2_raw_%d" % e, tag="bias2_raw_%d" % e) for e in HEADS]
         ones = keep.tile([P, 1], F32, name="ones", tag="ones")
@@ -71,24 +67,22 @@ def tile_rssmcell_pb_t_kernel(
                 name = "w1_%d_%d" % (head, a)
                 w1_rows[head, a] = keep.tile([P, 2, (1 + head) * KIN], BF16, name=name, tag=name)
                 w1_codes[head, a] = keep.tile([P, 1 + head, HALF], U32, name=name + "c", tag=name + "c", align_bytes=ALIGN)
-                w1_scales[head, a] = shifted(keep, (1 + head) * HALF, U8, 64, name=name + "s", tag=name + "s").rearrange(
-                    "p (g m) -> p g m", m=HALF)
+                w1_scales[head, a] = keep.tile([P, 1 + head, HALF], U8, name=name + "s", tag=name + "s", align_bytes=ALIGN)
         w2_rows = keep.tile([P, 2, HID], BF16, name="w2_rows", tag="w2_rows")
         value = keep.tile([P, 2, 2, GROUPS * J, LAT], F32, name="value", tag="value")
         soft = keep.tile([P, 2, GROUPS * J * LAT], F32, name="soft", tag="soft")
-        w2_codes = shifted(keep, 2 * DIST, U32, 32, name="w2_codes", tag="w2_codes").rearrange("p (e m) -> p e m", e=2)
-        w2_scales = shifted(keep, 2 * DIST, U8, 64, name="w2_scales", tag="w2_scales").rearrange("p (e m) -> p e m", e=2)
+        w2_codes = keep.tile([P, 2, DIST], U32, name="w2_codes", tag="w2_codes", align_bytes=ALIGN)
+        w2_scales = keep.tile([P, 2, DIST], U8, name="w2_scales", tag="w2_scales", align_bytes=ALIGN)
 
         h_raw, emb, h_wide, turned, c_grouped, c_codes, c_scales = {}, {}, {}, {}, {}, {}, {}
-        mixed = {}
-        sorted_chunks = set()
-        w1_grouped, acc, planes, a_grouped, a_codes, a_scales, result = {}, {}, {}, {}, {}, {}, {}
+        mixed, w1_grouped, acc, planes, a_grouped, a_codes, a_scales, result = {}, {}, {}, {}, {}, {}, {}, {}
 
-        taken = []
+        ring = list(range(BANKS))
+        pairs, plain_chunks = {}, set()
 
         def next_bank(shape, dtype=F32):
-            taken.append(len(taken) % BANKS)
-            return psum.tile(shape, dtype, name="bank", tag="bank_%d" % taken[-1])
+            ring.append(ring.pop(0))
+            return psum.tile(shape, dtype, name="bank", tag="bank_%d" % ring[-1])
 
         def turn(key, words):
             bank = next_bank([P, 2, HALF])
@@ -105,6 +99,8 @@ def tile_rssmcell_pb_t_kernel(
 
         def quantise(codes, scales, grouped):
             nc.vector.quantize_mx(out=codes.bitcast(FP8X4), scales=scales, in_=grouped.rearrange("p n t -> p (n t)"))
+
+        on_scalar, on_vector = nc.scalar.copy, nc.vector.tensor_copy
 
 
         def load_w1(head, a):
@@ -138,33 +134,33 @@ def tile_rssmcell_pb_t_kernel(
         def raw_values(i, j0=0, j1=J):
             return h_raw[i][:, j0:j1].rearrange("p j k -> p (j k)").bitcast(FP8)
 
-        def widen(i):
-            h_wide[i] = work.tile([P, 2, J * P, 2], BF16, name="h_wide", tag="h_wide", bufs=WIDE_BUFS, align_bytes=ALIGN)
-            sorted_chunks.add(i)
-            nc.scalar.copy(out=h_wide[i][:].rearrange("p u q e -> p (u q e)"),
-                           in_=raw_values(i).rearrange("p (q u e) -> p u q e", u=2, e=2))
+        def wide(i):
+            if i not in h_wide:
+                h_wide[i] = work.tile([P, 2, J * P, 2], BF16, name="h_wide", tag="h_wide", bufs=WIDE_BUFS, align_bytes=ALIGN)
+            return h_wide[i]
+
+        def widen(i, j0=0, j1=J):
+            nc.scalar.copy(out=wide(i)[:, :, j0 * P : j1 * P], in_=raw_values(i, j0, j1).rearrange("p (q u e) -> p u q e", u=2, e=2))
+
+        def widen_on_vector(i, j0=0, j1=J):
+            nc.vector.tensor_scalar(
+                out=wide(i)[:, :, j0 * P : j1 * P].rearrange("p u q e -> p q u e"),
+                in0=raw_values(i, j0, j1), scalar1=ones[:, 0:1], scalar2=None, op0=ALU.mult)
 
         def widen_on_gpsimd(i):
             h_wide[i] = work.tile([P, J, KIN], BF16, name="h_wide", tag="gpsimd_wide", bufs=1, align_bytes=ALIGN)
+            plain_chunks.add(i)
             nc.gpsimd.tensor_copy(out=h_wide[i][:].rearrange("p j k -> p (j k)"), in_=raw_values(i))
 
-        def widen_sorted(i, j0=0, j1=J):
-            if j0 == 0:
-                h_wide[i] = work.tile([P, 2, J * P, 2], BF16, name="h_wide", tag="h_wide", bufs=WIDE_BUFS, align_bytes=ALIGN)
-                sorted_chunks.add(i)
-            nc.vector.tensor_scalar(
-                out=h_wide[i][:, :, j0 * P : j1 * P].rearrange("p u q e -> p q u e"),
-                in0=raw_values(i, j0, j1), scalar1=ones[:, 0:1], scalar2=None, op0=ALU.mult)
-
         def turn_c(i, g, a):
-            if g == H and i in sorted_chunks:
-                pairs = h_wide[i][:, :, 2 * a * P : (2 * a + 2) * P].rearrange("p u q e -> p u (q e)").bitcast(F32)
-                turn((i, g, a), lambda b, u: pairs[:, u, b * P : (b + 1) * P])
+            if g == H and i not in plain_chunks:
+                words = h_wide[i][:, :, 2 * a * P : (2 * a + 2) * P].rearrange("p u q e -> p u (q e)").bitcast(F32)
+                turn((i, g, a), lambda b, u: words[:, u, b * P : (b + 1) * P])
             else:
                 turn((i, g, a), every_second_word((h_wide, emb)[g][i][:, 2 * a : 2 * a + 2]))
 
         def grouped_half(i, g, a):
-            if a == 0:
+            if (i, g) not in c_grouped:
                 c_grouped[i, g] = work.tile([P, CHUNK, PACK], BF16, name="c_grouped", tag="c_grouped_%d" % g, bufs=2, align_bytes=ALIGN)
             return c_grouped[i, g][:, a * HALF : (a + 1) * HALF]
 
@@ -179,8 +175,8 @@ def tile_rssmcell_pb_t_kernel(
             unload(copy, (i, E, a), grouped_half(i, E, a))
 
         def quantise_c(i, g):
-            c_codes[i, g] = shifted(work, CHUNK, U32, 32, name="c_codes", tag="c_codes_%d" % g, bufs=CODE_BUFS)
-            c_scales[i, g] = shifted(work, CHUNK, U8, 192, name="c_scales", tag="c_scales_%d" % g, bufs=CODE_BUFS)
+            c_codes[i, g] = work.tile([P, CHUNK], U32, name="c_codes", tag="c_codes_%d" % g, bufs=3 - g, align_bytes=ALIGN)
+            c_scales[i, g] = work.tile([P, CHUNK], U8, name="c_scales", tag="c_scales_%d" % g, bufs=3 - g, align_bytes=ALIGN)
             quantise(c_codes[i, g][:], c_scales[i, g][:], c_grouped[i, g][:])
 
 
@@ -206,8 +202,7 @@ def tile_rssmcell_pb_t_kernel(
                 out=plane(i, head, t, n0, n1), in0=acc[i, head, t], scalar1=bias1[head][:, t : t + 1], scalar2=0.0,
                 op0=ALU.add, op1=ALU.max)
 
-        def layer1(i, head, tiles=range(PACK), on_vector=(), n0=0):
-            n1 = CHUNK
+        def layer1(i, head, tiles=range(PACK), vector_tiles=(), n0=0, n1=CHUNK):
             fit = CHUNK // (n1 - n0)
             for t0 in tiles[::fit]:
                 bank = next_bank([P, fit, n1 - n0])
@@ -215,20 +210,23 @@ def tile_rssmcell_pb_t_kernel(
                     acc[i, head, t] = bank[:, t - t0]
                     passes(acc[i, head, t], i, head, t, n0, n1)
                 for t in range(t0, t0 + fit):
-                    (relu_on_vector if t in on_vector else relu)(i, head, t, n0, n1)
+                    (relu_on_vector if t in vector_tiles else relu)(i, head, t, n0, n1)
 
-        def layer1_grouped(i, head, j):
-            bank = next_bank([P, PACK, P])
-            for t in range(PACK):
-                passes(bank[:, t], i, head, t, j * P, (j + 1) * P)
-            n0 = head * CHUNK + j * P
-            nc.vector.tensor_tensor(
-                out=grouped(i + head, n0, n0 + P), in0=bank[:].rearrange("p t n -> p n t"),
-                in1=bias1[head][:].unsqueeze(1).to_broadcast([P, P, PACK]), op=ALU.add)
+        def layer1_pairs(i, head, a):
+            pairs[i + head, head, a] = work.tile([P, 2, HALF, 2], BF16, name="pairs", tag="pairs", bufs=PAIR_BUFS, align_bytes=ALIGN)
+            for u in (0, 1):
+                bank = next_bank([P, 2, HALF])
+                for e in (0, 1):
+                    passes(bank[:, e], i, head, 2 * u + e, a * HALF, (a + 1) * HALF)
+                nc.vector.tensor_tensor(
+                    out=pairs[i + head, head, a][:, u], in0=bank[:].rearrange("p e n -> p n e"),
+                    in1=bias1[head][:, 2 * u : 2 * u + 2].unsqueeze(1).to_broadcast([P, HALF, 2]), op=ALU.add)
 
-        def relu_grouped(s, n0, n1):
-            part = grouped(s, n0, n1).rearrange("p n t -> p (n t)")
-            nc.vector.tensor_scalar(out=part, in0=part, scalar1=0.0, scalar2=None, op0=ALU.max)
+        def relu_pairs(s, head, a):
+            n0 = head * CHUNK + a * HALF
+            nc.vector.tensor_scalar(
+                out=grouped(s, n0, n0 + HALF).rearrange("p n (u e) -> p n u e", u=2),
+                in0=pairs[s, head, a][:].rearrange("p u n e -> p n u e"), scalar1=0.0, scalar2=None, op0=ALU.max)
 
         def grouped(s, n0, n1):
             if s >= CHUNKS - 1:
@@ -252,15 +250,15 @@ def tile_rssmcell_pb_t_kernel(
         def interleave_on_gpsimd(s, n0, n1):
             nc.gpsimd.tensor_copy(out=grouped(s, n0, n1), in_=planes[s][:, :, n0:n1].rearrange("p t n -> p n t"))
 
-        def interleave_on_tensor(s, n0):
-            mixed[s, n0] = next_bank([P, HALF, PACK], BF16)
-            for m in (0, P):
+        def mix(s, n0, n1):
+            mixed[s, n0] = next_bank([P, n1 - n0, PACK], BF16)
+            for m in range(0, n1 - n0, P):
                 nc.tensor.matmul(
                     out=mixed[s, n0][:, m : m + P].rearrange("p n t -> p t n"), lhsT=ident16[:],
                     rhs=planes[s][:, :, n0 + m : n0 + m + P], start=True, stop=True)
 
-        def unload_mixed(s, n0):
-            nc.scalar.copy(out=grouped(s, n0, n0 + HALF).bitcast(F32), in_=mixed[s, n0][:].bitcast(F32))
+        def unload_mixed(copy, s, n0, n1):
+            copy(out=grouped(s, n0, n1).bitcast(F32), in_=mixed[s, n0][:].bitcast(F32))
 
         def quantise_a(s, heads=BOTH):
             if s not in a_codes:
@@ -298,7 +296,7 @@ def tile_rssmcell_pb_t_kernel(
                 out=dst.rearrange("(p n) d -> p n d", p=P)[:, (s0 - head) * J : (s1 - head) * J],
                 in_=value[:, head, half, s0 * J : s1 * J])
 
-        def add_bias(s, head, halves):
+        def add_bias(s, head, halves=(MEAN, STD)):
             part = slice(halves[0], halves[-1] + 1)
             nc.vector.tensor_tensor(
                 out=value[:, head, part, s * J : (s + 1) * J].rearrange("p h j c -> p j h c"),
@@ -308,7 +306,7 @@ def tile_rssmcell_pb_t_kernel(
 
         def layer2(s, head):
             second(s, head)
-            add_bias(s, head, (MEAN, STD))
+            add_bias(s, head)
             store(head, MEAN, s, s + 1)
 
         def w_of(heads, s0, s1):
@@ -331,27 +329,27 @@ def tile_rssmcell_pb_t_kernel(
         def turn_w2():
             turn("w2", every_second_word(w2_rows[:]))
             w1_grouped["w2"] = work.tile([P, CHUNK, PACK], BF16, name="w2_grouped", tag="w_grouped", bufs=2, align_bytes=ALIGN)
-            unload(nc.scalar.copy, "w2", w1_grouped["w2"][:, 0:HALF])
+            unload(on_scalar, "w2", w1_grouped["w2"][:, 0:HALF])
 
         def quantise_w2():
             quantise(w2_codes[:].rearrange("p e m -> p (e m)"), w2_scales[:].rearrange("p e m -> p (e m)"),
                      w1_grouped["w2"][:, 0:HALF])
 
         def spread_bias2():
-            spread = next_bank([P, 2, 2, LAT])
+            both = next_bank([P, 2, 2, LAT])
             for head in HEADS:
                 nc.tensor.matmul(
-                    out=spread[:, head].rearrange("p h c -> p (h c)"),
+                    out=both[:, head].rearrange("p h c -> p (h c)"),
                     lhsT=bias2_raw[head][:].to_broadcast([P, P]), rhs=ident16[:], start=True, stop=True)
-            nc.scalar.copy(out=bias2[:, :, MEAN], in_=spread[:, :, MEAN])
-            nc.scalar.activation(out=bias2[:, :, STD], in_=spread[:, :, STD], func=ACT.Copy, bias=0.1)
+            nc.scalar.copy(out=bias2[:, :, MEAN], in_=both[:, :, MEAN])
+            nc.scalar.activation(out=bias2[:, :, STD], in_=both[:, :, STD], func=ACT.Copy, bias=0.1)
 
         def turn_and_scale(i):
             for a in (0, 1):
                 turn_c(i, H, a)
                 scale_h(i, a)
 
-        def turn_embedding(i, copies=(nc.scalar.copy, nc.scalar.copy)):
+        def turn_embedding(i, copies=(on_scalar, on_scalar)):
             for a in (0, 1):
                 turn_c(i, E, a)
                 unload_e(copies[a], i, a)
@@ -366,64 +364,65 @@ def tile_rssmcell_pb_t_kernel(
             load_h(1)
             for a in (0, 1):
                 load_w1(PRIOR, a)
-            load_h(4)
+            load_h(2)
             load_embedding(0)
             nc.sync.dma_start(out=bias1[PRIOR][:], in_=bp1.rearrange("(m t) -> m t", t=PACK))
-            load_h(2)
             load_h(5)
+            load_h(4)
             load_w1(POST, 0)
             load_h(3)
             load_w1(POST, 1)
             nc.sync.dma_start(out=bias1[POST][:], in_=bq1.rearrange("(m t) -> m t", t=PACK))
+            nc.sync.dma_start(out=w2_rows[:, PRIOR, :], in_=wp2)
+            nc.sync.dma_start(out=w2_rows[:, POST, :], in_=wq2)
             load_embedding(1)
             nc.sync.dma_start(out=bias2_raw[PRIOR][:], in_=bp2.unsqueeze(1))
             nc.sync.dma_start(out=bias2_raw[POST][:], in_=bq2.unsqueeze(1))
             load_h(6)
-            nc.sync.dma_start(out=w2_rows[:, PRIOR, :], in_=wp2)
-            nc.sync.dma_start(out=w2_rows[:, POST, :], in_=wq2)
             load_h(7)
             for i in range(2, EMB_BUFS):
                 load_embedding(i)
 
-            widen_sorted(0, 0, 2)
-            widen_sorted(0, 2, J)
+            widen_on_vector(0, 0, 2)
+            widen_on_vector(0, 2, J)
             widen(1)
             turn_and_scale(0)
             for a in (0, 1):
                 turn_w1(PRIOR, a, H)
-                unload_w1(nc.scalar.copy, PRIOR, a, H)
-            widen(4)
+                unload_w1(on_scalar, PRIOR, a, H)
+            widen(2)
             quantise_w1(PRIOR, 0)
             quantise_c(0, H)
             quantise_w1(PRIOR, 1)
-            widen_on_gpsimd(2)
+            widen_on_gpsimd(5)
             turn_and_scale(1)
-            turn_embedding(0, (nc.scalar.copy, nc.vector.tensor_copy))
+            turn_embedding(0, (on_scalar, on_vector))
             load_embedding(EMB_BUFS)
-            widen(5)
+            widen(4)
             layer1(0, PRIOR)
             quantise_c(1, H)
             quantise_c(0, E)
-            widen_sorted(3)
+            widen_on_vector(3)
             for a in (0, 1):
                 for g in (H, E):
                     turn_w1(POST, a, g)
-                    unload_w1(nc.vector.tensor_copy if (a, g) == (1, E) else nc.scalar.copy, POST, a, g)
+                    unload_w1(on_vector if (a, g) == (1, E) else on_scalar, POST, a, g)
             layer1(1, PRIOR, n0=HALF)
-            widen(6)
             for a in (0, 1):
                 turn_c(2, H, a)
+            turn_w2()
+            widen(6)
             for a in (0, 1):
                 quantise_w1(POST, a)
             interleave_on_gpsimd(0, 0, CHUNK)
             for a in (0, 1):
                 scale_h(2, a)
             layer1(0, POST, range(0, 2))
-            turn_embedding(1, (nc.vector.tensor_copy, nc.scalar.copy))
+            turn_embedding(1, (on_vector, on_vector))
             load_embedding(EMB_BUFS + 1)
-            turn_w2()
             layer1(0, POST, range(2, PACK))
             spread_bias2()
+            widen(CHUNKS - 1)
             quantise_c(2, H)
             quantise_c(1, E)
             quantise_w2()
@@ -431,43 +430,51 @@ def tile_rssmcell_pb_t_kernel(
                 turn_c(3, H, a)
             for a in (0, 1):
                 turn_c(2, E, a)
-            unload_e(nc.scalar.copy, 2, 0)
+            unload_e(on_scalar, 2, 0)
+            layer1(1, POST)
             quantise_a(0, ONLY[PRIOR])
 
             last = CHUNKS - 1
             for s in range(1, last - 1):
                 first_step, final_step = s == 1, s + 2 == last
+                n1 = FINAL_SHARE if final_step else GPSIMD_SHARE
+                n2 = 2 * CHUNK - (0 if final_step else SCALAR_SHARE)
                 if first_step:
                     interleave_on_gpsimd(s, HALF, 2 * CHUNK)
                 else:
-                    interleave_on_gpsimd(s, 0, GPSIMD_SHARE)
+                    interleave_on_gpsimd(s, 0, n1)
                 for a in (0, 1):
                     scale_h(s + 2, a)
                 if first_step:
-                    unload_e(nc.scalar.copy, 2, 1)
+                    unload_e(on_vector, 2, 1)
                     load_embedding(EMB_BUFS + 2)
                 else:
                     exp(BOTH if s > 2 else ONLY[PRIOR], s - 2, s - 1)
-                layer1(s, POST, range(0, 2))
+                if not first_step:
+                    layer1(s, POST, range(0, 2))
                 if first_step:
-                    for j in (0, 1):
-                        layer1_grouped(s, PRIOR, j)
+                    layer1_pairs(s, PRIOR, 0)
                     layer2(0, PRIOR)
-                    widen(last)
+                elif final_step:
+                    for head in HEADS:
+                        layer2(s - 1, head)
+                    turn_embedding(last, (on_vector, on_scalar))
                 else:
                     for head in HEADS:
                         layer2(s - 1, head)
-                layer1(s, POST, range(2, PACK))
                 if not first_step:
-                    interleave_on_scalar(s, 2 * CHUNK - SCALAR_SHARE, 2 * CHUNK)
-                if final_step:
-                    turn_embedding(last)
+                    layer1(s, POST, range(2, PACK))
+                if not first_step and not final_step:
+                    interleave_on_scalar(s, n2, 2 * CHUNK)
                 layer1(s + 1, PRIOR)
                 if first_step:
-                    relu_grouped(s, 0, HALF)
-                else:
-                    interleave(s, GPSIMD_SHARE, 2 * CHUNK - SCALAR_SHARE)
-                quantise_c(s + 1, E)
+                    relu_pairs(s, PRIOR, 0)
+                if final_step:
+                    quantise_c(s + 1, E)
+                if not first_step:
+                    interleave(s, n1, n2)
+                if not final_step:
+                    quantise_c(s + 1, E)
                 if final_step:
                     quantise_c(last, H)
                     quantise_a(s)
@@ -481,29 +488,29 @@ def tile_rssmcell_pb_t_kernel(
 
             g6, g7, g8 = last - 1, last, CHUNKS
             late = g6 - 1
-            interleave_on_gpsimd(g6, 0, END_GPSIMD_SHARE)
-            layer1(last - 1, POST, on_vector=END_VECTOR_TILES[0])
+            interleave_on_gpsimd(g6, 0, 576)
+            layer1(last - 1, POST, vector_tiles=(3,))
+            layer1(last, PRIOR, vector_tiles=(1, 3))
             second_half(STD, late)
             add_bias_half(STD, late)
-            layer1(last, PRIOR, on_vector=END_VECTOR_TILES[1])
-            layer1(last, POST, on_vector=END_VECTOR_TILES[2])
-            interleave(g6, END_GPSIMD_SHARE, 2 * CHUNK)
+            layer1(last, POST, vector_tiles=(1,))
+            interleave(g6, 576, 2 * CHUNK)
             for n0 in (CHUNK, CHUNK + HALF):
-                interleave_on_tensor(g7, n0)
-            interleave_on_tensor(g8, CHUNK + HALF)
-            interleave_on_scalar(g7, CHUNK - END_SCALAR_SHARE, CHUNK)
+                mix(g7, n0, n0 + HALF)
+            mix(g8, CHUNK + HALF, 2 * CHUNK)
+            interleave_on_scalar(g7, CHUNK - 256, CHUNK)
             for n0 in (CHUNK, CHUNK + HALF):
-                unload_mixed(g7, n0)
-            interleave(g7, 0, CHUNK - END_SCALAR_SHARE)
+                unload_mixed(on_scalar, g7, n0, n0 + HALF)
+            interleave(g7, 0, CHUNK - 256)
             quantise_a(g6)
             quantise_a(g7, ONLY[PRIOR])
             for head in HEADS:
                 second(g6, head)
             second(g7, PRIOR)
-            interleave_on_scalar(g8, CHUNK + HALF - LAST_SCALAR_SHARE, CHUNK + HALF)
-            unload_mixed(g8, CHUNK + HALF)
+            interleave_on_scalar(g8, CHUNK + HALF - 64, CHUNK + HALF)
+            unload_mixed(on_scalar, g8, CHUNK + HALF, 2 * CHUNK)
             exp(BOTH, late - 1, g6)
-            interleave(g8, CHUNK, CHUNK + HALF - LAST_SCALAR_SHARE)
+            interleave(g8, CHUNK, CHUNK + HALF - 64)
             quantise_a(g7, ONLY[POST])
             second(g7, POST)
             add_bias(g6, PRIOR, (STD,))

@@ -31,10 +31,10 @@ HEADS = (PRIOR, POST)
 BOTH, ONLY = slice(0, 2), (slice(0, 1), slice(1, 2))
 MEAN, STD = 0, 1
 H, E = 0, 1
-GPSIMD_SHARE = 640
-SCALAR_SHARE = 48
-FINAL_SHARE = 736
-G6_FROM = 0
+GPSIMD_SHARE = 624
+SCALAR_SHARE = 112
+FINAL_SHARE = 704
+TENSOR_SHARE = 0
 
 WIDE_BUFS = 5
 PAIR_BUFS = 3
@@ -136,16 +136,19 @@ def tile_rssmcell_pb_t_kernel(
 
         def wide(i):
             if i not in h_wide:
-                h_wide[i] = work.tile([P, 2, J * P, 2], BF16, name="h_wide", tag="h_wide", bufs=WIDE_BUFS, align_bytes=ALIGN)
+                h_wide[i] = work.tile([P, 2, 2, HALF, 2], BF16, name="h_wide", tag="h_wide", bufs=WIDE_BUFS, align_bytes=ALIGN)
             return h_wide[i]
 
-        def widen(i, j0=0, j1=J):
-            nc.scalar.copy(out=wide(i)[:, :, j0 * P : j1 * P], in_=raw_values(i, j0, j1).rearrange("p (q u e) -> p u q e", u=2, e=2))
+        def widen(i, a0=0, a1=2):
+            nc.scalar.copy(out=wide(i)[:, a0:a1].rearrange("p a u q e -> p (a u q e)"),
+                           in_=raw_values(i, 2 * a0, 2 * a1).rearrange("p (a q u e) -> p a u q e", q=HALF, u=2, e=2))
 
         def widen_on_vector(i, j0=0, j1=J):
-            nc.vector.tensor_scalar(
-                out=wide(i)[:, :, j0 * P : j1 * P].rearrange("p u q e -> p q u e"),
-                in0=raw_values(i, j0, j1), scalar1=ones[:, 0:1], scalar2=None, op0=ALU.mult)
+            if j1 - j0 == 1:
+                out = wide(i)[:, j0 // 2, :, j0 % 2 * P : (j0 % 2 + 1) * P].rearrange("p u q e -> p q u e")
+            else:
+                out = wide(i)[:, j0 // 2 : j1 // 2].rearrange("p a u q e -> p a q u e")
+            nc.vector.tensor_copy(out=out, in_=raw_values(i, j0, j1))
 
         def widen_on_gpsimd(i):
             h_wide[i] = work.tile([P, J, KIN], BF16, name="h_wide", tag="gpsimd_wide", bufs=1, align_bytes=ALIGN)
@@ -154,7 +157,7 @@ def tile_rssmcell_pb_t_kernel(
 
         def turn_c(i, g, a):
             if g == H and i not in plain_chunks:
-                words = h_wide[i][:, :, 2 * a * P : (2 * a + 2) * P].rearrange("p u q e -> p u (q e)").bitcast(F32)
+                words = h_wide[i][:, a].rearrange("p u q e -> p u (q e)").bitcast(F32)
                 turn((i, g, a), lambda b, u: words[:, u, b * P : (b + 1) * P])
             else:
                 turn((i, g, a), every_second_word((h_wide, emb)[g][i][:, 2 * a : 2 * a + 2]))
@@ -360,7 +363,7 @@ def tile_rssmcell_pb_t_kernel(
             make_identity(nc, ident16[:])
             nc.scalar.dma_start(out=scale[:], in_=h_scale.rearrange("o (p t) -> p (o t)", t=PACK))
             nc.scalar.activation(out=exp_tenth[:], in_=ones[:, 0:1], func=ACT.Exp, scale=0.1)
-            load_h(0, ((0, 2), (2, J)))
+            load_h(0, ((0, 1), (1, 2), (2, J)))
             load_h(1)
             for a in (0, 1):
                 load_w1(PRIOR, a)
@@ -383,8 +386,9 @@ def tile_rssmcell_pb_t_kernel(
             for i in range(2, EMB_BUFS):
                 load_embedding(i)
 
-            widen_on_vector(0, 0, 2)
-            widen_on_vector(0, 2, J)
+            widen_on_vector(0, 0, 1)
+            widen_on_vector(0, 1, 2)
+            widen(0, 1, 2)
             widen(1)
             turn_and_scale(0)
             for a in (0, 1):
@@ -431,6 +435,7 @@ def tile_rssmcell_pb_t_kernel(
             for a in (0, 1):
                 turn_c(2, E, a)
             unload_e(on_scalar, 2, 0)
+            unload_e(on_scalar, 2, 1)
             layer1(1, POST)
             quantise_a(0, ONLY[PRIOR])
 
@@ -438,7 +443,8 @@ def tile_rssmcell_pb_t_kernel(
             for s in range(1, last - 1):
                 first_step, final_step = s == 1, s + 2 == last
                 n1 = FINAL_SHARE if final_step else GPSIMD_SHARE
-                n2 = 2 * CHUNK - (0 if final_step else SCALAR_SHARE)
+                n3 = 2 * CHUNK - (0 if first_step else TENSOR_SHARE)
+                n2 = n3 - (0 if final_step else SCALAR_SHARE)
                 if first_step:
                     interleave_on_gpsimd(s, HALF, 2 * CHUNK)
                 else:
@@ -446,12 +452,14 @@ def tile_rssmcell_pb_t_kernel(
                 for a in (0, 1):
                     scale_h(s + 2, a)
                 if first_step:
-                    unload_e(on_vector, 2, 1)
                     load_embedding(EMB_BUFS + 2)
                 else:
                     exp(BOTH if s > 2 else ONLY[PRIOR], s - 2, s - 1)
                 if not first_step:
                     layer1(s, POST, range(0, 2))
+                if n3 < 2 * CHUNK:
+                    mix(s, n3, 2 * CHUNK)
+                    unload_mixed(on_scalar, s, n3, 2 * CHUNK)
                 if first_step:
                     layer1_pairs(s, PRIOR, 0)
                     layer2(0, PRIOR)
@@ -464,8 +472,8 @@ def tile_rssmcell_pb_t_kernel(
                         layer2(s - 1, head)
                 if not first_step:
                     layer1(s, POST, range(2, PACK))
-                if not first_step and not final_step:
-                    interleave_on_scalar(s, n2, 2 * CHUNK)
+                if not first_step and n2 < n3:
+                    interleave_on_scalar(s, n2, n3)
                 layer1(s + 1, PRIOR)
                 if first_step:
                     relu_pairs(s, PRIOR, 0)
@@ -488,13 +496,13 @@ def tile_rssmcell_pb_t_kernel(
 
             g6, g7, g8 = last - 1, last, CHUNKS
             late = g6 - 1
-            interleave_on_gpsimd(g6, 0, 576)
+            interleave_on_gpsimd(g6, 0, 544)
             layer1(last - 1, POST, vector_tiles=(3,))
             layer1(last, PRIOR, vector_tiles=(1, 3))
             second_half(STD, late)
             add_bias_half(STD, late)
             layer1(last, POST, vector_tiles=(1,))
-            interleave(g6, 576, 2 * CHUNK)
+            interleave(g6, 544, 2 * CHUNK)
             for n0 in (CHUNK, CHUNK + HALF):
                 mix(g7, n0, n0 + HALF)
             mix(g8, CHUNK + HALF, 2 * CHUNK)

from contextlib import ExitStack

import concourse.mybir as mybir
from concourse.masks import make_identity

B, KIN, HID, DIST, LAT = 4096, 512, 512, 128, 64
FLOPS = 2 * B * (HID * KIN + HID * 2 * KIN + 2 * DIST * HID)

P = 128
J = 4
PACK = 4
CHUNK = P * J
CHUNKS = B // CHUNK
GROUPS = CHUNKS + 1
HALF = CHUNK // 2

F32 = mybir.dt.float32
BF16 = mybir.dt.bfloat16
U32 = mybir.dt.uint32
U8 = mybir.dt.uint8
FP8 = mybir.dt.float8_e4m3fn
FP8X4 = mybir.dt.float8_e4m3fn_x4
ACT = mybir.ActivationFunctionType
ALU = mybir.AluOpType

ALIGN = 64
BANKS = 8
EXACT_ABOVE = 40.0
PRIOR, POST = 0, 1
HEADS = (PRIOR, POST)
BOTH, ONLY = slice(0, 2), (slice(0, 1), slice(1, 2))
MEAN, STD = 0, 1
H, E = 0, 1
GPSIMD_SHARE = 624
SCALAR_SHARE = 112
FINAL_SHARE = 704
TENSOR_SHARE = 0

WIDE_BUFS = 5
PAIR_BUFS = 3
EMB_BUFS = 5
PLANE_BUFS = 3
A_BUFS = 4


def tile_rssmcell_pb_t_kernel(
    tc, h_bytes, h_scale, embedding, wp1, bp1, wp2, bp2, wq1, bq1, wq2, bq2,
    post_mean, post_std, prior_mean, prior_std,
):
    nc = tc.nc
    with ExitStack() as ctx:
        keep = ctx.enter_context(tc.tile_pool(name="keep", bufs=1))
        work = ctx.enter_context(tc.tile_pool(name="work", bufs=2))
        psum = ctx.enter_context(tc.psum_pool(name="psum", bufs=1))

        bias2_raw = [keep.tile([P, 1], BF16, name="bias2_raw_%d" % e, tag="bias2_raw_%d" % e) for e in HEADS]
        ones = keep.tile([P, 1], F32, name="ones", tag="ones")
        ident = keep.tile([P, P], F32, name="ident", tag="ident")
        ident16 = keep.tile([P, P], BF16, name="ident16", tag="ident16")
        scale = keep.tile([P, PACK], F32, name="scale", tag="scale")
        bias1 = [keep.tile([P, PACK], BF16, name="bias1_%d" % e, tag="bias1_%d" % e) for e in HEADS]
        bias2 = keep.tile([P, 2, 2, LAT], F32, name="bias2", tag="bias2")
        exp_tenth = keep.tile([P, 1], F32, name="exp_tenth", tag="exp_tenth")
        w1_rows, w1_codes, w1_scales = {}, {}, {}
        for head in HEADS:
            for a in (0, 1):
                name = "w1_%d_%d" % (head, a)
                w1_rows[head, a] = keep.tile([P, 2, (1 + head) * KIN], BF16, name=name, tag=name)
                w1_codes[head, a] = keep.tile([P, 1 + head, HALF], U32, name=name + "c", tag=name + "c", align_bytes=ALIGN)
                w1_scales[head, a] = keep.tile([P, 1 + head, HALF], U8, name=name + "s", tag=name + "s", align_bytes=ALIGN)
        w2_rows = keep.tile([P, 2, HID], BF16, name="w2_rows", tag="w2_rows")
        value = keep.tile([P, 2, 2, GROUPS * J, LAT], F32, name="value", tag="value")
        soft = keep.tile([P, 2, GROUPS * J * LAT], F32, name="soft", tag="soft")
        w2_codes = keep.tile([P, 2, DIST], U32, name="w2_codes", tag="w2_codes", align_bytes=ALIGN)
        w2_scales = keep.tile([P, 2, DIST], U8, name="w2_scales", tag="w2_scales", align_bytes=ALIGN)

        h_raw, emb, h_wide, turned, c_grouped, c_codes, c_scales = {}, {}, {}, {}, {}, {}, {}
        mixed, w1_grouped, acc, planes, a_grouped, a_codes, a_scales, result = {}, {}, {}, {}, {}, {}, {}, {}

        ring = list(range(BANKS))
        pairs, plain_chunks = {}, set()

        def next_bank(shape, dtype=F32):
            ring.append(ring.pop(0))
            return psum.tile(shape, dtype, name="bank", tag="bank_%d" % ring[-1])

        def turn(key, words):
            bank = next_bank([P, 2, HALF])
            turned[key] = bank
            for b in (0, 1):
                for u in (0, 1):
                    nc.tensor.transpose(bank[:, u, b * P : (b + 1) * P], words(b, u), ident[:])

        def every_second_word(rows):
            return lambda b, u: rows[:, b, :].bitcast(F32)[:, u : KIN // 2 : 2]

        def unload(copy, key, dst):
            copy(out=dst.bitcast(F32), in_=turned[key][:].rearrange("p u n -> p n u"))

        def quantise(codes, scales, grouped):
            nc.vector.quantize_mx(out=codes.bitcast(FP8X4), scales=scales, in_=grouped.rearrange("p n t -> p (n t)"))

        on_scalar, on_vector = nc.scalar.copy, nc.vector.tensor_copy


        def load_w1(head, a):
            rows = (wp1, wq1)[head].rearrange("(m t) k -> m t k", t=PACK)
            nc.sync.dma_start(out=w1_rows[head, a][:], in_=rows[:, 2 * a : 2 * a + 2])

        def turn_w1(head, a, g):
            turn(("w", head, a, g), every_second_word(w1_rows[head, a][:, :, g * KIN : (g + 1) * KIN]))

        def unload_w1(copy, head, a, g):
            if g == H:
                tag, bufs = (("w_grouped", 2), (("gpsimd_wide", "a_grouped")[head], 1))[a]
                w1_grouped[head, a] = work.tile([P, CHUNK, PACK], BF16, name="w1_grouped", tag=tag, bufs=bufs, align_bytes=ALIGN)
            unload(copy, ("w", head, a, g), w1_grouped[head, a][:, g * HALF : (g + 1) * HALF])

        def quantise_w1(head, a):
            quantise(w1_codes[head, a][:].rearrange("p g m -> p (g m)"), w1_scales[head, a][:].rearrange("p g m -> p (g m)"),
                     w1_grouped[head, a][:, 0 : (1 + head) * HALF])


        def load_h(i, pieces=((0, J),)):
            h_raw[i] = work.tile([P, J, KIN], U8, name="h_raw", tag="h_raw", bufs=CHUNKS, align_bytes=ALIGN)
            rows = h_bytes.rearrange("(p c j) k -> c p j k", p=P, j=J)[i]
            for j0, j1 in pieces:
                nc.sync.dma_start(out=h_raw[i][:, j0:j1], in_=rows[:, j0:j1])

        def load_embedding(i):
            emb[i] = work.tile([P, J, KIN], BF16, name="emb", tag="emb", bufs=EMB_BUFS)
            nc.sync.dma_start(out=emb[i][:], in_=embedding.rearrange("(p c j) k -> c p j k", p=P, j=J)[i])

        def raw_values(i, j0=0, j1=J):
            return h_raw[i][:, j0:j1].rearrange("p j k -> p (j k)").bitcast(FP8)

        def wide(i):
            if i not in h_wide:
                h_wide[i] = work.tile([P, 2, 2, HALF, 2], BF16, name="h_wide", tag="h_wide", bufs=WIDE_BUFS, align_bytes=ALIGN)
            return h_wide[i]

        def widen(i, a0=0, a1=2):
            nc.scalar.copy(out=wide(i)[:, a0:a1].rearrange("p a u q e -> p (a u q e)"),
                           in_=raw_values(i, 2 * a0, 2 * a1).rearrange("p (a q u e) -> p a u q e", q=HALF, u=2, e=2))

        def widen_on_vector(i, j0=0, j1=J):
            if j1 - j0 == 1:
                out = wide(i)[:, j0 // 2, :, j0 % 2 * P : (j0 % 2 + 1) * P].rearrange("p u q e -> p q u e")
            else:
                out = wide(i)[:, j0 // 2 : j1 // 2].rearrange("p a u q e -> p a q u e")
            nc.vector.tensor_copy(out=out, in_=raw_values(i, j0, j1))

        def widen_on_gpsimd(i):
            h_wide[i] = work.tile([P, J, KIN], BF16, name="h_wide", tag="gpsimd_wide", bufs=1, align_bytes=ALIGN)
            plain_chunks.add(i)
            nc.gpsimd.tensor_copy(out=h_wide[i][:].rearrange("p j k -> p (j k)"), in_=raw_values(i))

        def turn_c(i, g, a):
            if g == H and i not in plain_chunks:
                words = h_wide[i][:, a].rearrange("p u q e -> p u (q e)").bitcast(F32)
                turn((i, g, a), lambda b, u: words[:, u, b * P : (b + 1) * P])
            else:
                turn((i, g, a), every_second_word((h_wide, emb)[g][i][:, 2 * a : 2 * a + 2]))

        def grouped_half(i, g, a):
            if (i, g) not in c_grouped:
                c_grouped[i, g] = work.tile([P, CHUNK, PACK], BF16, name="c_grouped", tag="c_grouped_%d" % g, bufs=2, align_bytes=ALIGN)
            return c_grouped[i, g][:, a * HALF : (a + 1) * HALF]

        def scale_h(i, a):
            nc.vector.tensor_tensor(
                out=grouped_half(i, H, a).rearrange("p n (u e) -> p n u e", u=2),
                in0=turned[i, H, a][:].bitcast(BF16).rearrange("p u (n e) -> p n u e", e=2),
                in1=scale[:].rearrange("p (u e) -> p u e", u=2).unsqueeze(1).to_broadcast([P, HALF, 2, 2]),
                op=ALU.mult)

        def unload_e(copy, i, a):
            unload(copy, (i, E, a), grouped_half(i, E, a))

        def quantise_c(i, g):
            c_codes[i, g] = work.tile([P, CHUNK], U32, name="c_codes", tag="c_codes_%d" % g, bufs=3 - g, align_bytes=ALIGN)
            c_scales[i, g] = work.tile([P, CHUNK], U8, name="c_scales", tag="c_scales_%d" % g, bufs=3 - g, align_bytes=ALIGN)
            quantise(c_codes[i, g][:], c_scales[i, g][:], c_grouped[i, g][:])


        def passes(out, i, head, t, n0, n1):
            a, cols = t // 2, slice(t % 2 * P, (t % 2 + 1) * P)
            for g in range(1 + head):
                nc.tensor.matmul_mx(
                    out=out, lhsT=w1_codes[head, a][:, g, cols].bitcast(FP8X4), lhsT_scale=w1_scales[head, a][:, g, cols],
                    rhs=c_codes[i, g][:, n0:n1].bitcast(FP8X4), rhs_scale=c_scales[i, g][:, n0:n1],
                    start=(g == 0), stop=(g == head))

        def plane(i, head, t, n0, n1):
            s = i + head
            if s not in planes:
                planes[s] = work.tile([P, PACK, 2 * CHUNK], BF16, name="planes", tag="planes", bufs=PLANE_BUFS, align_bytes=ALIGN)
            return planes[s][:, t, head * CHUNK + n0 : head * CHUNK + n1]

        def relu(i, head, t, n0, n1):
            nc.scalar.activation(out=plane(i, head, t, n0, n1), in_=acc[i, head, t], func=ACT.Relu, bias=bias1[head][:, t : t + 1])

        def relu_on_vector(i, head, t, n0, n1):
            nc.vector.tensor_scalar(
                out=plane(i, head, t, n0, n1), in0=acc[i, head, t], scalar1=bias1[head][:, t : t + 1], scalar2=0.0,
                op0=ALU.add, op1=ALU.max)

        def layer1(i, head, tiles=range(PACK), vector_tiles=(), n0=0, n1=CHUNK):
            fit = CHUNK // (n1 - n0)
            for t0 in tiles[::fit]:
                bank = next_bank([P, fit, n1 - n0])
                for t in range(t0, t0 + fit):
                    acc[i, head, t] = bank[:, t - t0]
                    passes(acc[i, head, t], i, head, t, n0, n1)
                for t in range(t0, t0 + fit):
                    (relu_on_vector if t in vector_tiles else relu)(i, head, t, n0, n1)

        def layer1_pairs(i, head, a):
            pairs[i + head, head, a] = work.tile([P, 2, HALF, 2], BF16, name="pairs", tag="pairs", bufs=PAIR_BUFS, align_bytes=ALIGN)
            for u in (0, 1):
                bank = next_bank([P, 2, HALF])
                for e in (0, 1):
                    passes(bank[:, e], i, head, 2 * u + e, a * HALF, (a + 1) * HALF)
                nc.vector.tensor_tensor(
                    out=pairs[i + head, head, a][:, u], in0=bank[:].rearrange("p e n -> p n e"),
                    in1=bias1[head][:, 2 * u : 2 * u + 2].unsqueeze(1).to_broadcast([P, HALF, 2]), op=ALU.add)

        def relu_pairs(s, head, a):
            n0 = head * CHUNK + a * HALF
            nc.vector.tensor_scalar(
                out=grouped(s, n0, n0 + HALF).rearrange("p n (u e) -> p n u e", u=2),
                in0=pairs[s, head, a][:].rearrange("p u n e -> p n u e"), scalar1=0.0, scalar2=None, op0=ALU.max)

        def grouped(s, n0, n1):
            if s >= CHUNKS - 1:
                head = n0 // CHUNK
                if (s, head) not in a_grouped:
                    a_grouped[s, head] = work.tile([P, CHUNK, PACK], BF16, name="a_grouped", tag="c_grouped_%d" % head, bufs=2, align_bytes=ALIGN)
                return a_grouped[s, head][:, n0 - head * CHUNK : n1 - head * CHUNK]
            if s not in a_grouped:
                columns = 2 * CHUNK if s else CHUNK
                a_grouped[s] = work.tile([P, columns, PACK], BF16, name="a_grouped", tag="a_grouped", bufs=1, align_bytes=ALIGN)
            return a_grouped[s][:, n0:n1]

        def interleave(s, n0, n1):
            nc.vector.tensor_copy(
                out=grouped(s, n0, n1).rearrange("p (c i) t -> p c t i", i=4),
                in_=planes[s][:, :, n0:n1].rearrange("p t (c i) -> p c t i", i=4))

        def interleave_on_scalar(s, n0, n1):
            nc.scalar.copy(out=grouped(s, n0, n1), in_=planes[s][:, :, n0:n1].rearrange("p t n -> p n t"))

        def interleave_on_gpsimd(s, n0, n1):
            nc.gpsimd.tensor_copy(out=grouped(s, n0, n1), in_=planes[s][:, :, n0:n1].rearrange("p t n -> p n t"))

        def mix(s, n0, n1):
            mixed[s, n0] = next_bank([P, n1 - n0, PACK], BF16)
            for m in range(0, n1 - n0, P):
                nc.tensor.matmul(
                    out=mixed[s, n0][:, m : m + P].rearrange("p n t -> p t n"), lhsT=ident16[:],
                    rhs=planes[s][:, :, n0 + m : n0 + m + P], start=True, stop=True)

        def unload_mixed(copy, s, n0, n1):
            copy(out=grouped(s, n0, n1).bitcast(F32), in_=mixed[s, n0][:].bitcast(F32))

        def quantise_a(s, heads=BOTH):
            if s not in a_codes:
                a_codes[s] = work.tile([P, 2 * CHUNK], U32, name="a_codes", tag="a_codes", bufs=A_BUFS, align_bytes=ALIGN)
                a_scales[s] = work.tile([P, 2 * CHUNK], U8, name="a_scales", tag="a_scales", bufs=A_BUFS, align_bytes=ALIGN)
            cols = slice(heads.start * CHUNK, heads.stop * CHUNK)
            quantise(a_codes[s][:, cols], a_scales[s][:, cols], grouped(s, cols.start, cols.stop))


        def pass2(out, s, head, j, cols):
            tokens = slice(head * CHUNK + j * P, head * CHUNK + (j + 1) * P)
            nc.tensor.matmul_mx(
                out=out, lhsT=a_codes[s][:, tokens].bitcast(FP8X4), lhsT_scale=a_scales[s][:, tokens],
                rhs=w2_codes[:, head, cols].bitcast(FP8X4), rhs_scale=w2_scales[:, head, cols], start=True, stop=True)

        def second(s, head):
            result[s, head] = next_bank([P, J, 2, LAT])
            for j in range(J):
                pass2(result[s, head][:, j, :, :].rearrange("p h c -> p (h c)"), s, head, j, slice(0, DIST))

        def second_half(half, s):
            result["half", half, s] = next_bank([P, 2, J, LAT])
            for head in HEADS:
                for j in range(J):
                    pass2(result["half", half, s][:, head, j], s, head, j, slice(half * LAT, (half + 1) * LAT))

        def add_bias_half(half, s):
            nc.vector.tensor_tensor(
                out=value[:, :, half, s * J : (s + 1) * J], in0=result["half", half, s][:],
                in1=bias2[:, :, half].unsqueeze(2).to_broadcast([P, 2, J, LAT]), op=ALU.add)

        def store(head, half, s0, s1):
            dst = ((prior_mean, prior_std), (post_mean, post_std))[head][half]
            nc.sync.dma_start(
                out=dst.rearrange("(p n) d -> p n d", p=P)[:, (s0 - head) * J : (s1 - head) * J],
                in_=value[:, head, half, s0 * J : s1 * J])

        def add_bias(s, head, halves=(MEAN, STD)):
            part = slice(halves[0], halves[-1] + 1)
            nc.vector.tensor_tensor(
                out=value[:, head, part, s * J : (s + 1) * J].rearrange("p h j c -> p j h c"),
                in0=result[s, head][:, :, part],
                in1=bias2[:, head, part].unsqueeze(1).to_broadcast([P, J, len(halves), LAT]),
                op=ALU.add)

        def layer2(s, head):
            second(s, head)
            add_bias(s, head)
            store(head, MEAN, s, s + 1)

        def w_of(heads, s0, s1):
            return value[:, heads, STD, s0 * J : s1 * J].rearrange("p e n c -> p e (n c)")

        def soft_of(heads, s0, s1):
            return soft[:, heads, s0 * J * LAT : s1 * J * LAT]

        def exp(heads, s0, s1):
            nc.scalar.activation(out=soft_of(heads, s0, s1), in_=w_of(heads, s0, s1), func=ACT.Exp)

        def log(heads, s0, s1):
            nc.scalar.activation(out=soft_of(heads, s0, s1), in_=soft_of(heads, s0, s1), func=ACT.Ln, bias=exp_tenth[:])

        def std(heads, s0, s1):
            nc.vector.scalar_tensor_tensor(
                out=w_of(heads, s0, s1), in0=soft_of(heads, s0, s1), scalar=EXACT_ABOVE, in1=w_of(heads, s0, s1),
                op0=ALU.min, op1=ALU.max)

        def turn_w2():
            turn("w2", every_second_word(w2_rows[:]))
            w1_grouped["w2"] = work.tile([P, CHUNK, PACK], BF16, name="w2_grouped", tag="w_grouped", bufs=2, align_bytes=ALIGN)
            unload(on_scalar, "w2", w1_grouped["w2"][:, 0:HALF])

        def quantise_w2():
            quantise(w2_codes[:].rearrange("p e m -> p (e m)"), w2_scales[:].rearrange("p e m -> p (e m)"),
                     w1_grouped["w2"][:, 0:HALF])

        def spread_bias2():
            both = next_bank([P, 2, 2, LAT])
            for head in HEADS:
                nc.tensor.matmul(
                    out=both[:, head].rearrange("p h c -> p (h c)"),
                    lhsT=bias2_raw[head][:].to_broadcast([P, P]), rhs=ident16[:], start=True, stop=True)
            nc.scalar.copy(out=bias2[:, :, MEAN], in_=both[:, :, MEAN])
            nc.scalar.activation(out=bias2[:, :, STD], in_=both[:, :, STD], func=ACT.Copy, bias=0.1)

        def turn_and_scale(i):
            for a in (0, 1):
                turn_c(i, H, a)
                scale_h(i, a)

        def turn_embedding(i, copies=(on_scalar, on_scalar)):
            for a in (0, 1):
                turn_c(i, E, a)
                unload_e(copies[a], i, a)

        with tc.manual_schedule():
            nc.vector.memset(ones[:], 1.0)
            make_identity(nc, ident[:])
            make_identity(nc, ident16[:])
            nc.scalar.dma_start(out=scale[:], in_=h_scale.rearrange("o (p t) -> p (o t)", t=PACK))
            nc.scalar.activation(out=exp_tenth[:], in_=ones[:, 0:1], func=ACT.Exp, scale=0.1)
            load_h(0, ((0, 1), (1, 2), (2, J)))
            load_h(1)
            for a in (0, 1):
                load_w1(PRIOR, a)
            load_h(2)
            load_embedding(0)
            nc.sync.dma_start(out=bias1[PRIOR][:], in_=bp1.rearrange("(m t) -> m t", t=PACK))
            load_h(5)
            load_h(4)
            load_w1(POST, 0)
            load_h(3)
            load_w1(POST, 1)
            nc.sync.dma_start(out=bias1[POST][:], in_=bq1.rearrange("(m t) -> m t", t=PACK))
            nc.sync.dma_start(out=w2_rows[:, PRIOR, :], in_=wp2)
            nc.sync.dma_start(out=w2_rows[:, POST, :], in_=wq2)
            load_embedding(1)
            nc.sync.dma_start(out=bias2_raw[PRIOR][:], in_=bp2.unsqueeze(1))
            nc.sync.dma_start(out=bias2_raw[POST][:], in_=bq2.unsqueeze(1))
            load_h(6)
            load_h(7)
            for i in range(2, EMB_BUFS):
                load_embedding(i)

            widen_on_vector(0, 0, 1)
            widen_on_vector(0, 1, 2)
            widen(0, 1, 2)
            widen(1)
            turn_and_scale(0)
            for a in (0, 1):
                turn_w1(PRIOR, a, H)
                unload_w1(on_scalar, PRIOR, a, H)
            widen(2)
            quantise_w1(PRIOR, 0)
            quantise_c(0, H)
            quantise_w1(PRIOR, 1)
            widen_on_gpsimd(5)
            turn_and_scale(1)
            turn_embedding(0, (on_scalar, on_vector))
            load_embedding(EMB_BUFS)
            widen(4)
            layer1(0, PRIOR)
            quantise_c(1, H)
            quantise_c(0, E)
            widen_on_vector(3)
            for a in (0, 1):
                for g in (H, E):
                    turn_w1(POST, a, g)
                    unload_w1(on_vector if (a, g) == (1, E) else on_scalar, POST, a, g)
            layer1(1, PRIOR, n0=HALF)
            for a in (0, 1):
                turn_c(2, H, a)
            turn_w2()
            widen(6)
            for a in (0, 1):
                quantise_w1(POST, a)
            interleave_on_gpsimd(0, 0, CHUNK)
            for a in (0, 1):
                scale_h(2, a)
            layer1(0, POST, range(0, 2))
            turn_embedding(1, (on_vector, on_vector))
            load_embedding(EMB_BUFS + 1)
            layer1(0, POST, range(2, PACK))
            spread_bias2()
            widen(CHUNKS - 1)
            quantise_c(2, H)
            quantise_c(1, E)
            quantise_w2()
            for a in (0, 1):
                turn_c(3, H, a)
            for a in (0, 1):
                turn_c(2, E, a)
            unload_e(on_scalar, 2, 0)
            unload_e(on_scalar, 2, 1)
            layer1(1, POST)
            quantise_a(0, ONLY[PRIOR])

            last = CHUNKS - 1
            for s in range(1, last - 1):
                first_step, final_step = s == 1, s + 2 == last
                n1 = FINAL_SHARE if final_step else GPSIMD_SHARE
                n3 = 2 * CHUNK - (0 if first_step else TENSOR_SHARE)
                n2 = n3 - (0 if final_step else SCALAR_SHARE)
                if first_step:
                    interleave_on_gpsimd(s, HALF, 2 * CHUNK)
                else:
                    interleave_on_gpsimd(s, 0, n1)
                for a in (0, 1):
                    scale_h(s + 2, a)
                if first_step:
                    load_embedding(EMB_BUFS + 2)
                else:
                    exp(BOTH if s > 2 else ONLY[PRIOR], s - 2, s - 1)
                if not first_step:
                    layer1(s, POST, range(0, 2))
                if n3 < 2 * CHUNK:
                    mix(s, n3, 2 * CHUNK)
                    unload_mixed(on_scalar, s, n3, 2 * CHUNK)
                if first_step:
                    layer1_pairs(s, PRIOR, 0)
                    layer2(0, PRIOR)
                elif final_step:
                    for head in HEADS:
                        layer2(s - 1, head)
                    turn_embedding(last, (on_vector, on_scalar))
                else:
                    for head in HEADS:
                        layer2(s - 1, head)
                if not first_step:
                    layer1(s, POST, range(2, PACK))
                if not first_step and n2 < n3:
                    interleave_on_scalar(s, n2, n3)
                layer1(s + 1, PRIOR)
                if first_step:
                    relu_pairs(s, PRIOR, 0)
                if final_step:
                    quantise_c(s + 1, E)
                if not first_step:
                    interleave(s, n1, n2)
                if not final_step:
                    quantise_c(s + 1, E)
                if final_step:
                    quantise_c(last, H)
                    quantise_a(s)
                    quantise_c(last, E)
                else:
                    quantise_a(s)
                    quantise_c(s + 2, H)
                    turn_embedding(s + 2)
                    for a in (0, 1):
                        turn_c(s + 3, H, a)

            g6, g7, g8 = last - 1, last, CHUNKS
            late = g6 - 1
            interleave_on_gpsimd(g6, 0, 544)
            layer1(last - 1, POST, vector_tiles=(3,))
            layer1(last, PRIOR, vector_tiles=(1, 3))
            second_half(STD, late)
            add_bias_half(STD, late)
            layer1(last, POST, vector_tiles=(1,))
            interleave(g6, 544, 2 * CHUNK)
            for n0 in (CHUNK, CHUNK + HALF):
                mix(g7, n0, n0 + HALF)
            mix(g8, CHUNK + HALF, 2 * CHUNK)
            interleave_on_scalar(g7, CHUNK - 256, CHUNK)
            for n0 in (CHUNK, CHUNK + HALF):
                unload_mixed(on_scalar, g7, n0, n0 + HALF)
            interleave(g7, 0, CHUNK - 256)
            quantise_a(g6)
            quantise_a(g7, ONLY[PRIOR])
            for head in HEADS:
                second(g6, head)
            second(g7, PRIOR)
            interleave_on_scalar(g8, CHUNK + HALF - 64, CHUNK + HALF)
            unload_mixed(on_scalar, g8, CHUNK + HALF, 2 * CHUNK)
            exp(BOTH, late - 1, g6)
            interleave(g8, CHUNK, CHUNK + HALF - 64)
            quantise_a(g7, ONLY[POST])
            second(g7, POST)
            add_bias(g6, PRIOR, (STD,))
            quantise_a(g8, ONLY[POST])
            add_bias(g6, POST, (STD,))
            exp(BOTH, g6, g7)
            second(g8, POST)
            second_half(MEAN, late)
            for head in HEADS:
                add_bias(g7, head, (STD,))
                exp(ONLY[head], g7, g8)
            add_bias(g8, POST, (STD,))
            exp(ONLY[POST], g8, g8 + 1)

            add_bias_half(MEAN, late)
            for head in HEADS:
                add_bias(g6, head, (MEAN,))
                store(head, MEAN, late, g7)
                for s in range(g7, g8 + head):
                    add_bias(s, head, (MEAN,))
                store(head, MEAN, g7, g8 + head)
            for pair in range(0, CHUNKS, 2):
                for head in HEADS:
                    final = pair + 2 == CHUNKS and head == POST
                    for s in (pair + head, pair + head + 1):
                        log(ONLY[head], s, s + 1)
                        std(ONLY[head], s, s + 1)
                        if final:
                            store(head, STD, s, s + 1)
                    if not final:
                        store(head, STD, pair + head, pair + head + 2)
